import numpy as np
import ml_dtypes


def mxq(x, axis, fmt="e4m3"):
    dtype, down = {"e4m3": (ml_dtypes.float8_e4m3fn, 7), "e5m2": (ml_dtypes.float8_e5m2, 14)}[fmt]
    v = np.moveaxis(np.asarray(x, np.float32).astype(ml_dtypes.bfloat16).astype(np.float64), axis, -1)
    blocks = v.reshape(v.shape[:-1] + (-1, 32))
    amax = np.abs(blocks).max(-1, keepdims=True)
    byte = np.maximum(np.where(amax > 0, np.frexp(amax)[1] - 1 + 127, 0) - down, 1)
    scale = np.exp2(byte - 127.0)
    codes = (blocks / scale).astype(np.float32).astype(dtype).astype(np.float64)
    return np.moveaxis((codes * scale).reshape(v.shape), -1, axis)


WIDE = False


def mx_kscale(k):
    if not WIDE:
        return np.ones(k)
    levels = np.array([10, -10, 5, -5, 0])
    if k % 512:
        return np.exp2(np.random.permutation(np.resize(levels, k // 32))).repeat(32)
    a = np.empty((k // 512, 16))
    for p in range(k // 512):
        a[p, :8] = np.random.permutation(np.resize(levels, 8))
        for g in range(8):
            far = levels[np.abs(levels - a[p, g]) >= 10]
            a[p, g + 8] = far[np.random.randint(len(far))]
    return np.exp2(a.ravel()).repeat(32)


BF16 = ml_dtypes.bfloat16


def bf(x):
    return np.asarray(x, np.float32).astype(BF16)


def f64(x):
    return np.asarray(x).astype(np.float64)


E2M1 = np.array([0.0, 0.5, 1.0, 1.5, 2.0, 3.0, 4.0, 6.0, -0.0, -0.5, -1.0, -1.5, -2.0, -3.0, -4.0, -6.0])


def pack_weight(w, fmt):
    k, n = w.shape
    w = f64(bf(w)).reshape(k // 32, 32, n)
    amax = np.abs(w).max(1)
    if fmt == "e4m3":
        byte = np.frexp(amax)[1] - 1 + 127 - 7
    else:
        mant, ex = np.frexp(amax / 6.0)
        byte = np.where(mant > 0.5, ex, ex - 1) + 127
    byte = np.clip(np.where(amax > 0, byte, 1), 1, 254)
    scaled = (w * np.exp2(127.0 - byte)[:, None, :]).reshape(k, n).astype(np.float32)
    by_word = np.ascontiguousarray(scaled.reshape(k // 512, 128, 4, n).transpose(0, 1, 3, 2))
    if fmt == "e4m3":
        words = by_word.astype(ml_dtypes.float8_e4m3fn).view(np.uint8)
    else:
        c = by_word.astype(ml_dtypes.float4_e2m1fn).view(np.uint8) & 0xF
        words = c[..., 0::2] | (c[..., 1::2] << 4)
    return np.ascontiguousarray(words), np.ascontiguousarray(byte.astype(np.uint8).reshape(k // 512, 16, n))


def unpack_weight(words, scales, fmt):
    g, p, n, _ = words.shape
    if fmt == "e4m3":
        vals = np.ascontiguousarray(words).view(ml_dtypes.float8_e4m3fn).astype(np.float64)
    else:
        nib = np.empty((g, p, n, 4), np.uint8)
        nib[..., 0::2] = words & 0xF
        nib[..., 1::2] = words >> 4
        vals = E2M1[nib]
    vals = vals * np.repeat(np.exp2(scales.astype(np.float64) - 127.0), 8, axis=1)[..., None]
    return vals.transpose(0, 1, 3, 2).reshape(g * 512, n)


B, L, E, H, DH, RK, RD, MAXLEN = 4, 1024, 512, 4, 64, 512, 128, 4096


def apply_rope(x, cos, sin):
    cos = cos[None, :, None, :]
    sin = sin[None, :, None, :]
    x1, x2 = x[..., 0::2], x[..., 1::2]
    out_real = x1 * cos - x2 * sin
    out_imag = x1 * sin + x2 * cos
    return np.stack([out_real, out_imag], axis=-1).reshape(x.shape)


def draw0():
    s, t = mx_kscale(E), mx_kscale(RK)
    tc = np.concatenate([t, np.ones(RD)])
    x = bf(np.random.standard_normal((B, L, E)) * s)
    cos = bf(np.random.uniform(size=(L, RD // 2)))
    sin = bf(np.random.uniform(size=(L, RD // 2)))
    wkv_down_words, wkv_down_scales = pack_weight(np.random.standard_normal((E, RK + RD)) / np.sqrt(E) / s[:, None] * tc, "e4m3")
    w_up_words, w_up_scales = pack_weight(np.random.standard_normal((RK, H * (2 * DH + RD))) / np.sqrt(RK) / t[:, None], "e4m3")
    return {"x": x,
            "cos": cos,
            "sin": sin,
            "wkv_down_words": wkv_down_words,
            "wkv_down_scales": wkv_down_scales,
            "w_up_words": w_up_words,
            "w_up_scales": w_up_scales}


def core(x, cos, sin, wkv_down_words, wkv_down_scales, w_up_words, w_up_scales):
    kv_lat = mxq(f64(x), 2, "e4m3") @ unpack_weight(wkv_down_words, wkv_down_scales, "e4m3")
    c_kv = kv_lat[..., :RK]
    k_rope = kv_lat[..., RK:]
    k_rope = apply_rope(k_rope[:, :, None, :], f64(cos), f64(sin))[:, :, 0, :]
    up = (mxq(c_kv, 2, "e4m3") @ unpack_weight(w_up_words, w_up_scales, "e4m3")).reshape(B, L, H, 2 * DH + RD)
    k_head = up[..., :DH]
    v_head = up[..., DH:2 * DH]
    v_rope = up[..., 2 * DH:]
    k_rope_b = np.broadcast_to(k_rope[:, :, None, :], (B, L, H, RD))
    k = np.concatenate([k_head, k_rope_b], axis=-1)
    v = np.concatenate([v_head, v_rope], axis=-1)
    return k, v


def e4m3fn_bytes(y):
    return np.clip(np.asarray(y, np.float64), -448.0, 448.0).astype(np.float32).astype(ml_dtypes.float8_e4m3fn).view(np.uint8)


def e4m3fn_values(b):
    return np.asarray(b, np.uint8).view(ml_dtypes.float8_e4m3fn).astype(np.float64)


def setup_inputs():
    d = draw0()
    x0 = np.asarray(d['x']).astype(np.float64)
    s = (np.max(np.abs(x0), axis=(0, 1), keepdims=True) / 448.0).astype(np.float32)
    out = {}
    for k, v in d.items():
        if k == 'x':
            out['x_bytes'] = e4m3fn_bytes(x0 / s.astype(np.float64))
            out['x_scale'] = s
        else:
            out[k] = v
    return out


def reference(x_bytes, x_scale, cos, sin, wkv_down_words, wkv_down_scales, w_up_words, w_up_scales):
    return core(e4m3fn_values(x_bytes) * x_scale.astype(np.float64), cos, sin, wkv_down_words, wkv_down_scales, w_up_words, w_up_scales)

@@ -1,0 +1,314 @@
+from contextlib import ExitStack
+
+import concourse.mybir as mybir
+from concourse.masks import make_identity
+
+F32 = mybir.dt.float32
+BF16 = mybir.dt.bfloat16
+I32 = mybir.dt.int32
+U32 = mybir.dt.uint32
+U8 = mybir.dt.uint8
+FP8 = mybir.dt.float8_e4m3fn
+FP8X4 = mybir.dt.float8_e4m3fn_x4
+MULT = mybir.AluOpType.mult
+ADD = mybir.AluOpType.add
+
+P = 128
+B, L, E, H, DH, RK, RD = 4, 1024, 512, 4, 64, 512, 128
+I = L // P
+DV = DH + RD
+UP = DH + DV
+
+FLOPS = 2 * B * L * E * (RK + RD + H * UP)
+
+
+def tile_multiheadlatentattention_pa_t_w8_kernel(
+    tc, x_bytes, x_scale, cos, sin, wd_words, wd_scales, wu_words, wu_scales, k_out, v_out
+):
+    nc = tc.nc
+    tiles = [(b, i) for b in range(B) for i in range(I)]
+    units = []
+    while tiles:
+        width = 1 if len(units) < 4 or len(tiles) <= 2 else 2
+        units.append((tiles[0][0], tiles[0][1], width))
+        tiles = tiles[width:]
+    last = len(units) - 1
+
+    with ExitStack() as ctx:
+        keep = ctx.enter_context(tc.tile_pool(name="keep", bufs=1))
+        work = ctx.enter_context(tc.tile_pool(name="work", bufs=3))
+        outs = ctx.enter_context(tc.tile_pool(name="outs", bufs=5))
+        ps_x = ctx.enter_context(tc.psum_pool(name="ps_x", bufs=2))
+        ps_c = ctx.enter_context(tc.psum_pool(name="ps_c", bufs=2))
+        ps_r = ctx.enter_context(tc.psum_pool(name="ps_r", bufs=1))
+        ps_u = ctx.enter_context(tc.psum_pool(name="ps_u", bufs=3))
+        ctx.enter_context(tc.manual_schedule())
+
+        wd_raw = keep.tile([P, RK + 2 * RD], U32, align_bytes=64)
+        wd_s_raw = keep.tile([P, RK + 2 * RD], U8, align_bytes=64)
+        wd = keep.tile([P, RK], U32, align_bytes=64)
+        wd_s = keep.tile([P, RK], U8, align_bytes=64)
+        wu = keep.tile([P, H * UP], U32, align_bytes=64)
+        wu_s = keep.tile([P, H * UP], U8, align_bytes=64)
+        xb_first = keep.tile([P, 2 * E], U8, align_bytes=64)
+        xb_rest = keep.tile([P, (I - 2) * E], U8, align_bytes=64)
+        xb_1 = keep.tile([P, I * E], U8, align_bytes=64)
+        xb_2 = keep.tile([P, I * E], U8, align_bytes=64)
+        xb_3 = keep.tile([P, I * E], U8, align_bytes=64)
+        xsc = keep.tile([P, 2, 2], F32)
+        cos_sb = keep.tile([P, I, RD // 2], BF16)
+        sin_sb = keep.tile([P, I, RD // 2], BF16)
+        tab_a = keep.tile([P, I // 2, 2, RD], BF16)
+        tab_b = keep.tile([P, I // 2, 2, RD], BF16)
+        ident = keep.tile([P, P], F32)
+        warm = keep.tile([P, 8], F32)
+
+        nc.vector.memset(wd_s_raw[:].bitcast(I32), 0)
+        nc.vector.memset(wu_s[:].bitcast(I32), 0)
+        nc.vector.memset(warm[:], 0.0)
+        nc.scalar.copy(out=warm[:, 4:8], in_=warm[:, 0:4])
+        make_identity(nc, ident[:])
+        nc.gpsimd.dma_start(out=xsc[:], in_=x_scale.rearrange("a b (p u e) -> p (a b u) e", u=2, e=2))
+        nc.gpsimd.dma_start(out=cos_sb[:], in_=cos.rearrange("(p i) j -> p i j", i=I))
+        nc.gpsimd.dma_start(out=sin_sb[:], in_=sin.rearrange("(p i) j -> p i j", i=I))
+        xv = [x_bytes[b].rearrange("(p i) k -> p (i k)", i=I) for b in range(B)]
+        nc.sync.dma_start(out=xb_first[:], in_=xv[0][:, 0 : 2 * E])
+        nc.sync.dma_start(
+            out=wd_raw[:, 0 : RK + RD].bitcast(I32), in_=wd_words[0].rearrange("p n t -> p (n t)").bitcast(I32)
+        )
+        for q in range(4):
+            nc.sync.dma_start(
+                out=wd_s_raw[32 * q : 32 * q + 4, 0 : RK + RD].bitcast(I32),
+                in_=wd_scales[0, 4 * q : 4 * q + 4, :].bitcast(I32),
+            )
+        nc.sync.dma_start(out=xb_rest[:], in_=xv[0][:, 2 * E :])
+        nc.sync.dma_start(out=wu[:].bitcast(I32), in_=wu_words[0].rearrange("p n t -> p (n t)").bitcast(I32))
+        for q in range(4):
+            nc.sync.dma_start(
+                out=wu_s[32 * q : 32 * q + 4, :].bitcast(I32), in_=wu_scales[0, 4 * q : 4 * q + 4, :].bitcast(I32)
+            )
+        nc.sync.dma_start(out=xb_1[:], in_=xv[1])
+        nc.sync.dma_start(out=xb_2[:], in_=xv[2])
+        nc.sync.dma_start(out=xb_3[:], in_=xv[3])
+
+        def tables(tab, i0):
+            view = tab[:].rearrange("p i g (j e) -> p i g j e", e=2)
+            for g, src in ((0, cos_sb), (1, sin_sb)):
+                for e in range(2):
+                    factor = -1.0 if (g, e) == (1, 0) else 1.0
+                    nc.gpsimd.tensor_scalar(
+                        out=view[:, :, g, :, e],
+                        in0=src[:, i0 : i0 + I // 2, :],
+                        scalar1=factor,
+                        scalar2=0.0,
+                        op0=MULT,
+                        op1=ADD,
+                    )
+
+        def permute(dst, src):
+            nc.vector.tensor_copy(
+                out=dst.rearrange("p (t m) -> p t m", t=4), in_=src.rearrange("p (m t) -> p t m", t=4)
+            )
+
+        xw, xt, xg, xq, xs, pc, cg, cq, cs, pr, ab, kt, vt, pu = [{} for j in range(14)]
+
+        def x_source(n):
+            b, i, w = units[n]
+            if b > 0:
+                return [xb_1, xb_2, xb_3][b - 1][:, i * E : (i + w) * E]
+            return xb_first[:, i * E : (i + w) * E] if i < 2 else xb_rest[:, (i - 2) * E : (i - 2 + w) * E]
+
+        def widen(n):
+            w = units[n][2]
+            xw[n] = work.tile([P, 2 * E], BF16, name="xw", bufs=4)
+            copy = nc.scalar.copy if n in (1, 2, 3) else nc.vector.tensor_copy
+            copy(out=xw[n][:, 0 : w * E], in_=x_source(n).bitcast(FP8))
+
+        def turn(n):
+            w = units[n][2]
+            xt[n] = ps_x.tile([P, 2, 2 * P], F32, name="xt")
+            words = xw[n][:].bitcast(F32)
+            for j in range(w):
+                for u in range(2):
+                    nc.tensor.transpose(
+                        xt[n][:, u, j * P : (j + 1) * P], words[:, j * 256 + u : (j + 1) * 256 : 2], ident[:]
+                    )
+
+        def scale_x(n):
+            r = units[n][2] * P
+            xg[n] = work.tile([P, 2 * P, 4], BF16, name="xg", align_bytes=64)
+            nc.vector.tensor_tensor(
+                out=xg[n][:, 0:r, :].rearrange("p r (u e) -> p r u e", e=2),
+                in0=xt[n][:].bitcast(BF16).rearrange("p u (r e) -> p r u e", e=2)[:, 0:r],
+                in1=xsc[:].unsqueeze(1).to_broadcast([P, r, 2, 2]),
+                op=MULT,
+            )
+
+        def quant_x(n):
+            r = units[n][2] * P
+            xq[n] = work.tile([P, 2 * P], U32, name="xq", align_bytes=64)
+            xs[n] = work.tile([P, 2 * P], U8, name="xs", align_bytes=64)
+            nc.vector.quantize_mx(
+                out=xq[n][:, 0:r].bitcast(FP8X4),
+                scales=xs[n][:, 0:r],
+                in_=xg[n][:, 0:r, :].rearrange("p r t -> p (r t)"),
+            )
+
+        def latent(n):
+            pc[n] = []
+            for j in range(units[n][2]):
+                acc = ps_c.tile([P, 4, P], F32, name="pc")
+                pc[n].append(acc)
+                for t in range(4):
+                    nc.tensor.matmul_mx(
+                        out=acc[:, t, :],
+                        lhsT=wd[:, t * P : (t + 1) * P].bitcast(FP8X4),
+                        lhsT_scale=wd_s[:, t * P : (t + 1) * P],
+                        rhs=xq[n][:, j * P : (j + 1) * P].bitcast(FP8X4),
+                        rhs_scale=xs[n][:, j * P : (j + 1) * P],
+                        start=True,
+                        stop=True,
+                    )
+
+        def rope_key(n):
+            pr[n] = ps_r.tile([P, 2, 2 * RD], F32, name="pr")
+            for j in range(units[n][2]):
+                nc.tensor.matmul_mx(
+                    out=pr[n][:, j, :],
+                    lhsT=xq[n][:, j * P : (j + 1) * P].bitcast(FP8X4),
+                    lhsT_scale=xs[n][:, j * P : (j + 1) * P],
+                    rhs=wd_raw[:, RK:].bitcast(FP8X4),
+                    rhs_scale=wd_s_raw[:, RK:],
+                    start=True,
+                    stop=True,
+                )
+
+        def latent_out(n):
+            cg[n] = work.tile([P, 2 * P, 4], BF16, name="cg", align_bytes=64)
+            for j in range(units[n][2]):
+                nc.scalar.copy(out=cg[n][:, j * P : (j + 1) * P, :], in_=pc[n][j][:].rearrange("p t r -> p r t"))
+
+        def quant_c(n):
+            r = units[n][2] * P
+            cq[n] = work.tile([P, 2 * P], U32, name="cq", align_bytes=64)
+            cs[n] = work.tile([P, 2 * P], U8, name="cs", align_bytes=64)
+            nc.vector.quantize_mx(
+                out=cq[n][:, 0:r].bitcast(FP8X4),
+                scales=cs[n][:, 0:r],
+                in_=cg[n][:, 0:r, :].rearrange("p r t -> p (r t)"),
+            )
+
+        def rotate(n):
+            b, i, w = units[n]
+            tab, i0 = (tab_a, 0) if i < I // 2 else (tab_b, I // 2)
+            ab[n] = work.tile([P, 2, 2, RD], F32, name="ab")
+            nc.vector.tensor_tensor(
+                out=ab[n][:, 0:w],
+                in0=pr[n][:, 0:w, :].rearrange("p w (g c) -> p w g c", g=2),
+                in1=tab[:, i - i0 : i - i0 + w],
+                op=MULT,
+            )
+
+        def rotate_sum(n):
+            w = units[n][2]
+            nc.vector.tensor_tensor(
+                out=kt[n][:, 0:w, 0, DH:], in0=ab[n][:, 0:w, 0, :], in1=ab[n][:, 0:w, 1, :], op=ADD
+            )
+
+        def spread(n):
+            w = units[n][2]
+            out = kt[n][:, 0:w, 1:, DH:]
+            src = kt[n][:, 0:w, 0:1, DH:].to_broadcast([P, w, H - 1, RD])
+            if n == last:
+                nc.vector.tensor_copy(out=out, in_=src)
+            else:
+                nc.gpsimd.tensor_scalar(out=out, in0=src, scalar1=1.0, scalar2=0.0, op0=MULT, op1=ADD)
+
+        def new_out(n):
+            kt[n] = outs.tile([P, 2, H, DV], F32, name="kt")
+            vt[n] = outs.tile([P, 2, H, DV], F32, name="vt")
+
+        def expand(n, j):
+            for g in range(2):
+                acc = ps_u.tile([P, 2, UP], F32, name="pu")
+                pu[n, j, g] = acc
+                cols = slice(g * 2 * UP, (g + 1) * 2 * UP)
+                nc.tensor.matmul_mx(
+                    out=acc[:].rearrange("p h c -> p (h c)"),
+                    lhsT=cq[n][:, j * P : (j + 1) * P].bitcast(FP8X4),
+                    lhsT_scale=cs[n][:, j * P : (j + 1) * P],
+                    rhs=wu[:, cols].bitcast(FP8X4),
+                    rhs_scale=wu_s[:, cols],
+                    start=True,
+                    stop=True,
+                )
+
+        def v_out_copy(n, j, g, copy):
+            copy(out=vt[n][:, j, 2 * g : 2 * g + 2, :], in_=pu[n, j, g][:, :, DH:])
+
+        def k_out_copy(n, j, g, copy):
+            copy(out=kt[n][:, j, 2 * g : 2 * g + 2, 0:DH], in_=pu[n, j, g][:, :, 0:DH])
+
+        def expand_out(n, j):
+            for g in range(2):
+                copy = nc.vector.tensor_copy if n in (0, last) and g == 1 else nc.scalar.copy
+                v_out_copy(n, j, g, copy)
+                k_out_copy(n, j, g, copy)
+
+        def store(n):
+            b, i, w = units[n]
+            for hbm, sb in ((v_out, vt[n]), (k_out, kt[n])):
+                nc.sync.dma_start(
+                    out=hbm[b].rearrange("(p i) h d -> p i (h d)", i=I)[:, i : i + w, :],
+                    in_=sb[:, 0:w].rearrange("p w h d -> p w (h d)"),
+                )
+
+        src = wd_raw[:, RK : RK + RD].bitcast(I32).rearrange("p (j e) -> p j e", e=2)
+        dst = wd_raw[:, RK + RD :].bitcast(I32).rearrange("p (j e) -> p j e", e=2)
+        src_s = wd_s_raw[:, RK : RK + RD].rearrange("p (j e) -> p j e", e=2)
+        dst_s = wd_s_raw[:, RK + RD :].rearrange("p (j e) -> p j e", e=2)
+        for e in range(2):
+            nc.gpsimd.tensor_copy(out=dst[:, :, e], in_=src[:, :, 1 - e])
+        for e in range(2):
+            nc.gpsimd.tensor_copy(out=dst_s[:, :, e], in_=src_s[:, :, 1 - e])
+        tables(tab_a, 0)
+
+        for m in range(4):
+            widen(m)
+        for n in range(-4, last + 1):
+            if n >= 0:
+                new_out(n)
+                quant_c(n)
+                expand(n, 0)
+                if n + 4 <= last:
+                    widen(n + 4)
+                rotate(n)
+            if n == -3:
+                permute(wd[:].bitcast(I32), wd_raw[:, 0:RK].bitcast(I32))
+            if n == -2:
+                permute(wd_s[:], wd_s_raw[:, 0:RK])
+            if 0 <= n + 2 <= last:
+                quant_x(n + 2)
+            if n >= 0:
+                expand_out(n, 0)
+            if 0 <= n + 2 <= last:
+                latent(n + 2)
+            if n >= 0 and units[n][2] == 2:
+                expand(n, 1)
+            if 0 <= n + 2 <= last:
+                latent_out(n + 2)
+            if 0 <= n + 1 <= last:
+                rope_key(n + 1)
+            if n + 4 <= last:
+                turn(n + 4)
+            if n >= 0:
+                rotate_sum(n)
+                spread(n)
+            if n == 0:
+                tables(tab_b, I // 2)
+            if 0 <= n + 3 <= last:
+                scale_x(n + 3)
+            if n >= 0:
+                if units[n][2] == 2:
+                    expand_out(n, 1)
+                store(n)

@@ -16,8 +16,10 @@ ADD = mybir.AluOpType.add
 P = 128
 B, L, E, H, DH, RK, RD = 4, 1024, 512, 4, 64, 512, 128
 I = L // P
+J = RD // 2
 DV = DH + RD
 UP = DH + DV
+HALF = UP // 2
 
 FLOPS = 2 * B * L * E * (RK + RD + H * UP)
 
@@ -26,107 +28,89 @@ def tile_multiheadlatentattention_pa_t_w8_kernel(
     tc, x_bytes, x_scale, cos, sin, wd_words, wd_scales, wu_words, wu_scales, k_out, v_out
 ):
     nc = tc.nc
-    tiles = [(b, i) for b in range(B) for i in range(I)]
+    widths = [1, 1] + [2] * ((B * I - 4) // 2) + [1, 1]
     units = []
-    while tiles:
-        width = 1 if len(units) < 4 or len(tiles) <= 2 else 2
-        units.append((tiles[0][0], tiles[0][1], width))
-        tiles = tiles[width:]
+    for w in widths:
+        first = sum(u[2] for u in units)
+        units.append((first // I, first % I, w))
     last = len(units) - 1
 
     with ExitStack() as ctx:
         keep = ctx.enter_context(tc.tile_pool(name="keep", bufs=1))
         work = ctx.enter_context(tc.tile_pool(name="work", bufs=3))
-        outs = ctx.enter_context(tc.tile_pool(name="outs", bufs=5))
-        ps_x = ctx.enter_context(tc.psum_pool(name="ps_x", bufs=2))
+        outs = ctx.enter_context(tc.tile_pool(name="outs", bufs=6))
+        ps_x = ctx.enter_context(tc.psum_pool(name="ps_x", bufs=1))
         ps_c = ctx.enter_context(tc.psum_pool(name="ps_c", bufs=2))
         ps_r = ctx.enter_context(tc.psum_pool(name="ps_r", bufs=1))
-        ps_u = ctx.enter_context(tc.psum_pool(name="ps_u", bufs=3))
+        ps_u = ctx.enter_context(tc.psum_pool(name="ps_u", bufs=4))
         ctx.enter_context(tc.manual_schedule())
 
-        wd_raw = keep.tile([P, RK + 2 * RD], U32, align_bytes=64)
-        wd_s_raw = keep.tile([P, RK + 2 * RD], U8, align_bytes=64)
+        wd_raw = keep.tile([P, RK + RD], U32, align_bytes=64)
+        wd_s_raw = keep.tile([P, RK + RD], U8, align_bytes=64)
         wd = keep.tile([P, RK], U32, align_bytes=64)
         wd_s = keep.tile([P, RK], U8, align_bytes=64)
-        wu = keep.tile([P, H * UP], U32, align_bytes=64)
+        wu_a = keep.tile([P, H * HALF], U32, align_bytes=64)
+        wu_b = keep.tile([P, H * HALF], U32, align_bytes=64)
+        wu_s_raw = keep.tile([P, H * UP], U8, align_bytes=64)
         wu_s = keep.tile([P, H * UP], U8, align_bytes=64)
-        xb_first = keep.tile([P, 2 * E], U8, align_bytes=64)
-        xb_rest = keep.tile([P, (I - 2) * E], U8, align_bytes=64)
+        xb_a = keep.tile([P, E], U8, align_bytes=64)
+        xb_b = keep.tile([P, 3 * E], U8, align_bytes=64)
+        xb_c = keep.tile([P, (I - 4) * E], U8, align_bytes=64)
         xb_1 = keep.tile([P, I * E], U8, align_bytes=64)
         xb_2 = keep.tile([P, I * E], U8, align_bytes=64)
         xb_3 = keep.tile([P, I * E], U8, align_bytes=64)
         xsc = keep.tile([P, 2, 2], F32)
-        cos_sb = keep.tile([P, I, RD // 2], BF16)
-        sin_sb = keep.tile([P, I, RD // 2], BF16)
-        tab_a = keep.tile([P, I // 2, 2, RD], BF16)
-        tab_b = keep.tile([P, I // 2, 2, RD], BF16)
+        tab = keep.tile([P, 2, 2, I * J], BF16)
         ident = keep.tile([P, P], F32)
-        warm = keep.tile([P, 8], F32)
 
         nc.vector.memset(wd_s_raw[:].bitcast(I32), 0)
-        nc.vector.memset(wu_s[:].bitcast(I32), 0)
-        nc.vector.memset(warm[:], 0.0)
-        nc.scalar.copy(out=warm[:, 4:8], in_=warm[:, 0:4])
+        nc.vector.memset(wu_s_raw[:].bitcast(I32), 0)
         make_identity(nc, ident[:])
-        nc.gpsimd.dma_start(out=xsc[:], in_=x_scale.rearrange("a b (p u e) -> p (a b u) e", u=2, e=2))
-        nc.gpsimd.dma_start(out=cos_sb[:], in_=cos.rearrange("(p i) j -> p i j", i=I))
-        nc.gpsimd.dma_start(out=sin_sb[:], in_=sin.rearrange("(p i) j -> p i j", i=I))
+        nc.gpsimd.dma_start(out=tab[:, 0, 0, :], in_=cos.rearrange("(p i) j -> p (i j)", i=I))
+        nc.gpsimd.dma_start(out=tab[:, 0, 1, :], in_=sin.rearrange("(p i) j -> p (i j)", i=I))
         xv = [x_bytes[b].rearrange("(p i) k -> p (i k)", i=I) for b in range(B)]
-        nc.sync.dma_start(out=xb_first[:], in_=xv[0][:, 0 : 2 * E])
-        nc.sync.dma_start(
-            out=wd_raw[:, 0 : RK + RD].bitcast(I32), in_=wd_words[0].rearrange("p n t -> p (n t)").bitcast(I32)
-        )
+        nc.sync.dma_start(out=xb_a[:], in_=xv[0][:, 0:E])
+        nc.sync.dma_start(out=xsc[:], in_=x_scale.rearrange("a b (p u e) -> p (a b u) e", u=2, e=2))
+        nc.sync.dma_start(out=wd_raw[:].bitcast(I32), in_=wd_words[0].rearrange("p n t -> p (n t)").bitcast(I32))
+        nc.sync.dma_start(out=xb_b[:], in_=xv[0][:, E : 4 * E])
         for q in range(4):
             nc.sync.dma_start(
-                out=wd_s_raw[32 * q : 32 * q + 4, 0 : RK + RD].bitcast(I32),
+                out=wd_s_raw[32 * q : 32 * q + 4, :].bitcast(I32),
                 in_=wd_scales[0, 4 * q : 4 * q + 4, :].bitcast(I32),
             )
-        nc.sync.dma_start(out=xb_rest[:], in_=xv[0][:, 2 * E :])
-        nc.sync.dma_start(out=wu[:].bitcast(I32), in_=wu_words[0].rearrange("p n t -> p (n t)").bitcast(I32))
+        wu_v = wu_words[0].rearrange("p n t -> p (n t)").bitcast(I32).rearrange("p (h s c) -> p h s c", h=H, s=2)
+        nc.sync.dma_start(out=wu_a[:].bitcast(I32).rearrange("p (h c) -> p h c", h=H), in_=wu_v[:, :, 0, :])
         for q in range(4):
             nc.sync.dma_start(
-                out=wu_s[32 * q : 32 * q + 4, :].bitcast(I32), in_=wu_scales[0, 4 * q : 4 * q + 4, :].bitcast(I32)
+                out=wu_s_raw[32 * q : 32 * q + 4, :].bitcast(I32), in_=wu_scales[0, 4 * q : 4 * q + 4, :].bitcast(I32)
             )
+        nc.sync.dma_start(out=wu_b[:].bitcast(I32).rearrange("p (h c) -> p h c", h=H), in_=wu_v[:, :, 1, :])
+        nc.sync.dma_start(out=xb_c[:], in_=xv[0][:, 4 * E :])
         nc.sync.dma_start(out=xb_1[:], in_=xv[1])
         nc.sync.dma_start(out=xb_2[:], in_=xv[2])
         nc.sync.dma_start(out=xb_3[:], in_=xv[3])
 
-        def tables(tab, i0):
-            view = tab[:].rearrange("p i g (j e) -> p i g j e", e=2)
-            for g, src in ((0, cos_sb), (1, sin_sb)):
-                for e in range(2):
-                    factor = -1.0 if (g, e) == (1, 0) else 1.0
-                    nc.gpsimd.tensor_scalar(
-                        out=view[:, :, g, :, e],
-                        in0=src[:, i0 : i0 + I // 2, :],
-                        scalar1=factor,
-                        scalar2=0.0,
-                        op0=MULT,
-                        op1=ADD,
-                    )
-
-        def permute(dst, src):
-            nc.vector.tensor_copy(
-                out=dst.rearrange("p (t m) -> p t m", t=4), in_=src.rearrange("p (m t) -> p t m", t=4)
-            )
-
-        xw, xt, xg, xq, xs, pc, cg, cq, cs, pr, ab, kt, vt, pu = [{} for j in range(14)]
+        xw, xt, xg, xq, xs, pc, cg, cq, cs, pr, ab, kv, pu = [{} for j in range(13)]
 
         def x_source(n):
             b, i, w = units[n]
             if b > 0:
                 return [xb_1, xb_2, xb_3][b - 1][:, i * E : (i + w) * E]
-            return xb_first[:, i * E : (i + w) * E] if i < 2 else xb_rest[:, (i - 2) * E : (i - 2 + w) * E]
+            if i == 0:
+                return xb_a[:]
+            return xb_b[:, (i - 1) * E : (i - 1 + w) * E] if i < 4 else xb_c[:, (i - 4) * E : (i - 4 + w) * E]
 
-        def widen(n):
+        def widen(n, copy):
             w = units[n][2]
             xw[n] = work.tile([P, 2 * E], BF16, name="xw", bufs=4)
-            copy = nc.scalar.copy if n in (1, 2, 3) else nc.vector.tensor_copy
             copy(out=xw[n][:, 0 : w * E], in_=x_source(n).bitcast(FP8))
 
         def turn(n):
             w = units[n][2]
-            xt[n] = ps_x.tile([P, 2, 2 * P], F32, name="xt")
+            if n == 1:
+                xt[n] = ps_u.tile([P, 2, 2 * P], F32, name="pu")
+            else:
+                xt[n] = ps_x.tile([P, 2, 2 * P], F32, name="xt")
             words = xw[n][:].bitcast(F32)
             for j in range(w):
                 for u in range(2):
@@ -171,10 +155,10 @@ def tile_multiheadlatentattention_pa_t_w8_kernel(
                     )
 
         def rope_key(n):
-            pr[n] = ps_r.tile([P, 2, 2 * RD], F32, name="pr")
+            pr[n] = ps_r.tile([P, 2 * RD], F32, name="pr")
             for j in range(units[n][2]):
                 nc.tensor.matmul_mx(
-                    out=pr[n][:, j, :],
+                    out=pr[n][:, j * RD : (j + 1) * RD],
                     lhsT=xq[n][:, j * P : (j + 1) * P].bitcast(FP8X4),
                     lhsT_scale=xs[n][:, j * P : (j + 1) * P],
                     rhs=wd_raw[:, RK:].bitcast(FP8X4),
@@ -200,115 +184,122 @@ def tile_multiheadlatentattention_pa_t_w8_kernel(
 
         def rotate(n):
             b, i, w = units[n]
-            tab, i0 = (tab_a, 0) if i < I // 2 else (tab_b, I // 2)
-            ab[n] = work.tile([P, 2, 2, RD], F32, name="ab")
+            ab[n] = work.tile([P, 2, 2 * RD], F32, name="ab")
             nc.vector.tensor_tensor(
-                out=ab[n][:, 0:w],
-                in0=pr[n][:, 0:w, :].rearrange("p w (g c) -> p w g c", g=2),
-                in1=tab[:, i - i0 : i - i0 + w],
+                out=ab[n][:, :, 0 : w * RD].rearrange("p a (q e) -> p a q e", e=2),
+                in0=pr[n][:, 0 : w * RD].rearrange("p (q a) -> p a q", a=2).unsqueeze(3).to_broadcast([P, 2, w * J, 2]),
+                in1=tab[:, :, :, i * J : (i + w) * J].rearrange("p a e q -> p a q e"),
                 op=MULT,
             )
 
         def rotate_sum(n):
             w = units[n][2]
+            kv[n] = outs.tile([P, 2, 2, H, DV], F32, name="kv")
             nc.vector.tensor_tensor(
-                out=kt[n][:, 0:w, 0, DH:], in0=ab[n][:, 0:w, 0, :], in1=ab[n][:, 0:w, 1, :], op=ADD
+                out=kv[n][:, 0, 0:w, 0, DH:],
+                in0=ab[n][:, 0, 0 : w * RD].rearrange("p (w c) -> p w c", w=w),
+                in1=ab[n][:, 1, 0 : w * RD].rearrange("p (w c) -> p w c", w=w),
+                op=ADD,
             )
 
         def spread(n):
             w = units[n][2]
-            out = kt[n][:, 0:w, 1:, DH:]
-            src = kt[n][:, 0:w, 0:1, DH:].to_broadcast([P, w, H - 1, RD])
-            if n == last:
-                nc.vector.tensor_copy(out=out, in_=src)
-            else:
-                nc.gpsimd.tensor_scalar(out=out, in0=src, scalar1=1.0, scalar2=0.0, op0=MULT, op1=ADD)
+            out = kv[n][:, 0, 0:w, 1:, DH:]
+            src = kv[n][:, 0, 0:w, 0:1, DH:].to_broadcast([P, w, H - 1, RD])
+            nc.gpsimd.tensor_scalar(out=out, in0=src, scalar1=1.0, scalar2=0.0, op0=MULT, op1=ADD)
 
-        def new_out(n):
-            kt[n] = outs.tile([P, 2, H, DV], F32, name="kt")
-            vt[n] = outs.tile([P, 2, H, DV], F32, name="vt")
+        def expand(n):
+            for s, words in enumerate((wu_a, wu_b)):
+                for j in range(units[n][2]):
+                    acc = ps_u.tile([P, H * HALF], F32, name="pu")
+                    pu[n, s, j] = acc
+                    nc.tensor.matmul_mx(
+                        out=acc[:],
+                        lhsT=cq[n][:, j * P : (j + 1) * P].bitcast(FP8X4),
+                        lhsT_scale=cs[n][:, j * P : (j + 1) * P],
+                        rhs=words[:].bitcast(FP8X4),
+                        rhs_scale=wu_s[:, s * H * HALF : (s + 1) * H * HALF],
+                        start=True,
+                        stop=True,
+                    )
 
-        def expand(n, j):
-            for g in range(2):
-                acc = ps_u.tile([P, 2, UP], F32, name="pu")
-                pu[n, j, g] = acc
-                cols = slice(g * 2 * UP, (g + 1) * 2 * UP)
-                nc.tensor.matmul_mx(
-                    out=acc[:].rearrange("p h c -> p (h c)"),
-                    lhsT=cq[n][:, j * P : (j + 1) * P].bitcast(FP8X4),
-                    lhsT_scale=cs[n][:, j * P : (j + 1) * P],
-                    rhs=wu[:, cols].bitcast(FP8X4),
-                    rhs_scale=wu_s[:, cols],
-                    start=True,
-                    stop=True,
+        def first_out(n):
+            for j in range(units[n][2]):
+                nc.scalar.copy(
+                    out=kv[n][:, :, j, :, 0:DH].rearrange("p g h c -> p h g c"),
+                    in_=pu[n, 0, j][:].rearrange("p (h g c) -> p h g c", h=H, g=2),
                 )
 
-        def v_out_copy(n, j, g, copy):
-            copy(out=vt[n][:, j, 2 * g : 2 * g + 2, :], in_=pu[n, j, g][:, :, DH:])
+        def second_out(n, copy):
+            for j in range(units[n][2]):
+                copy(out=kv[n][:, 1, j, :, DH:], in_=pu[n, 1, j][:].rearrange("p (h c) -> p h c", h=H))
 
-        def k_out_copy(n, j, g, copy):
-            copy(out=kt[n][:, j, 2 * g : 2 * g + 2, 0:DH], in_=pu[n, j, g][:, :, 0:DH])
-
-        def expand_out(n, j):
-            for g in range(2):
-                copy = nc.vector.tensor_copy if n in (0, last) and g == 1 else nc.scalar.copy
-                v_out_copy(n, j, g, copy)
-                k_out_copy(n, j, g, copy)
-
-        def store(n):
+        def store(n, g):
             b, i, w = units[n]
-            for hbm, sb in ((v_out, vt[n]), (k_out, kt[n])):
-                nc.sync.dma_start(
-                    out=hbm[b].rearrange("(p i) h d -> p i (h d)", i=I)[:, i : i + w, :],
-                    in_=sb[:, 0:w].rearrange("p w h d -> p w (h d)"),
-                )
+            nc.sync.dma_start(
+                out=(k_out, v_out)[g][b].rearrange("(p i) h d -> p i (h d)", i=I)[:, i : i + w, :],
+                in_=kv[n][:, g, 0:w].rearrange("p w h d -> p w (h d)"),
+            )
 
-        src = wd_raw[:, RK : RK + RD].bitcast(I32).rearrange("p (j e) -> p j e", e=2)
-        dst = wd_raw[:, RK + RD :].bitcast(I32).rearrange("p (j e) -> p j e", e=2)
-        src_s = wd_s_raw[:, RK : RK + RD].rearrange("p (j e) -> p j e", e=2)
-        dst_s = wd_s_raw[:, RK + RD :].rearrange("p (j e) -> p j e", e=2)
-        for e in range(2):
-            nc.gpsimd.tensor_copy(out=dst[:, :, e], in_=src[:, :, 1 - e])
-        for e in range(2):
-            nc.gpsimd.tensor_copy(out=dst_s[:, :, e], in_=src_s[:, :, 1 - e])
-        tables(tab_a, 0)
-
-        for m in range(4):
-            widen(m)
-        for n in range(-4, last + 1):
-            if n >= 0:
-                new_out(n)
-                quant_c(n)
-                expand(n, 0)
-                if n + 4 <= last:
-                    widen(n + 4)
-                rotate(n)
-            if n == -3:
-                permute(wd[:].bitcast(I32), wd_raw[:, 0:RK].bitcast(I32))
-            if n == -2:
-                permute(wd_s[:], wd_s_raw[:, 0:RK])
-            if 0 <= n + 2 <= last:
-                quant_x(n + 2)
-            if n >= 0:
-                expand_out(n, 0)
-            if 0 <= n + 2 <= last:
-                latent(n + 2)
-            if n >= 0 and units[n][2] == 2:
-                expand(n, 1)
-            if 0 <= n + 2 <= last:
-                latent_out(n + 2)
-            if 0 <= n + 1 <= last:
-                rope_key(n + 1)
-            if n + 4 <= last:
-                turn(n + 4)
-            if n >= 0:
-                rotate_sum(n)
-                spread(n)
+        widen(0, nc.vector.tensor_copy)
+        turn(0)
+        widen(1, nc.scalar.copy)
+        widen(2, nc.scalar.copy)
+        nc.vector.tensor_copy(
+            out=wd[:].bitcast(I32).rearrange("p (t m) -> p t m", t=4),
+            in_=wd_raw[:, 0:RK].bitcast(I32).rearrange("p (m t) -> p t m", t=4),
+        )
+        scale_x(0)
+        turn(1)
+        nc.vector.tensor_copy(
+            out=wd_s[:].rearrange("p (t m) -> p t m", t=4),
+            in_=wd_s_raw[:, 0:RK].rearrange("p (m t) -> p t m", t=4),
+        )
+        quant_x(0)
+        latent(0)
+        rope_key(0)
+        latent_out(0)
+        scale_x(1)
+        turn(2)
+        nc.vector.tensor_copy(out=tab[:, 1, 1, :], in_=tab[:, 0, 0, :])
+        nc.vector.tensor_scalar(out=tab[:, 1, 0, :], in0=tab[:, 0, 1, :], scalar1=-1.0, scalar2=None, op0=MULT)
+        quant_x(1)
+        latent(1)
+        rotate(0)
+        rope_key(1)
+        nc.vector.tensor_copy(
+            out=wu_s[:].bitcast(I32).rearrange("p (s h c) -> p s h c", s=2, h=H),
+            in_=wu_s_raw[:].bitcast(I32).rearrange("p (h s c) -> p s h c", s=2, h=H),
+        )
+        quant_c(0)
+        expand(0)
+        for n in range(last + 1):
+            on_vector = n >= last - 2
+            rotate_sum(n)
+            spread(n)
             if n == 0:
-                tables(tab_b, I // 2)
-            if 0 <= n + 3 <= last:
-                scale_x(n + 3)
-            if n >= 0:
-                if units[n][2] == 2:
-                    expand_out(n, 1)
-                store(n)
+                widen(3, nc.vector.tensor_copy)
+            if n + 2 <= last:
+                scale_x(n + 2)
+            if n + 3 <= last:
+                turn(n + 3)
+            if n + 1 <= last:
+                latent_out(n + 1)
+                rotate(n + 1)
+            first_out(n)
+            store(n, 0)
+            if not on_vector:
+                second_out(n, nc.scalar.copy)
+                store(n, 1)
+            if n + 2 <= last:
+                quant_x(n + 2)
+                latent(n + 2)
+                rope_key(n + 2)
+            if on_vector:
+                second_out(n, nc.vector.tensor_copy)
+                store(n, 1)
+            if n + 1 <= last:
+                quant_c(n + 1)
+                expand(n + 1)
+            if n + 4 <= last:
+                widen(n + 4, nc.vector.tensor_copy)

@@ -39,10 +39,10 @@ def tile_multiheadlatentattention_pa_t_w8_kernel(
         keep = ctx.enter_context(tc.tile_pool(name="keep", bufs=1))
         work = ctx.enter_context(tc.tile_pool(name="work", bufs=3))
         outs = ctx.enter_context(tc.tile_pool(name="outs", bufs=6))
-        ps_x = ctx.enter_context(tc.psum_pool(name="ps_x", bufs=1))
+        ps_x = ctx.enter_context(tc.psum_pool(name="ps_x", bufs=2))
         ps_c = ctx.enter_context(tc.psum_pool(name="ps_c", bufs=2))
         ps_r = ctx.enter_context(tc.psum_pool(name="ps_r", bufs=1))
-        ps_u = ctx.enter_context(tc.psum_pool(name="ps_u", bufs=4))
+        ps_u = ctx.enter_context(tc.psum_pool(name="ps_u", bufs=3))
         ctx.enter_context(tc.manual_schedule())
 
         wd_raw = keep.tile([P, RK + RD], U32, align_bytes=64)
@@ -53,8 +53,8 @@ def tile_multiheadlatentattention_pa_t_w8_kernel(
         wu_b = keep.tile([P, H * HALF], U32, align_bytes=64)
         wu_s_raw = keep.tile([P, H * UP], U8, align_bytes=64)
         wu_s = keep.tile([P, H * UP], U8, align_bytes=64)
-        xb_a = keep.tile([P, E], U8, align_bytes=64)
-        xb_b = keep.tile([P, 3 * E], U8, align_bytes=64)
+        xb_a = keep.tile([P, 2 * E], U8, align_bytes=64)
+        xb_b = keep.tile([P, 2 * E], U8, align_bytes=64)
         xb_c = keep.tile([P, (I - 4) * E], U8, align_bytes=64)
         xb_1 = keep.tile([P, I * E], U8, align_bytes=64)
         xb_2 = keep.tile([P, I * E], U8, align_bytes=64)
@@ -63,29 +63,29 @@ def tile_multiheadlatentattention_pa_t_w8_kernel(
         tab = keep.tile([P, 2, 2, I * J], BF16)
         ident = keep.tile([P, P], F32)
 
-        nc.vector.memset(wd_s_raw[:].bitcast(I32), 0)
+        nc.gpsimd.memset(wd_s_raw[:].bitcast(I32), 0)
         nc.vector.memset(wu_s_raw[:].bitcast(I32), 0)
         make_identity(nc, ident[:])
-        nc.gpsimd.dma_start(out=tab[:, 0, 0, :], in_=cos.rearrange("(p i) j -> p (i j)", i=I))
-        nc.gpsimd.dma_start(out=tab[:, 0, 1, :], in_=sin.rearrange("(p i) j -> p (i j)", i=I))
         xv = [x_bytes[b].rearrange("(p i) k -> p (i k)", i=I) for b in range(B)]
-        nc.sync.dma_start(out=xb_a[:], in_=xv[0][:, 0:E])
+        wu_v = wu_words[0].rearrange("p n t -> p (n t)").bitcast(I32).rearrange("p (h s c) -> p h s c", h=H, s=2)
+        nc.sync.dma_start(out=xb_a[:], in_=xv[0][:, 0 : 2 * E])
         nc.sync.dma_start(out=xsc[:], in_=x_scale.rearrange("a b (p u e) -> p (a b u) e", u=2, e=2))
-        nc.sync.dma_start(out=wd_raw[:].bitcast(I32), in_=wd_words[0].rearrange("p n t -> p (n t)").bitcast(I32))
-        nc.sync.dma_start(out=xb_b[:], in_=xv[0][:, E : 4 * E])
         for q in range(4):
             nc.sync.dma_start(
                 out=wd_s_raw[32 * q : 32 * q + 4, :].bitcast(I32),
                 in_=wd_scales[0, 4 * q : 4 * q + 4, :].bitcast(I32),
             )
-        wu_v = wu_words[0].rearrange("p n t -> p (n t)").bitcast(I32).rearrange("p (h s c) -> p h s c", h=H, s=2)
-        nc.sync.dma_start(out=wu_a[:].bitcast(I32).rearrange("p (h c) -> p h c", h=H), in_=wu_v[:, :, 0, :])
+        nc.sync.dma_start(out=xb_b[:], in_=xv[0][:, 2 * E : 4 * E])
+        nc.sync.dma_start(out=wd_raw[:].bitcast(I32), in_=wd_words[0].rearrange("p n t -> p (n t)").bitcast(I32))
+        nc.sync.dma_start(out=xb_c[:], in_=xv[0][:, 4 * E :])
+        nc.sync.dma_start(out=tab[:, 0, 0, :], in_=cos.rearrange("(p i) j -> p (i j)", i=I))
+        nc.sync.dma_start(out=tab[:, 0, 1, :], in_=sin.rearrange("(p i) j -> p (i j)", i=I))
         for q in range(4):
             nc.sync.dma_start(
                 out=wu_s_raw[32 * q : 32 * q + 4, :].bitcast(I32), in_=wu_scales[0, 4 * q : 4 * q + 4, :].bitcast(I32)
             )
+        nc.sync.dma_start(out=wu_a[:].bitcast(I32).rearrange("p (h c) -> p h c", h=H), in_=wu_v[:, :, 0, :])
         nc.sync.dma_start(out=wu_b[:].bitcast(I32).rearrange("p (h c) -> p h c", h=H), in_=wu_v[:, :, 1, :])
-        nc.sync.dma_start(out=xb_c[:], in_=xv[0][:, 4 * E :])
         nc.sync.dma_start(out=xb_1[:], in_=xv[1])
         nc.sync.dma_start(out=xb_2[:], in_=xv[2])
         nc.sync.dma_start(out=xb_3[:], in_=xv[3])
@@ -96,18 +96,18 @@ def tile_multiheadlatentattention_pa_t_w8_kernel(
             b, i, w = units[n]
             if b > 0:
                 return [xb_1, xb_2, xb_3][b - 1][:, i * E : (i + w) * E]
-            if i == 0:
-                return xb_a[:]
-            return xb_b[:, (i - 1) * E : (i - 1 + w) * E] if i < 4 else xb_c[:, (i - 4) * E : (i - 4 + w) * E]
+            if i < 2:
+                return xb_a[:, i * E : (i + w) * E]
+            return xb_b[:] if i < 4 else xb_c[:, (i - 4) * E : (i - 4 + w) * E]
 
         def widen(n, copy):
             w = units[n][2]
-            xw[n] = work.tile([P, 2 * E], BF16, name="xw", bufs=4)
+            xw[n] = work.tile([P, 2 * E], BF16, name="xw", bufs=5)
             copy(out=xw[n][:, 0 : w * E], in_=x_source(n).bitcast(FP8))
 
         def turn(n):
             w = units[n][2]
-            if n == 1:
+            if n == 2:
                 xt[n] = ps_u.tile([P, 2, 2 * P], F32, name="pu")
             else:
                 xt[n] = ps_x.tile([P, 2, 2 * P], F32, name="xt")
@@ -138,21 +138,18 @@ def tile_multiheadlatentattention_pa_t_w8_kernel(
                 in_=xg[n][:, 0:r, :].rearrange("p r t -> p (r t)"),
             )
 
-        def latent(n):
-            pc[n] = []
-            for j in range(units[n][2]):
-                acc = ps_c.tile([P, 4, P], F32, name="pc")
-                pc[n].append(acc)
-                for t in range(4):
-                    nc.tensor.matmul_mx(
-                        out=acc[:, t, :],
-                        lhsT=wd[:, t * P : (t + 1) * P].bitcast(FP8X4),
-                        lhsT_scale=wd_s[:, t * P : (t + 1) * P],
-                        rhs=xq[n][:, j * P : (j + 1) * P].bitcast(FP8X4),
-                        rhs_scale=xs[n][:, j * P : (j + 1) * P],
-                        start=True,
-                        stop=True,
-                    )
+        def latent(n, j):
+            pc[n, j] = ps_c.tile([P, 4, P], F32, name="pc")
+            for t in range(4):
+                nc.tensor.matmul_mx(
+                    out=pc[n, j][:, t, :],
+                    lhsT=wd[:, t * P : (t + 1) * P].bitcast(FP8X4),
+                    lhsT_scale=wd_s[:, t * P : (t + 1) * P],
+                    rhs=xq[n][:, j * P : (j + 1) * P].bitcast(FP8X4),
+                    rhs_scale=xs[n][:, j * P : (j + 1) * P],
+                    start=True,
+                    stop=True,
+                )
 
         def rope_key(n):
             pr[n] = ps_r.tile([P, 2 * RD], F32, name="pr")
@@ -167,19 +164,15 @@ def tile_multiheadlatentattention_pa_t_w8_kernel(
                     stop=True,
                 )
 
-        def latent_out(n):
-            cg[n] = work.tile([P, 2 * P, 4], BF16, name="cg", align_bytes=64)
-            for j in range(units[n][2]):
-                nc.scalar.copy(out=cg[n][:, j * P : (j + 1) * P, :], in_=pc[n][j][:].rearrange("p t r -> p r t"))
+        def latent_out(n, j):
+            cg[n, j] = work.tile([P, P, 4], BF16, name="cg", align_bytes=64, bufs=4)
+            nc.scalar.copy(out=cg[n, j][:], in_=pc[n, j][:].rearrange("p t r -> p r t"))
 
-        def quant_c(n):
-            r = units[n][2] * P
-            cq[n] = work.tile([P, 2 * P], U32, name="cq", align_bytes=64)
-            cs[n] = work.tile([P, 2 * P], U8, name="cs", align_bytes=64)
+        def quant_c(n, j):
+            cq[n, j] = work.tile([P, P], U32, name="cq", align_bytes=64, bufs=4)
+            cs[n, j] = work.tile([P, P], U8, name="cs", align_bytes=64, bufs=4)
             nc.vector.quantize_mx(
-                out=cq[n][:, 0:r].bitcast(FP8X4),
-                scales=cs[n][:, 0:r],
-                in_=cg[n][:, 0:r, :].rearrange("p r t -> p (r t)"),
+                out=cq[n, j][:].bitcast(FP8X4), scales=cs[n, j][:], in_=cg[n, j][:].rearrange("p r t -> p (r t)")
             )
 
         def rotate(n):
@@ -195,44 +188,75 @@ def tile_multiheadlatentattention_pa_t_w8_kernel(
         def rotate_sum(n):
             w = units[n][2]
             kv[n] = outs.tile([P, 2, 2, H, DV], F32, name="kv")
-            nc.vector.tensor_tensor(
-                out=kv[n][:, 0, 0:w, 0, DH:],
-                in0=ab[n][:, 0, 0 : w * RD].rearrange("p (w c) -> p w c", w=w),
-                in1=ab[n][:, 1, 0 : w * RD].rearrange("p (w c) -> p w c", w=w),
-                op=ADD,
-            )
-
-        def spread(n):
-            w = units[n][2]
-            out = kv[n][:, 0, 0:w, 1:, DH:]
-            src = kv[n][:, 0, 0:w, 0:1, DH:].to_broadcast([P, w, H - 1, RD])
-            nc.gpsimd.tensor_scalar(out=out, in0=src, scalar1=1.0, scalar2=0.0, op0=MULT, op1=ADD)
-
-        def expand(n):
-            for s, words in enumerate((wu_a, wu_b)):
-                for j in range(units[n][2]):
-                    acc = ps_u.tile([P, H * HALF], F32, name="pu")
-                    pu[n, s, j] = acc
-                    nc.tensor.matmul_mx(
-                        out=acc[:],
-                        lhsT=cq[n][:, j * P : (j + 1) * P].bitcast(FP8X4),
-                        lhsT_scale=cs[n][:, j * P : (j + 1) * P],
-                        rhs=words[:].bitcast(FP8X4),
-                        rhs_scale=wu_s[:, s * H * HALF : (s + 1) * H * HALF],
-                        start=True,
-                        stop=True,
-                    )
-
-        def first_out(n):
-            for j in range(units[n][2]):
-                nc.scalar.copy(
-                    out=kv[n][:, :, j, :, 0:DH].rearrange("p g h c -> p h g c"),
-                    in_=pu[n, 0, j][:].rearrange("p (h g c) -> p h g c", h=H, g=2),
+            if w == 1:
+                nc.vector.tensor_tensor(
+                    out=kv[n][:, 0, 0, :, DH:],
+                    in0=ab[n][:, 0:1, 0:RD].to_broadcast([P, H, RD]),
+                    in1=ab[n][:, 1:2, 0:RD].to_broadcast([P, H, RD]),
+                    op=ADD,
+                )
+            else:
+                nc.vector.tensor_tensor(
+                    out=kv[n][:, 0, :, 0, DH:],
+                    in0=ab[n][:, 0, :].rearrange("p (w c) -> p w c", w=w),
+                    in1=ab[n][:, 1, :].rearrange("p (w c) -> p w c", w=w),
+                    op=ADD,
                 )
 
-        def second_out(n, copy):
-            for j in range(units[n][2]):
-                copy(out=kv[n][:, 1, j, :, DH:], in_=pu[n, 1, j][:].rearrange("p (h c) -> p h c", h=H))
+        def spread(n):
+            if units[n][2] == 2:
+                nc.gpsimd.tensor_scalar(
+                    out=kv[n][:, 0, :, 1:, DH:],
+                    in0=kv[n][:, 0, :, 0:1, DH:].to_broadcast([P, 2, H - 1, RD]),
+                    scalar1=1.0,
+                    scalar2=0.0,
+                    op0=MULT,
+                    op1=ADD,
+                )
+
+        def expand(n, s, j):
+            acc = ps_u.tile([P, H * HALF], F32, name="pu")
+            pu[n, s, j] = acc
+            nc.tensor.matmul_mx(
+                out=acc[:],
+                lhsT=cq[n, j][:].bitcast(FP8X4),
+                lhsT_scale=cs[n, j][:],
+                rhs=(wu_a, wu_b)[s][:].bitcast(FP8X4),
+                rhs_scale=wu_s[:, s * H * HALF : (s + 1) * H * HALF],
+                start=True,
+                stop=True,
+            )
+
+        def first_out(n, j):
+            nc.scalar.copy(
+                out=kv[n][:, :, j, :, 0:DH].rearrange("p g h c -> p h g c"),
+                in_=pu[n, 0, j][:].rearrange("p (h g c) -> p h g c", h=H, g=2),
+            )
+
+        def second_out(n, j, copy):
+            copy(out=kv[n][:, 1, j, :, DH:], in_=pu[n, 1, j][:].rearrange("p (h c) -> p h c", h=H))
+
+        def order_latent_words():
+            nc.vector.tensor_copy(
+                out=wd[:].bitcast(I32).rearrange("p (t m) -> p t m", t=4),
+                in_=wd_raw[:, 0:RK].bitcast(I32).rearrange("p (m t) -> p t m", t=4),
+            )
+
+        def order_latent_scales():
+            nc.vector.tensor_copy(
+                out=wd_s[:].rearrange("p (t m) -> p t m", t=4),
+                in_=wd_s_raw[:, 0:RK].rearrange("p (m t) -> p t m", t=4),
+            )
+
+        def order_up_scales():
+            nc.vector.tensor_copy(
+                out=wu_s[:].bitcast(I32).rearrange("p (s h c) -> p s h c", s=2, h=H),
+                in_=wu_s_raw[:].bitcast(I32).rearrange("p (h s c) -> p s h c", s=2, h=H),
+            )
+
+        def finish_table():
+            nc.vector.tensor_copy(out=tab[:, 1, 1, :], in_=tab[:, 0, 0, :])
+            nc.vector.tensor_scalar(out=tab[:, 1, 0, :], in0=tab[:, 0, 1, :], scalar1=-1.0, scalar2=None, op0=MULT)
 
         def store(n, g):
             b, i, w = units[n]
@@ -243,63 +267,87 @@ def tile_multiheadlatentattention_pa_t_w8_kernel(
 
         widen(0, nc.vector.tensor_copy)
         turn(0)
-        widen(1, nc.scalar.copy)
-        widen(2, nc.scalar.copy)
-        nc.vector.tensor_copy(
-            out=wd[:].bitcast(I32).rearrange("p (t m) -> p t m", t=4),
-            in_=wd_raw[:, 0:RK].bitcast(I32).rearrange("p (m t) -> p t m", t=4),
-        )
-        scale_x(0)
+        widen(1, nc.vector.tensor_copy)
         turn(1)
-        nc.vector.tensor_copy(
-            out=wd_s[:].rearrange("p (t m) -> p t m", t=4),
-            in_=wd_s_raw[:, 0:RK].rearrange("p (m t) -> p t m", t=4),
-        )
-        quant_x(0)
-        latent(0)
-        rope_key(0)
-        latent_out(0)
-        scale_x(1)
+        widen(2, nc.scalar.copy)
         turn(2)
-        nc.vector.tensor_copy(out=tab[:, 1, 1, :], in_=tab[:, 0, 0, :])
-        nc.vector.tensor_scalar(out=tab[:, 1, 0, :], in0=tab[:, 0, 1, :], scalar1=-1.0, scalar2=None, op0=MULT)
+        widen(3, nc.scalar.copy)
+        order_latent_scales()
+        scale_x(0)
+        order_latent_words()
+        quant_x(0)
+        latent(0, 0)
+        rope_key(0)
+        scale_x(1)
+        finish_table()
         quant_x(1)
-        latent(1)
+        latent(1, 0)
+        latent_out(0, 0)
+        latent_out(1, 0)
+        widen(4, nc.scalar.copy)
+        scale_x(2)
+        turn(3)
+        order_up_scales()
+        quant_c(0, 0)
         rotate(0)
+        quant_x(2)
+        expand(0, 0, 0)
         rope_key(1)
-        nc.vector.tensor_copy(
-            out=wu_s[:].bitcast(I32).rearrange("p (s h c) -> p s h c", s=2, h=H),
-            in_=wu_s_raw[:].bitcast(I32).rearrange("p (h s c) -> p s h c", s=2, h=H),
-        )
-        quant_c(0)
-        expand(0)
-        for n in range(last + 1):
-            on_vector = n >= last - 2
-            rotate_sum(n)
-            spread(n)
-            if n == 0:
-                widen(3, nc.vector.tensor_copy)
-            if n + 2 <= last:
-                scale_x(n + 2)
-            if n + 3 <= last:
-                turn(n + 3)
-            if n + 1 <= last:
-                latent_out(n + 1)
-                rotate(n + 1)
-            first_out(n)
-            store(n, 0)
-            if not on_vector:
-                second_out(n, nc.scalar.copy)
-                store(n, 1)
-            if n + 2 <= last:
-                quant_x(n + 2)
-                latent(n + 2)
-                rope_key(n + 2)
-            if on_vector:
-                second_out(n, nc.vector.tensor_copy)
-                store(n, 1)
-            if n + 1 <= last:
-                quant_c(n + 1)
-                expand(n + 1)
-            if n + 4 <= last:
-                widen(n + 4, nc.vector.tensor_copy)
+        latent(2, 0)
+        rotate_sum(0)
+        quant_c(1, 0)
+        expand(1, 0, 0)
+        latent(2, 1)
+        rotate(1)
+        rope_key(2)
+        first_out(0, 0)
+        store(0, 0)
+        latent_out(2, 0)
+        expand(0, 1, 0)
+        scale_x(3)
+        rotate_sum(1)
+        first_out(1, 0)
+        store(1, 0)
+        expand(1, 1, 0)
+        turn(4)
+        rotate(2)
+        for n in range(2, last + 2):
+            w = units[n][2] if n <= last else 0
+            ahead = units[n + 1][2] if n < last else 0
+            for j in range(w):
+                if (n, j) not in cg:
+                    latent_out(n, j)
+            for m in range(n - 1 if n > 2 else 0, n):
+                for j in range(units[m][2]):
+                    second_out(m, j, nc.vector.tensor_copy if n >= last else nc.scalar.copy)
+                store(m, 1)
+            if w:
+                quant_c(n, 0)
+                expand(n, 0, 0)
+                if ahead and n + 1 not in xq:
+                    quant_x(n + 1)
+                if ahead and (n + 1, 0) not in pc:
+                    latent(n + 1, 0)
+                if w == 2:
+                    quant_c(n, 1)
+                    expand(n, 0, 1)
+                if ahead == 2:
+                    latent(n + 1, 1)
+                if ahead and n + 1 not in pr:
+                    rope_key(n + 1)
+                rotate_sum(n)
+                if n + 3 <= last and n + 3 not in xw:
+                    widen(n + 3, nc.vector.tensor_copy)
+                spread(n)
+                for j in range(w):
+                    first_out(n, j)
+                store(n, 0)
+                if n + 2 <= last and n + 2 not in xg:
+                    scale_x(n + 2)
+                expand(n, 1, 0)
+                if n + 3 <= last and n + 3 not in xt:
+                    turn(n + 3)
+                if w == 2:
+                    expand(n, 1, 1)
+                if ahead:
+                    rotate(n + 1)

@@ -28,7 +28,7 @@ def tile_multiheadlatentattention_pa_t_w8_kernel(
     tc, x_bytes, x_scale, cos, sin, wd_words, wd_scales, wu_words, wu_scales, k_out, v_out
 ):
     nc = tc.nc
-    widths = [1, 1] + [2] * ((B * I - 4) // 2) + [1, 1]
+    widths = [1, 1] + [2] * ((B * I - 2) // 2)
     units = []
     for w in widths:
         first = sum(u[2] for u in units)
@@ -54,8 +54,8 @@ def tile_multiheadlatentattention_pa_t_w8_kernel(
         wu_s_raw = keep.tile([P, H * UP], U8, align_bytes=64)
         wu_s = keep.tile([P, H * UP], U8, align_bytes=64)
         xb_a = keep.tile([P, 2 * E], U8, align_bytes=64)
-        xb_b = keep.tile([P, 2 * E], U8, align_bytes=64)
-        xb_c = keep.tile([P, (I - 4) * E], U8, align_bytes=64)
+        xb_b = keep.tile([P, 4 * E], U8, align_bytes=64)
+        xb_c = keep.tile([P, (I - 6) * E], U8, align_bytes=64)
         xb_1 = keep.tile([P, I * E], U8, align_bytes=64)
         xb_2 = keep.tile([P, I * E], U8, align_bytes=64)
         xb_3 = keep.tile([P, I * E], U8, align_bytes=64)
@@ -75,11 +75,11 @@ def tile_multiheadlatentattention_pa_t_w8_kernel(
                 out=wd_s_raw[32 * q : 32 * q + 4, :].bitcast(I32),
                 in_=wd_scales[0, 4 * q : 4 * q + 4, :].bitcast(I32),
             )
-        nc.sync.dma_start(out=xb_b[:], in_=xv[0][:, 2 * E : 4 * E])
+        nc.sync.dma_start(out=xb_b[:], in_=xv[0][:, 2 * E : 6 * E])
         nc.sync.dma_start(out=wd_raw[:].bitcast(I32), in_=wd_words[0].rearrange("p n t -> p (n t)").bitcast(I32))
-        nc.sync.dma_start(out=xb_c[:], in_=xv[0][:, 4 * E :])
         nc.sync.dma_start(out=tab[:, 0, 0, :], in_=cos.rearrange("(p i) j -> p (i j)", i=I))
         nc.sync.dma_start(out=tab[:, 0, 1, :], in_=sin.rearrange("(p i) j -> p (i j)", i=I))
+        nc.sync.dma_start(out=xb_c[:], in_=xv[0][:, 6 * E :])
         for q in range(4):
             nc.sync.dma_start(
                 out=wu_s_raw[32 * q : 32 * q + 4, :].bitcast(I32), in_=wu_scales[0, 4 * q : 4 * q + 4, :].bitcast(I32)
@@ -98,12 +98,13 @@ def tile_multiheadlatentattention_pa_t_w8_kernel(
                 return [xb_1, xb_2, xb_3][b - 1][:, i * E : (i + w) * E]
             if i < 2:
                 return xb_a[:, i * E : (i + w) * E]
-            return xb_b[:] if i < 4 else xb_c[:, (i - 4) * E : (i - 4 + w) * E]
+            return xb_b[:, (i - 2) * E : (i - 2 + w) * E] if i < 6 else xb_c[:]
 
-        def widen(n, copy):
-            w = units[n][2]
-            xw[n] = work.tile([P, 2 * E], BF16, name="xw", bufs=5)
-            copy(out=xw[n][:, 0 : w * E], in_=x_source(n).bitcast(FP8))
+        def widen(n, copy, j0=0, j1=2):
+            cols = slice(j0 * E, min(j1, units[n][2]) * E)
+            if j0 == 0:
+                xw[n] = work.tile([P, 2 * E], BF16, name="xw", bufs=5)
+            copy(out=xw[n][:, cols], in_=x_source(n)[:, cols].bitcast(FP8))
 
         def turn(n):
             w = units[n][2]
@@ -188,31 +189,23 @@ def tile_multiheadlatentattention_pa_t_w8_kernel(
         def rotate_sum(n):
             w = units[n][2]
             kv[n] = outs.tile([P, 2, 2, H, DV], F32, name="kv")
-            if w == 1:
-                nc.vector.tensor_tensor(
-                    out=kv[n][:, 0, 0, :, DH:],
-                    in0=ab[n][:, 0:1, 0:RD].to_broadcast([P, H, RD]),
-                    in1=ab[n][:, 1:2, 0:RD].to_broadcast([P, H, RD]),
-                    op=ADD,
-                )
-            else:
-                nc.vector.tensor_tensor(
-                    out=kv[n][:, 0, :, 0, DH:],
-                    in0=ab[n][:, 0, :].rearrange("p (w c) -> p w c", w=w),
-                    in1=ab[n][:, 1, :].rearrange("p (w c) -> p w c", w=w),
-                    op=ADD,
-                )
+            nc.vector.tensor_tensor(
+                out=kv[n][:, 0, 0:w, 0, DH:],
+                in0=ab[n][:, 0, 0 : w * RD].rearrange("p (w c) -> p w c", w=w),
+                in1=ab[n][:, 1, 0 : w * RD].rearrange("p (w c) -> p w c", w=w),
+                op=ADD,
+            )
 
         def spread(n):
-            if units[n][2] == 2:
-                nc.gpsimd.tensor_scalar(
-                    out=kv[n][:, 0, :, 1:, DH:],
-                    in0=kv[n][:, 0, :, 0:1, DH:].to_broadcast([P, 2, H - 1, RD]),
-                    scalar1=1.0,
-                    scalar2=0.0,
-                    op0=MULT,
-                    op1=ADD,
-                )
+            w = units[n][2]
+            nc.gpsimd.tensor_scalar(
+                out=kv[n][:, 0, 0:w, 1:, DH:],
+                in0=kv[n][:, 0, 0:w, 0:1, DH:].to_broadcast([P, w, H - 1, RD]),
+                scalar1=1.0,
+                scalar2=0.0,
+                op0=MULT,
+                op1=ADD,
+            )
 
         def expand(n, s, j):
             acc = ps_u.tile([P, H * HALF], F32, name="pu")
@@ -254,8 +247,10 @@ def tile_multiheadlatentattention_pa_t_w8_kernel(
                 in_=wu_s_raw[:].bitcast(I32).rearrange("p (h s c) -> p s h c", s=2, h=H),
             )
 
-        def finish_table():
-            nc.vector.tensor_copy(out=tab[:, 1, 1, :], in_=tab[:, 0, 0, :])
+        def repeat_cos():
+            nc.scalar.copy(out=tab[:, 1, 1, :], in_=tab[:, 0, 0, :])
+
+        def negate_sin():
             nc.vector.tensor_scalar(out=tab[:, 1, 0, :], in0=tab[:, 0, 1, :], scalar1=-1.0, scalar2=None, op0=MULT)
 
         def store(n, g):
@@ -272,6 +267,7 @@ def tile_multiheadlatentattention_pa_t_w8_kernel(
         widen(2, nc.scalar.copy)
         turn(2)
         widen(3, nc.scalar.copy)
+        repeat_cos()
         order_latent_scales()
         scale_x(0)
         order_latent_words()
@@ -279,38 +275,40 @@ def tile_multiheadlatentattention_pa_t_w8_kernel(
         latent(0, 0)
         rope_key(0)
         scale_x(1)
-        finish_table()
+        order_up_scales()
+        negate_sin()
         quant_x(1)
         latent(1, 0)
-        latent_out(0, 0)
-        latent_out(1, 0)
-        widen(4, nc.scalar.copy)
-        scale_x(2)
         turn(3)
-        order_up_scales()
+        latent_out(0, 0)
+        widen(4, nc.scalar.copy, 0, 1)
+        latent_out(1, 0)
+        widen(4, nc.scalar.copy, 1, 2)
+        scale_x(2)
         quant_c(0, 0)
-        rotate(0)
-        quant_x(2)
         expand(0, 0, 0)
+        rotate(0)
         rope_key(1)
+        quant_x(2)
         latent(2, 0)
         rotate_sum(0)
+        spread(0)
         quant_c(1, 0)
         expand(1, 0, 0)
         latent(2, 1)
         rotate(1)
+        expand(0, 1, 0)
         rope_key(2)
+        turn(4)
         first_out(0, 0)
         store(0, 0)
         latent_out(2, 0)
-        expand(0, 1, 0)
-        scale_x(3)
         rotate_sum(1)
+        spread(1)
+        scale_x(3)
+        expand(1, 1, 0)
         first_out(1, 0)
         store(1, 0)
-        expand(1, 1, 0)
-        turn(4)
-        rotate(2)
         for n in range(2, last + 2):
             w = units[n][2] if n <= last else 0
             ahead = units[n + 1][2] if n < last else 0
@@ -318,17 +316,28 @@ def tile_multiheadlatentattention_pa_t_w8_kernel(
                 if (n, j) not in cg:
                     latent_out(n, j)
             for m in range(n - 1 if n > 2 else 0, n):
-                for j in range(units[m][2]):
-                    second_out(m, j, nc.vector.tensor_copy if n >= last else nc.scalar.copy)
-                store(m, 1)
+                if n < last:
+                    for j in range(units[m][2]):
+                        second_out(m, j, nc.scalar.copy)
+                    store(m, 1)
+                elif n == last:
+                    second_out(m, 0, nc.scalar.copy)
+                else:
+                    second_out(m, 0, nc.vector.tensor_copy)
+                    second_out(m, 1, nc.scalar.copy)
+                    store(m, 1)
             if w:
                 quant_c(n, 0)
                 expand(n, 0, 0)
+                if n not in ab:
+                    rotate(n)
+                    quant_c(n, 1)
+                    expand(n, 0, 1)
                 if ahead and n + 1 not in xq:
                     quant_x(n + 1)
                 if ahead and (n + 1, 0) not in pc:
                     latent(n + 1, 0)
-                if w == 2:
+                if (n, 1) not in cq:
                     quant_c(n, 1)
                     expand(n, 0, 1)
                 if ahead == 2:
@@ -336,6 +345,9 @@ def tile_multiheadlatentattention_pa_t_w8_kernel(
                 if ahead and n + 1 not in pr:
                     rope_key(n + 1)
                 rotate_sum(n)
+                if n == last:
+                    second_out(n - 1, 1, nc.vector.tensor_copy)
+                    store(n - 1, 1)
                 if n + 3 <= last and n + 3 not in xw:
                     widen(n + 3, nc.vector.tensor_copy)
                 spread(n)

@@ -62,8 +62,10 @@ def tile_multiheadlatentattention_pa_t_w8_kernel(
         xsc = keep.tile([P, 2, 2], F32)
         tab = keep.tile([P, 2, 2, I * J], BF16)
         ident = keep.tile([P, P], F32)
+        zeros = keep.tile([P, 4 * P], BF16)
 
         nc.gpsimd.memset(wd_s_raw[:].bitcast(I32), 0)
+        nc.vector.memset(zeros[:], 0.0)
         nc.vector.memset(wu_s_raw[:].bitcast(I32), 0)
         make_identity(nc, ident[:])
         xv = [x_bytes[b].rearrange("(p i) k -> p (i k)", i=I) for b in range(B)]
@@ -90,6 +92,7 @@ def tile_multiheadlatentattention_pa_t_w8_kernel(
         nc.sync.dma_start(out=xb_2[:], in_=xv[2])
         nc.sync.dma_start(out=xb_3[:], in_=xv[3])
 
+        warm = ps_c.tile([P, 4 * P], F32, name="pc")
         xw, xt, xg, xq, xs, pc, cg, cq, cs, pr, ab, kv, pu = [{} for j in range(13)]
 
         def x_source(n):
@@ -229,6 +232,10 @@ def tile_multiheadlatentattention_pa_t_w8_kernel(
         def second_out(n, j, copy):
             copy(out=kv[n][:, 1, j, :, DH:], in_=pu[n, 1, j][:].rearrange("p (h c) -> p h c", h=H))
 
+        def warm_up(count):
+            for j in range(count):
+                nc.tensor.matmul(out=warm[:], lhsT=zeros[:, 0:P], rhs=zeros[:], start=True, stop=True)
+
         def order_latent_words():
             nc.vector.tensor_copy(
                 out=wd[:].bitcast(I32).rearrange("p (t m) -> p t m", t=4),
@@ -260,10 +267,12 @@ def tile_multiheadlatentattention_pa_t_w8_kernel(
                 in_=kv[n][:, g, 0:w].rearrange("p w h d -> p w (h d)"),
             )
 
+        warm_up(3)
         widen(0, nc.vector.tensor_copy)
         turn(0)
         widen(1, nc.vector.tensor_copy)
         turn(1)
+        warm_up(2)
         widen(2, nc.scalar.copy)
         turn(2)
         widen(3, nc.scalar.copy)

@@ -12,6 +12,7 @@ FP8 = mybir.dt.float8_e4m3fn
 FP8X4 = mybir.dt.float8_e4m3fn_x4
 MULT = mybir.AluOpType.mult
 ADD = mybir.AluOpType.add
+COPY = mybir.ActivationFunctionType.Copy
 
 P = 128
 B, L, E, H, DH, RK, RD = 4, 1024, 512, 4, 64, 512, 128
@@ -28,7 +29,7 @@ def tile_multiheadlatentattention_pa_t_w8_kernel(
     tc, x_bytes, x_scale, cos, sin, wd_words, wd_scales, wu_words, wu_scales, k_out, v_out
 ):
     nc = tc.nc
-    widths = [1, 1] + [2] * ((B * I - 2) // 2)
+    widths = [2] * (B * I // 2)
     units = []
     for w in widths:
         first = sum(u[2] for u in units)
@@ -54,11 +55,9 @@ def tile_multiheadlatentattention_pa_t_w8_kernel(
         wu_s_raw = keep.tile([P, H * UP], U8, align_bytes=64)
         wu_s = keep.tile([P, H * UP], U8, align_bytes=64)
         xb_a = keep.tile([P, 2 * E], U8, align_bytes=64)
-        xb_b = keep.tile([P, 4 * E], U8, align_bytes=64)
-        xb_c = keep.tile([P, (I - 6) * E], U8, align_bytes=64)
-        xb_1 = keep.tile([P, I * E], U8, align_bytes=64)
-        xb_2 = keep.tile([P, I * E], U8, align_bytes=64)
-        xb_3 = keep.tile([P, I * E], U8, align_bytes=64)
+        xb_b = keep.tile([P, (I - 2) * E], U8, align_bytes=64)
+        xb_c = keep.tile([P, I * E], U8, align_bytes=64)
+        xb_d = keep.tile([P, (B - 2) * I * E], U8, align_bytes=64)
         xsc = keep.tile([P, 2, 2], F32)
         tab = keep.tile([P, 2, 2, I * J], BF16)
         ident = keep.tile([P, P], F32)
@@ -68,40 +67,38 @@ def tile_multiheadlatentattention_pa_t_w8_kernel(
         nc.vector.memset(zeros[:], 0.0)
         nc.vector.memset(wu_s_raw[:].bitcast(I32), 0)
         make_identity(nc, ident[:])
-        xv = [x_bytes[b].rearrange("(p i) k -> p (i k)", i=I) for b in range(B)]
+        xv = x_bytes.rearrange("b (p i) k -> p b (i k)", i=I)
         wu_v = wu_words[0].rearrange("p n t -> p (n t)").bitcast(I32).rearrange("p (h s c) -> p h s c", h=H, s=2)
-        nc.sync.dma_start(out=xb_a[:], in_=xv[0][:, 0 : 2 * E])
+        nc.sync.dma_start(out=xb_a[:], in_=xv[:, 0, 0 : 2 * E])
+        nc.sync.dma_start(out=xb_b[:], in_=xv[:, 0, 2 * E :])
         nc.sync.dma_start(out=xsc[:], in_=x_scale.rearrange("a b (p u e) -> p (a b u) e", u=2, e=2))
         for q in range(4):
             nc.sync.dma_start(
                 out=wd_s_raw[32 * q : 32 * q + 4, :].bitcast(I32),
                 in_=wd_scales[0, 4 * q : 4 * q + 4, :].bitcast(I32),
             )
-        nc.sync.dma_start(out=xb_b[:], in_=xv[0][:, 2 * E : 6 * E])
         nc.sync.dma_start(out=wd_raw[:].bitcast(I32), in_=wd_words[0].rearrange("p n t -> p (n t)").bitcast(I32))
-        nc.sync.dma_start(out=tab[:, 0, 0, :], in_=cos.rearrange("(p i) j -> p (i j)", i=I))
         nc.sync.dma_start(out=tab[:, 0, 1, :], in_=sin.rearrange("(p i) j -> p (i j)", i=I))
-        nc.sync.dma_start(out=xb_c[:], in_=xv[0][:, 6 * E :])
+        nc.sync.dma_start(out=tab[:, 0, 0, :], in_=cos.rearrange("(p i) j -> p (i j)", i=I))
+        nc.sync.dma_start(out=wu_a[:].bitcast(I32).rearrange("p (h c) -> p h c", h=H), in_=wu_v[:, :, 0, :])
         for q in range(4):
             nc.sync.dma_start(
                 out=wu_s_raw[32 * q : 32 * q + 4, :].bitcast(I32), in_=wu_scales[0, 4 * q : 4 * q + 4, :].bitcast(I32)
             )
-        nc.sync.dma_start(out=wu_a[:].bitcast(I32).rearrange("p (h c) -> p h c", h=H), in_=wu_v[:, :, 0, :])
         nc.sync.dma_start(out=wu_b[:].bitcast(I32).rearrange("p (h c) -> p h c", h=H), in_=wu_v[:, :, 1, :])
-        nc.sync.dma_start(out=xb_1[:], in_=xv[1])
-        nc.sync.dma_start(out=xb_2[:], in_=xv[2])
-        nc.sync.dma_start(out=xb_3[:], in_=xv[3])
+        nc.sync.dma_start(out=xb_c[:], in_=xv[:, 1, :])
+        nc.sync.dma_start(out=xb_d[:].rearrange("p (b c) -> p b c", b=B - 2), in_=xv[:, 2:, :])
 
         warm = ps_c.tile([P, 4 * P], F32, name="pc")
         xw, xt, xg, xq, xs, pc, cg, cq, cs, pr, ab, kv, pu = [{} for j in range(13)]
 
         def x_source(n):
             b, i, w = units[n]
-            if b > 0:
-                return [xb_1, xb_2, xb_3][b - 1][:, i * E : (i + w) * E]
-            if i < 2:
-                return xb_a[:, i * E : (i + w) * E]
-            return xb_b[:, (i - 2) * E : (i - 2 + w) * E] if i < 6 else xb_c[:]
+            if b > 1:
+                return xb_d[:, ((b - 2) * I + i) * E : ((b - 2) * I + i + w) * E]
+            if b == 1:
+                return xb_c[:, i * E : (i + w) * E]
+            return xb_a[:, i * E : (i + w) * E] if i < 2 else xb_b[:, (i - 2) * E : (i - 2 + w) * E]
 
         def widen(n, copy, j0=0, j1=2):
             cols = slice(j0 * E, min(j1, units[n][2]) * E)
@@ -109,37 +106,40 @@ def tile_multiheadlatentattention_pa_t_w8_kernel(
                 xw[n] = work.tile([P, 2 * E], BF16, name="xw", bufs=5)
             copy(out=xw[n][:, cols], in_=x_source(n)[:, cols].bitcast(FP8))
 
-        def turn(n):
-            w = units[n][2]
-            if n == 2:
-                xt[n] = ps_u.tile([P, 2, 2 * P], F32, name="pu")
-            else:
-                xt[n] = ps_x.tile([P, 2, 2 * P], F32, name="xt")
+        def turn(n, j0=0, j1=2):
             words = xw[n][:].bitcast(F32)
-            for j in range(w):
+            if n > 0:
+                xt[n] = (ps_u if n == 1 else ps_x).tile([P, 2, 2 * P], F32, name="pu" if n == 1 else "xt")
+            else:
+                xt[n, j0] = ps_x.tile([P, 2, 2 * P], F32, name="xt")
+            for j in range(j0, j1):
                 for u in range(2):
                     nc.tensor.transpose(
-                        xt[n][:, u, j * P : (j + 1) * P], words[:, j * 256 + u : (j + 1) * 256 : 2], ident[:]
+                        xt[n if n > 0 else (n, j0)][:, u, j * P : (j + 1) * P],
+                        words[:, j * 256 + u : (j + 1) * 256 : 2],
+                        ident[:],
                     )
 
-        def scale_x(n):
-            r = units[n][2] * P
-            xg[n] = work.tile([P, 2 * P, 4], BF16, name="xg", align_bytes=64)
+        def scale_x(n, j0=0, j1=2):
+            rows = slice(j0 * P, min(j1, units[n][2]) * P)
+            if j0 == 0:
+                xg[n] = work.tile([P, 2 * P, 4], BF16, name="xg", align_bytes=64)
             nc.vector.tensor_tensor(
-                out=xg[n][:, 0:r, :].rearrange("p r (u e) -> p r u e", e=2),
-                in0=xt[n][:].bitcast(BF16).rearrange("p u (r e) -> p r u e", e=2)[:, 0:r],
-                in1=xsc[:].unsqueeze(1).to_broadcast([P, r, 2, 2]),
+                out=xg[n][:, rows, :].rearrange("p r (u e) -> p r u e", e=2),
+                in0=xt[n if n > 0 else (n, j0)][:].bitcast(BF16).rearrange("p u (r e) -> p r u e", e=2)[:, rows],
+                in1=xsc[:].unsqueeze(1).to_broadcast([P, rows.stop - rows.start, 2, 2]),
                 op=MULT,
             )
 
-        def quant_x(n):
-            r = units[n][2] * P
-            xq[n] = work.tile([P, 2 * P], U32, name="xq", align_bytes=64)
-            xs[n] = work.tile([P, 2 * P], U8, name="xs", align_bytes=64)
+        def quant_x(n, j0=0, j1=2):
+            rows = slice(j0 * P, min(j1, units[n][2]) * P)
+            if j0 == 0:
+                xq[n] = work.tile([P, 2 * P], U32, name="xq", align_bytes=64)
+                xs[n] = work.tile([P, 2 * P], U8, name="xs", align_bytes=64)
             nc.vector.quantize_mx(
-                out=xq[n][:, 0:r].bitcast(FP8X4),
-                scales=xs[n][:, 0:r],
-                in_=xg[n][:, 0:r, :].rearrange("p r t -> p (r t)"),
+                out=xq[n][:, rows].bitcast(FP8X4),
+                scales=xs[n][:, rows],
+                in_=xg[n][:, rows, :].rearrange("p r t -> p (r t)"),
             )
 
         def latent(n, j):
@@ -157,7 +157,7 @@ def tile_multiheadlatentattention_pa_t_w8_kernel(
 
         def rope_key(n):
             pr[n] = ps_r.tile([P, 2 * RD], F32, name="pr")
-            for j in range(units[n][2]):
+            for j in range(2):
                 nc.tensor.matmul_mx(
                     out=pr[n][:, j * RD : (j + 1) * RD],
                     lhsT=xq[n][:, j * P : (j + 1) * P].bitcast(FP8X4),
@@ -189,9 +189,11 @@ def tile_multiheadlatentattention_pa_t_w8_kernel(
                 op=MULT,
             )
 
+        def new_rows(n):
+            kv[n] = outs.tile([P, 2, 2, H, DV], F32, name="kv")
+
         def rotate_sum(n):
             w = units[n][2]
-            kv[n] = outs.tile([P, 2, 2, H, DV], F32, name="kv")
             nc.vector.tensor_tensor(
                 out=kv[n][:, 0, 0:w, 0, DH:],
                 in0=ab[n][:, 0, 0 : w * RD].rearrange("p (w c) -> p w c", w=w),
@@ -255,120 +257,133 @@ def tile_multiheadlatentattention_pa_t_w8_kernel(
             )
 
         def repeat_cos():
-            nc.scalar.copy(out=tab[:, 1, 1, :], in_=tab[:, 0, 0, :])
+            nc.vector.tensor_copy(out=tab[:, 1, 1, :], in_=tab[:, 0, 0, :])
 
         def negate_sin():
-            nc.vector.tensor_scalar(out=tab[:, 1, 0, :], in0=tab[:, 0, 1, :], scalar1=-1.0, scalar2=None, op0=MULT)
+            nc.scalar.activation(out=tab[:, 1, 0, :], in_=tab[:, 0, 1, :], func=COPY, scale=-1.0)
 
-        def store(n, g):
+        def store(n, g, j0=0, j1=2):
             b, i, w = units[n]
             nc.sync.dma_start(
-                out=(k_out, v_out)[g][b].rearrange("(p i) h d -> p i (h d)", i=I)[:, i : i + w, :],
-                in_=kv[n][:, g, 0:w].rearrange("p w h d -> p w (h d)"),
+                out=(k_out, v_out)[g][b].rearrange("(p i) h d -> p i (h d)", i=I)[:, i + j0 : i + j1, :],
+                in_=kv[n][:, g, j0:j1].rearrange("p w h d -> p w (h d)"),
             )
 
-        warm_up(3)
-        widen(0, nc.vector.tensor_copy)
-        turn(0)
-        widen(1, nc.vector.tensor_copy)
+        warm_up(4)
+        widen(0, nc.vector.tensor_copy, 0, 1)
+        turn(0, 0, 1)
+        widen(0, nc.vector.tensor_copy, 1, 2)
+        turn(0, 1, 2)
+        warm_up(1)
+        widen(1, nc.vector.tensor_copy, 0, 1)
+        widen(1, nc.scalar.copy, 1, 2)
         turn(1)
-        warm_up(2)
+        warm_up(1)
         widen(2, nc.scalar.copy)
-        turn(2)
-        widen(3, nc.scalar.copy)
-        repeat_cos()
-        order_latent_scales()
-        scale_x(0)
-        order_latent_words()
-        quant_x(0)
-        latent(0, 0)
-        rope_key(0)
-        scale_x(1)
-        order_up_scales()
+        widen(3, nc.scalar.copy, 0, 1)
         negate_sin()
-        quant_x(1)
-        latent(1, 0)
-        turn(3)
+        order_latent_scales()
+        scale_x(0, 0, 1)
+        order_latent_words()
+        quant_x(0, 0, 1)
+        latent(0, 0)
+        scale_x(0, 1, 2)
+        turn(2)
+        scale_x(1, 0, 1)
+        quant_x(0, 1, 2)
+        latent(0, 1)
         latent_out(0, 0)
-        widen(4, nc.scalar.copy, 0, 1)
-        latent_out(1, 0)
-        widen(4, nc.scalar.copy, 1, 2)
-        scale_x(2)
+        widen(3, nc.scalar.copy, 1, 2)
+        repeat_cos()
+        quant_x(1, 0, 1)
+        latent(1, 0)
+        rope_key(0)
+        latent_out(0, 1)
+        scale_x(1, 1, 2)
         quant_c(0, 0)
+        order_up_scales()
         expand(0, 0, 0)
+        expand(0, 1, 0)
+        latent_out(1, 0)
+        quant_x(1, 1, 2)
+        latent(1, 1)
         rotate(0)
+        quant_c(0, 1)
+        expand(0, 0, 1)
         rope_key(1)
+        new_rows(0)
+        rotate_sum(0)
+        quant_c(1, 0)
+        spread(0)
+        first_out(0, 0)
+        second_out(0, 0, nc.scalar.copy)
+        store(0, 1, 0, 1)
+        expand(0, 1, 1)
+        turn(3)
+        first_out(0, 1)
+        store(0, 0)
+        expand(1, 0, 0)
+        latent_out(1, 1)
+        second_out(0, 1, nc.scalar.copy)
+        store(0, 1, 1, 2)
+        scale_x(2)
+        rotate(1)
         quant_x(2)
         latent(2, 0)
-        rotate_sum(0)
-        spread(0)
-        quant_c(1, 0)
-        expand(1, 0, 0)
+        quant_c(1, 1)
+        expand(1, 0, 1)
         latent(2, 1)
-        rotate(1)
-        expand(0, 1, 0)
         rope_key(2)
-        turn(4)
-        first_out(0, 0)
-        store(0, 0)
-        latent_out(2, 0)
+        new_rows(1)
         rotate_sum(1)
+        widen(4, nc.vector.tensor_copy)
         spread(1)
+        first_out(1, 0)
+        latent_out(2, 0)
+        first_out(1, 1)
+        store(1, 0)
         scale_x(3)
         expand(1, 1, 0)
-        first_out(1, 0)
-        store(1, 0)
-        for n in range(2, last + 2):
-            w = units[n][2] if n <= last else 0
-            ahead = units[n + 1][2] if n < last else 0
-            for j in range(w):
+        turn(4)
+        expand(1, 1, 1)
+        rotate(2)
+        for n in range(2, last + 1):
+            for j in range(2):
                 if (n, j) not in cg:
                     latent_out(n, j)
-            for m in range(n - 1 if n > 2 else 0, n):
-                if n < last:
-                    for j in range(units[m][2]):
-                        second_out(m, j, nc.scalar.copy)
-                    store(m, 1)
-                elif n == last:
-                    second_out(m, 0, nc.scalar.copy)
-                else:
-                    second_out(m, 0, nc.vector.tensor_copy)
-                    second_out(m, 1, nc.scalar.copy)
-                    store(m, 1)
-            if w:
-                quant_c(n, 0)
-                expand(n, 0, 0)
-                if n not in ab:
-                    rotate(n)
-                    quant_c(n, 1)
-                    expand(n, 0, 1)
-                if ahead and n + 1 not in xq:
-                    quant_x(n + 1)
-                if ahead and (n + 1, 0) not in pc:
-                    latent(n + 1, 0)
-                if (n, 1) not in cq:
-                    quant_c(n, 1)
-                    expand(n, 0, 1)
-                if ahead == 2:
-                    latent(n + 1, 1)
-                if ahead and n + 1 not in pr:
-                    rope_key(n + 1)
-                rotate_sum(n)
-                if n == last:
-                    second_out(n - 1, 1, nc.vector.tensor_copy)
-                    store(n - 1, 1)
-                if n + 3 <= last and n + 3 not in xw:
-                    widen(n + 3, nc.vector.tensor_copy)
-                spread(n)
-                for j in range(w):
-                    first_out(n, j)
-                store(n, 0)
-                if n + 2 <= last and n + 2 not in xg:
-                    scale_x(n + 2)
-                expand(n, 1, 0)
-                if n + 3 <= last and n + 3 not in xt:
-                    turn(n + 3)
-                if w == 2:
-                    expand(n, 1, 1)
-                if ahead:
-                    rotate(n + 1)
+            second_out(n - 1, 0, nc.scalar.copy)
+            if n < last:
+                second_out(n - 1, 1, nc.scalar.copy)
+                store(n - 1, 1)
+            quant_c(n, 0)
+            expand(n, 0, 0)
+            if n < last:
+                quant_x(n + 1)
+                latent(n + 1, 0)
+            quant_c(n, 1)
+            expand(n, 0, 1)
+            if n < last:
+                latent(n + 1, 1)
+                rope_key(n + 1)
+            new_rows(n)
+            rotate_sum(n)
+            if n == last:
+                second_out(n - 1, 1, nc.vector.tensor_copy)
+                store(n - 1, 1)
+            if n + 3 <= last:
+                widen(n + 3, nc.vector.tensor_copy)
+            spread(n)
+            first_out(n, 0)
+            first_out(n, 1)
+            store(n, 0)
+            if n + 2 <= last:
+                scale_x(n + 2)
+            expand(n, 1, 0)
+            if n + 3 <= last:
+                turn(n + 3)
+            expand(n, 1, 1)
+            if n < last:
+                rotate(n + 1)
+        second_out(last, 0, nc.vector.tensor_copy)
+        second_out(last, 1, nc.scalar.copy)
+        store(last, 1)

@@ -74,8 +74,8 @@ def tile_multiheadlatentattention_pa_t_w8_kernel(
         nc.sync.dma_start(out=xsc[:], in_=x_scale.rearrange("a b (p u e) -> p (a b u) e", u=2, e=2))
         for q in range(4):
             nc.sync.dma_start(
-                out=wd_s_raw[32 * q : 32 * q + 4, :].bitcast(I32),
-                in_=wd_scales[0, 4 * q : 4 * q + 4, :].bitcast(I32),
+                out=wd_s_raw[q:P:32, :].bitcast(I32),
+                in_=wd_scales[0, q:16:4, :].bitcast(I32),
             )
         nc.sync.dma_start(out=wd_raw[:].bitcast(I32), in_=wd_words[0].rearrange("p n t -> p (n t)").bitcast(I32))
         nc.sync.dma_start(out=tab[:, 0, 1, :], in_=sin.rearrange("(p i) j -> p (i j)", i=I))
@@ -83,7 +83,7 @@ def tile_multiheadlatentattention_pa_t_w8_kernel(
         nc.sync.dma_start(out=wu_a[:].bitcast(I32).rearrange("p (h c) -> p h c", h=H), in_=wu_v[:, :, 0, :])
         for q in range(4):
             nc.sync.dma_start(
-                out=wu_s_raw[32 * q : 32 * q + 4, :].bitcast(I32), in_=wu_scales[0, 4 * q : 4 * q + 4, :].bitcast(I32)
+                out=wu_s_raw[q:P:32, :].bitcast(I32), in_=wu_scales[0, q:16:4, :].bitcast(I32)
             )
         nc.sync.dma_start(out=wu_b[:].bitcast(I32).rearrange("p (h c) -> p h c", h=H), in_=wu_v[:, :, 1, :])
         nc.sync.dma_start(out=xb_c[:], in_=xv[:, 1, :])
@@ -272,20 +272,20 @@ def tile_multiheadlatentattention_pa_t_w8_kernel(
         warm_up(4)
         widen(0, nc.vector.tensor_copy, 0, 1)
         turn(0, 0, 1)
-        widen(0, nc.vector.tensor_copy, 1, 2)
+        widen(0, nc.scalar.copy, 1, 2)
         turn(0, 1, 2)
         warm_up(1)
-        widen(1, nc.vector.tensor_copy, 0, 1)
+        widen(1, nc.scalar.copy, 0, 1)
         widen(1, nc.scalar.copy, 1, 2)
         turn(1)
         warm_up(1)
         widen(2, nc.scalar.copy)
         widen(3, nc.scalar.copy, 0, 1)
         negate_sin()
-        order_latent_scales()
         scale_x(0, 0, 1)
-        order_latent_words()
+        order_latent_scales()
         quant_x(0, 0, 1)
+        order_latent_words()
         latent(0, 0)
         scale_x(0, 1, 2)
         turn(2)

@@ -240,14 +240,14 @@ def tile_multiheadlatentattention_pa_t_w8_kernel(
 
         def order_latent_words():
             nc.vector.tensor_copy(
-                out=wd[:].bitcast(I32).rearrange("p (t m) -> p t m", t=4),
-                in_=wd_raw[:, 0:RK].bitcast(I32).rearrange("p (m t) -> p t m", t=4),
+                out=wd[:].bitcast(I32).rearrange("p (t m i) -> p m t i", t=4, i=4),
+                in_=wd_raw[:, 0:RK].bitcast(I32).rearrange("p (m i t) -> p m t i", t=4, i=4),
             )
 
         def order_latent_scales():
             nc.vector.tensor_copy(
-                out=wd_s[:].rearrange("p (t m) -> p t m", t=4),
-                in_=wd_s_raw[:, 0:RK].rearrange("p (m t) -> p t m", t=4),
+                out=wd_s[:].rearrange("p (t m i) -> p m t i", t=4, i=16),
+                in_=wd_s_raw[:, 0:RK].rearrange("p (m i t) -> p m t i", t=4, i=16),
             )
 
         def order_up_scales():

@@ -39,7 +39,7 @@ def tile_multiheadlatentattention_pa_t_w8_kernel(
     with ExitStack() as ctx:
         keep = ctx.enter_context(tc.tile_pool(name="keep", bufs=1))
         work = ctx.enter_context(tc.tile_pool(name="work", bufs=3))
-        outs = ctx.enter_context(tc.tile_pool(name="outs", bufs=6))
+        outs = ctx.enter_context(tc.tile_pool(name="outs", bufs=3))
         ps_x = ctx.enter_context(tc.psum_pool(name="ps_x", bufs=2))
         ps_c = ctx.enter_context(tc.psum_pool(name="ps_c", bufs=2))
         ps_r = ctx.enter_context(tc.psum_pool(name="ps_r", bufs=1))
@@ -70,8 +70,8 @@ def tile_multiheadlatentattention_pa_t_w8_kernel(
         xv = x_bytes.rearrange("b (p i) k -> p b (i k)", i=I)
         wu_v = wu_words[0].rearrange("p n t -> p (n t)").bitcast(I32).rearrange("p (h s c) -> p h s c", h=H, s=2)
         nc.sync.dma_start(out=xb_a[:], in_=xv[:, 0, 0 : 2 * E])
-        nc.sync.dma_start(out=xb_b[:], in_=xv[:, 0, 2 * E :])
         nc.sync.dma_start(out=xsc[:], in_=x_scale.rearrange("a b (p u e) -> p (a b u) e", u=2, e=2))
+        nc.sync.dma_start(out=xb_b[:], in_=xv[:, 0, 2 * E :])
         for q in range(4):
             nc.sync.dma_start(
                 out=wd_s_raw[q:P:32, :].bitcast(I32),
@@ -80,17 +80,17 @@ def tile_multiheadlatentattention_pa_t_w8_kernel(
         nc.sync.dma_start(out=wd_raw[:].bitcast(I32), in_=wd_words[0].rearrange("p n t -> p (n t)").bitcast(I32))
         nc.sync.dma_start(out=tab[:, 0, 1, :], in_=sin.rearrange("(p i) j -> p (i j)", i=I))
         nc.sync.dma_start(out=tab[:, 0, 0, :], in_=cos.rearrange("(p i) j -> p (i j)", i=I))
-        nc.sync.dma_start(out=wu_a[:].bitcast(I32).rearrange("p (h c) -> p h c", h=H), in_=wu_v[:, :, 0, :])
         for q in range(4):
             nc.sync.dma_start(
                 out=wu_s_raw[q:P:32, :].bitcast(I32), in_=wu_scales[0, q:16:4, :].bitcast(I32)
             )
+        nc.sync.dma_start(out=wu_a[:].bitcast(I32).rearrange("p (h c) -> p h c", h=H), in_=wu_v[:, :, 0, :])
         nc.sync.dma_start(out=wu_b[:].bitcast(I32).rearrange("p (h c) -> p h c", h=H), in_=wu_v[:, :, 1, :])
         nc.sync.dma_start(out=xb_c[:], in_=xv[:, 1, :])
         nc.sync.dma_start(out=xb_d[:].rearrange("p (b c) -> p b c", b=B - 2), in_=xv[:, 2:, :])
 
         warm = ps_c.tile([P, 4 * P], F32, name="pc")
-        xw, xt, xg, xq, xs, pc, cg, cq, cs, pr, ab, kv, pu = [{} for j in range(13)]
+        xw, xt, xg, xq, xs, pc, cg, cq, cs, pr, ab, kv, pu, rows = [{} for j in range(14)]
 
         def x_source(n):
             b, i, w = units[n]
@@ -190,7 +190,10 @@ def tile_multiheadlatentattention_pa_t_w8_kernel(
             )
 
         def new_rows(n):
-            kv[n] = outs.tile([P, 2, 2, H, DV], F32, name="kv")
+            b, i, w = units[n]
+            if i == 0:
+                rows[b] = outs.tile([P, 2, I, H, DV], F32, name="rows")
+            kv[n] = rows[b][:, :, i : i + w]
 
         def rotate_sum(n):
             w = units[n][2]
@@ -234,6 +237,11 @@ def tile_multiheadlatentattention_pa_t_w8_kernel(
         def second_out(n, j, copy):
             copy(out=kv[n][:, 1, j, :, DH:], in_=pu[n, 1, j][:].rearrange("p (h c) -> p h c", h=H))
 
+        def leave(n, g):
+            pairs = 2 if g == 1 and n >= last - 3 else 1
+            if n % pairs == pairs - 1:
+                store(n, g, 2 - 2 * pairs, 2)
+
         def warm_up(count):
             for j in range(count):
                 nc.tensor.matmul(out=warm[:], lhsT=zeros[:, 0:P], rhs=zeros[:], start=True, stop=True)
@@ -266,7 +274,7 @@ def tile_multiheadlatentattention_pa_t_w8_kernel(
             b, i, w = units[n]
             nc.sync.dma_start(
                 out=(k_out, v_out)[g][b].rearrange("(p i) h d -> p i (h d)", i=I)[:, i + j0 : i + j1, :],
-                in_=kv[n][:, g, j0:j1].rearrange("p w h d -> p w (h d)"),
+                in_=rows[b][:, g, i + j0 : i + j1].rearrange("p w h d -> p w (h d)"),
             )
 
         warm_up(4)
@@ -354,7 +362,7 @@ def tile_multiheadlatentattention_pa_t_w8_kernel(
             second_out(n - 1, 0, nc.scalar.copy)
             if n < last:
                 second_out(n - 1, 1, nc.scalar.copy)
-                store(n - 1, 1)
+                leave(n - 1, 1)
             quant_c(n, 0)
             expand(n, 0, 0)
             if n < last:
@@ -369,13 +377,13 @@ def tile_multiheadlatentattention_pa_t_w8_kernel(
             rotate_sum(n)
             if n == last:
                 second_out(n - 1, 1, nc.vector.tensor_copy)
-                store(n - 1, 1)
+                leave(n - 1, 1)
             if n + 3 <= last:
                 widen(n + 3, nc.vector.tensor_copy)
             spread(n)
             first_out(n, 0)
             first_out(n, 1)
-            store(n, 0)
+            leave(n, 0)
             if n + 2 <= last:
                 scale_x(n + 2)
             expand(n, 1, 0)
@@ -386,4 +394,4 @@ def tile_multiheadlatentattention_pa_t_w8_kernel(
                 rotate(n + 1)
         second_out(last, 0, nc.vector.tensor_copy)
         second_out(last, 1, nc.scalar.copy)
-        store(last, 1)
+        leave(last, 1)

@@ -20,7 +20,10 @@ I = L // P
 J = RD // 2
 DV = DH + RD
 UP = DH + DV
-HALF = UP // 2
+KW = H * DH
+VW = H * DV
+BANK = 512
+PAIRS = B * I // 2
 
 FLOPS = 2 * B * L * E * (RK + RD + H * UP)
 
@@ -29,12 +32,7 @@ def tile_multiheadlatentattention_pa_t_w8_kernel(
     tc, x_bytes, x_scale, cos, sin, wd_words, wd_scales, wu_words, wu_scales, k_out, v_out
 ):
     nc = tc.nc
-    widths = [2] * (B * I // 2)
-    units = []
-    for w in widths:
-        first = sum(u[2] for u in units)
-        units.append((first // I, first % I, w))
-    last = len(units) - 1
+    last = PAIRS - 1
 
     with ExitStack() as ctx:
         keep = ctx.enter_context(tc.tile_pool(name="keep", bufs=1))
@@ -46,93 +44,88 @@ def tile_multiheadlatentattention_pa_t_w8_kernel(
         ps_u = ctx.enter_context(tc.psum_pool(name="ps_u", bufs=3))
         ctx.enter_context(tc.manual_schedule())
 
-        wd_raw = keep.tile([P, RK + RD], U32, align_bytes=64)
-        wd_s_raw = keep.tile([P, RK + RD], U8, align_bytes=64)
-        wd = keep.tile([P, RK], U32, align_bytes=64)
-        wd_s = keep.tile([P, RK], U8, align_bytes=64)
-        wu_a = keep.tile([P, H * HALF], U32, align_bytes=64)
-        wu_b = keep.tile([P, H * HALF], U32, align_bytes=64)
-        wu_s_raw = keep.tile([P, H * UP], U8, align_bytes=64)
-        wu_s = keep.tile([P, H * UP], U8, align_bytes=64)
-        xb_a = keep.tile([P, 2 * E], U8, align_bytes=64)
-        xb_b = keep.tile([P, (I - 2) * E], U8, align_bytes=64)
-        xb_c = keep.tile([P, I * E], U8, align_bytes=64)
-        xb_d = keep.tile([P, (B - 2) * I * E], U8, align_bytes=64)
-        xsc = keep.tile([P, 2, 2], F32)
-        tab = keep.tile([P, 2, 2, I * J], BF16)
-        ident = keep.tile([P, P], F32)
-        zeros = keep.tile([P, 4 * P], BF16)
+        wd_raw = keep.tile([P, RK + RD], U32, name="wd_raw", align_bytes=64)
+        wd_s_raw = keep.tile([P, RK + RD], U8, name="wd_s_raw", align_bytes=64)
+        wd = keep.tile([P, RK], U32, name="wd", align_bytes=64)
+        wd_s = keep.tile([P, RK], U8, name="wd_s", align_bytes=64)
+        wk = keep.tile([P, KW], U32, name="wk", align_bytes=64)
+        wv = keep.tile([P, VW], U32, name="wv", align_bytes=64)
+        wu_s_raw = keep.tile([P, H * UP], U8, name="wu_s_raw", align_bytes=64)
+        wk_s = keep.tile([P, KW], U8, name="wk_s", align_bytes=64)
+        wv_s = keep.tile([P, VW], U8, name="wv_s", align_bytes=64)
+        xb_a = keep.tile([P, 2 * E], U8, name="xb_a", align_bytes=64)
+        xb_b = keep.tile([P, (I - 2) * E], U8, name="xb_b", align_bytes=64)
+        xb_c = keep.tile([P, I * E], U8, name="xb_c", align_bytes=64)
+        xb_d = keep.tile([P, (B - 2) * I * E], U8, name="xb_d", align_bytes=64)
+        xsc = keep.tile([P, 2, 2], F32, name="xsc")
+        tab = keep.tile([P, 2, 2, I * J], BF16, name="tab")
+        ident = keep.tile([P, P], F32, name="ident")
+        zeros = keep.tile([P, BANK], BF16, name="zeros")
 
         nc.gpsimd.memset(wd_s_raw[:].bitcast(I32), 0)
         nc.vector.memset(zeros[:], 0.0)
         nc.vector.memset(wu_s_raw[:].bitcast(I32), 0)
         make_identity(nc, ident[:])
         xv = x_bytes.rearrange("b (p i) k -> p b (i k)", i=I)
-        wu_v = wu_words[0].rearrange("p n t -> p (n t)").bitcast(I32).rearrange("p (h s c) -> p h s c", h=H, s=2)
+        wu_heads = wu_words[0].rearrange("p n t -> p (n t)").bitcast(I32).rearrange("p (h c) -> p h c", h=H)
         nc.sync.dma_start(out=xb_a[:], in_=xv[:, 0, 0 : 2 * E])
-        nc.sync.dma_start(out=xsc[:], in_=x_scale.rearrange("a b (p u e) -> p (a b u) e", u=2, e=2))
-        nc.sync.dma_start(out=xb_b[:], in_=xv[:, 0, 2 * E :])
-        for q in range(4):
-            nc.sync.dma_start(
-                out=wd_s_raw[q:P:32, :].bitcast(I32),
-                in_=wd_scales[0, q:16:4, :].bitcast(I32),
-            )
         nc.sync.dma_start(out=wd_raw[:].bitcast(I32), in_=wd_words[0].rearrange("p n t -> p (n t)").bitcast(I32))
+        nc.sync.dma_start(out=xsc[:], in_=x_scale.rearrange("a b (p u e) -> p (a b u) e", u=2, e=2))
+        for q in range(4):
+            nc.sync.dma_start(out=wd_s_raw[q:P:32, :].bitcast(I32), in_=wd_scales[0, q:16:4, :].bitcast(I32))
+        nc.sync.dma_start(out=xb_b[:], in_=xv[:, 0, 2 * E :])
         nc.sync.dma_start(out=tab[:, 0, 1, :], in_=sin.rearrange("(p i) j -> p (i j)", i=I))
         nc.sync.dma_start(out=tab[:, 0, 0, :], in_=cos.rearrange("(p i) j -> p (i j)", i=I))
         for q in range(4):
-            nc.sync.dma_start(
-                out=wu_s_raw[q:P:32, :].bitcast(I32), in_=wu_scales[0, q:16:4, :].bitcast(I32)
-            )
-        nc.sync.dma_start(out=wu_a[:].bitcast(I32).rearrange("p (h c) -> p h c", h=H), in_=wu_v[:, :, 0, :])
-        nc.sync.dma_start(out=wu_b[:].bitcast(I32).rearrange("p (h c) -> p h c", h=H), in_=wu_v[:, :, 1, :])
+            nc.sync.dma_start(out=wu_s_raw[q:P:32, :].bitcast(I32), in_=wu_scales[0, q:16:4, :].bitcast(I32))
+        nc.sync.dma_start(out=wv[:].bitcast(I32).rearrange("p (h c) -> p h c", h=H), in_=wu_heads[:, :, DH:])
+        nc.sync.dma_start(out=wk[:].bitcast(I32).rearrange("p (h c) -> p h c", h=H), in_=wu_heads[:, :, 0:DH])
         nc.sync.dma_start(out=xb_c[:], in_=xv[:, 1, :])
         nc.sync.dma_start(out=xb_d[:].rearrange("p (b c) -> p b c", b=B - 2), in_=xv[:, 2:, :])
 
-        warm = ps_c.tile([P, 4 * P], F32, name="pc")
-        xw, xt, xg, xq, xs, pc, cg, cq, cs, pr, ab, kv, pu, rows = [{} for j in range(14)]
+        warm = ps_c.tile([P, BANK], F32, name="pc")
+        xw, xt, xg, xq, xs, pc, cg, cq, cs, pr, ab, pk, pv, k_rows, v_rows = [{} for j in range(15)]
+
+        def place(n):
+            return divmod(2 * n, I)
 
         def x_source(n):
-            b, i, w = units[n]
+            b, i = place(n)
             if b > 1:
-                return xb_d[:, ((b - 2) * I + i) * E : ((b - 2) * I + i + w) * E]
+                return xb_d[:, ((b - 2) * I + i) * E : ((b - 2) * I + i + 2) * E]
             if b == 1:
-                return xb_c[:, i * E : (i + w) * E]
-            return xb_a[:, i * E : (i + w) * E] if i < 2 else xb_b[:, (i - 2) * E : (i - 2 + w) * E]
+                return xb_c[:, i * E : (i + 2) * E]
+            return xb_a[:] if i == 0 else xb_b[:, (i - 2) * E : i * E]
 
         def widen(n, copy, j0=0, j1=2):
-            cols = slice(j0 * E, min(j1, units[n][2]) * E)
-            if j0 == 0:
+            cols = slice(j0 * E, j1 * E)
+            if n not in xw:
                 xw[n] = work.tile([P, 2 * E], BF16, name="xw", bufs=5)
             copy(out=xw[n][:, cols], in_=x_source(n)[:, cols].bitcast(FP8))
 
         def turn(n, j0=0, j1=2):
             words = xw[n][:].bitcast(F32)
-            if n > 0:
-                xt[n] = (ps_u if n == 1 else ps_x).tile([P, 2, 2 * P], F32, name="pu" if n == 1 else "xt")
-            else:
-                xt[n, j0] = ps_x.tile([P, 2, 2 * P], F32, name="xt")
+            bank = ps_x.tile([P, 2, 2 * P], F32, name="xt")
             for j in range(j0, j1):
+                xt[n, j] = bank
                 for u in range(2):
                     nc.tensor.transpose(
-                        xt[n if n > 0 else (n, j0)][:, u, j * P : (j + 1) * P],
-                        words[:, j * 256 + u : (j + 1) * 256 : 2],
-                        ident[:],
+                        bank[:, u, j * P : (j + 1) * P], words[:, j * 256 + u : (j + 1) * 256 : 2], ident[:]
                     )
 
         def scale_x(n, j0=0, j1=2):
-            rows = slice(j0 * P, min(j1, units[n][2]) * P)
+            rows = slice(j0 * P, j1 * P)
             if j0 == 0:
                 xg[n] = work.tile([P, 2 * P, 4], BF16, name="xg", align_bytes=64)
             nc.vector.tensor_tensor(
                 out=xg[n][:, rows, :].rearrange("p r (u e) -> p r u e", e=2),
-                in0=xt[n if n > 0 else (n, j0)][:].bitcast(BF16).rearrange("p u (r e) -> p r u e", e=2)[:, rows],
+                in0=xt[n, j0][:].bitcast(BF16).rearrange("p u (r e) -> p r u e", e=2)[:, rows],
                 in1=xsc[:].unsqueeze(1).to_broadcast([P, rows.stop - rows.start, 2, 2]),
                 op=MULT,
             )
 
         def quant_x(n, j0=0, j1=2):
-            rows = slice(j0 * P, min(j1, units[n][2]) * P)
+            rows = slice(j0 * P, j1 * P)
             if j0 == 0:
                 xq[n] = work.tile([P, 2 * P], U32, name="xq", align_bytes=64)
                 xs[n] = work.tile([P, 2 * P], U8, name="xs", align_bytes=64)
@@ -142,31 +135,29 @@ def tile_multiheadlatentattention_pa_t_w8_kernel(
                 in_=xg[n][:, rows, :].rearrange("p r t -> p (r t)"),
             )
 
+        def product(out, lhs, lhs_s, rhs, rhs_s):
+            nc.tensor.matmul_mx(
+                out=out,
+                lhsT=lhs.bitcast(FP8X4),
+                lhsT_scale=lhs_s,
+                rhs=rhs.bitcast(FP8X4),
+                rhs_scale=rhs_s,
+                start=True,
+                stop=True,
+            )
+
         def latent(n, j):
+            rows = slice(j * P, (j + 1) * P)
             pc[n, j] = ps_c.tile([P, 4, P], F32, name="pc")
             for t in range(4):
-                nc.tensor.matmul_mx(
-                    out=pc[n, j][:, t, :],
-                    lhsT=wd[:, t * P : (t + 1) * P].bitcast(FP8X4),
-                    lhsT_scale=wd_s[:, t * P : (t + 1) * P],
-                    rhs=xq[n][:, j * P : (j + 1) * P].bitcast(FP8X4),
-                    rhs_scale=xs[n][:, j * P : (j + 1) * P],
-                    start=True,
-                    stop=True,
-                )
+                cols = slice(t * P, (t + 1) * P)
+                product(pc[n, j][:, t, :], wd[:, cols], wd_s[:, cols], xq[n][:, rows], xs[n][:, rows])
 
         def rope_key(n):
             pr[n] = ps_r.tile([P, 2 * RD], F32, name="pr")
             for j in range(2):
-                nc.tensor.matmul_mx(
-                    out=pr[n][:, j * RD : (j + 1) * RD],
-                    lhsT=xq[n][:, j * P : (j + 1) * P].bitcast(FP8X4),
-                    lhsT_scale=xs[n][:, j * P : (j + 1) * P],
-                    rhs=wd_raw[:, RK:].bitcast(FP8X4),
-                    rhs_scale=wd_s_raw[:, RK:],
-                    start=True,
-                    stop=True,
-                )
+                rows = slice(j * P, (j + 1) * P)
+                product(pr[n][:, j * RD : (j + 1) * RD], xq[n][:, rows], xs[n][:, rows], wd_raw[:, RK:], wd_s_raw[:, RK:])
 
         def latent_out(n, j):
             cg[n, j] = work.tile([P, P, 4], BF16, name="cg", align_bytes=64, bufs=4)
@@ -180,67 +171,79 @@ def tile_multiheadlatentattention_pa_t_w8_kernel(
             )
 
         def rotate(n):
-            b, i, w = units[n]
+            i = place(n)[1]
             ab[n] = work.tile([P, 2, 2 * RD], F32, name="ab")
             nc.vector.tensor_tensor(
-                out=ab[n][:, :, 0 : w * RD].rearrange("p a (q e) -> p a q e", e=2),
-                in0=pr[n][:, 0 : w * RD].rearrange("p (q a) -> p a q", a=2).unsqueeze(3).to_broadcast([P, 2, w * J, 2]),
-                in1=tab[:, :, :, i * J : (i + w) * J].rearrange("p a e q -> p a q e"),
+                out=ab[n][:].rearrange("p a (q e) -> p a q e", e=2),
+                in0=pr[n][:].rearrange("p (q a) -> p a q", a=2).unsqueeze(3).to_broadcast([P, 2, 2 * J, 2]),
+                in1=tab[:, :, :, i * J : (i + 2) * J].rearrange("p a e q -> p a q e"),
                 op=MULT,
             )
 
-        def new_rows(n):
-            b, i, w = units[n]
-            if i == 0:
-                rows[b] = outs.tile([P, 2, I, H, DV], F32, name="rows")
-            kv[n] = rows[b][:, :, i : i + w]
+        def k_pair(n):
+            b, i = place(n)
+            if b not in k_rows:
+                k_rows[b] = outs.tile([P, I, H, DV], F32, name="k_rows")
+            return k_rows[b][:, i : i + 2]
 
         def rotate_sum(n):
-            w = units[n][2]
             nc.vector.tensor_tensor(
-                out=kv[n][:, 0, 0:w, 0, DH:],
-                in0=ab[n][:, 0, 0 : w * RD].rearrange("p (w c) -> p w c", w=w),
-                in1=ab[n][:, 1, 0 : w * RD].rearrange("p (w c) -> p w c", w=w),
+                out=k_pair(n)[:, :, 0, DH:],
+                in0=ab[n][:, 0, :].rearrange("p (w c) -> p w c", w=2),
+                in1=ab[n][:, 1, :].rearrange("p (w c) -> p w c", w=2),
                 op=ADD,
             )
 
         def spread(n):
-            w = units[n][2]
             nc.gpsimd.tensor_scalar(
-                out=kv[n][:, 0, 0:w, 1:, DH:],
-                in0=kv[n][:, 0, 0:w, 0:1, DH:].to_broadcast([P, w, H - 1, RD]),
+                out=k_pair(n)[:, :, 1:, DH:],
+                in0=k_pair(n)[:, :, 0:1, DH:].to_broadcast([P, 2, H - 1, RD]),
                 scalar1=1.0,
                 scalar2=0.0,
                 op0=MULT,
                 op1=ADD,
             )
 
-        def expand(n, s, j):
-            acc = ps_u.tile([P, H * HALF], F32, name="pu")
-            pu[n, s, j] = acc
-            nc.tensor.matmul_mx(
-                out=acc[:],
-                lhsT=cq[n, j][:].bitcast(FP8X4),
-                lhsT_scale=cs[n, j][:],
-                rhs=(wu_a, wu_b)[s][:].bitcast(FP8X4),
-                rhs_scale=wu_s[:, s * H * HALF : (s + 1) * H * HALF],
-                start=True,
-                stop=True,
+        def expand_k(n):
+            pk[n] = ps_u.tile([P, BANK], F32, name="pu")
+            for j in range(2):
+                product(pk[n][:, j * KW : (j + 1) * KW], cq[n, j][:], cs[n, j][:], wk[:], wk_s[:])
+
+        def expand_v(n, s):
+            pv[n, s] = ps_u.tile([P, BANK], F32, name="pu")
+            for j in range(2):
+                lo, hi = max(s * BANK, j * VW), min((s + 1) * BANK, (j + 1) * VW)
+                if lo < hi:
+                    cols = slice(lo - j * VW, hi - j * VW)
+                    product(
+                        pv[n, s][:, lo - s * BANK : hi - s * BANK], cq[n, j][:], cs[n, j][:], wv[:, cols], wv_s[:, cols]
+                    )
+
+        def k_out_copy(n):
+            nc.scalar.copy(out=k_pair(n)[:, :, :, 0:DH], in_=pk[n][:].rearrange("p (w h c) -> p w h c", w=2, h=H))
+
+        def v_out_copy(n, s, copy):
+            b, i = place(n)
+            if b not in v_rows:
+                v_rows[b] = outs.tile([P, I * VW], F32, name="v_rows")
+            copy(out=v_rows[b][:, i * VW + s * BANK : i * VW + (s + 1) * BANK], in_=pv[n, s][:])
+
+        def store_k(n, pairs=1):
+            b, i = place(n)
+            tiles = slice(i + 2 - 2 * pairs, i + 2)
+            nc.sync.dma_start(
+                out=k_out[b].rearrange("(p i) h d -> p i (h d)", i=I)[:, tiles, :],
+                in_=k_rows[b][:, tiles].rearrange("p w h d -> p w (h d)"),
             )
 
-        def first_out(n, j):
-            nc.scalar.copy(
-                out=kv[n][:, :, j, :, 0:DH].rearrange("p g h c -> p h g c"),
-                in_=pu[n, 0, j][:].rearrange("p (h g c) -> p h g c", h=H, g=2),
-            )
+        def store_v(n, pairs=1):
+            b, i = place(n)
+            cols = slice((i + 2 - 2 * pairs) * VW, (i + 2) * VW)
+            nc.sync.dma_start(out=v_out[b].rearrange("(p i) h d -> p (i h d)", i=I)[:, cols], in_=v_rows[b][:, cols])
 
-        def second_out(n, j, copy):
-            copy(out=kv[n][:, 1, j, :, DH:], in_=pu[n, 1, j][:].rearrange("p (h c) -> p h c", h=H))
-
-        def leave(n, g):
-            pairs = 2 if g == 1 and n >= last - 3 else 1
-            if n % pairs == pairs - 1:
-                store(n, g, 2 - 2 * pairs, 2)
+        def leave(n, store, waits):
+            if n not in waits:
+                store(n, 2 if n - 1 in waits else 1)
 
         def warm_up(count):
             for j in range(count):
@@ -258,140 +261,106 @@ def tile_multiheadlatentattention_pa_t_w8_kernel(
                 in_=wd_s_raw[:, 0:RK].rearrange("p (m i t) -> p m t i", t=4, i=16),
             )
 
-        def order_up_scales():
+        def order_up_scales(part, lo, hi):
             nc.vector.tensor_copy(
-                out=wu_s[:].bitcast(I32).rearrange("p (s h c) -> p s h c", s=2, h=H),
-                in_=wu_s_raw[:].bitcast(I32).rearrange("p (h s c) -> p s h c", s=2, h=H),
+                out=part[:].bitcast(I32).rearrange("p (h c) -> p h c", h=H),
+                in_=wu_s_raw[:].bitcast(I32).rearrange("p (h c) -> p h c", h=H)[:, :, lo // 4 : hi // 4],
             )
 
         def repeat_cos():
             nc.vector.tensor_copy(out=tab[:, 1, 1, :], in_=tab[:, 0, 0, :])
 
         def negate_sin():
-            nc.scalar.activation(out=tab[:, 1, 0, :], in_=tab[:, 0, 1, :], func=COPY, scale=-1.0)
+            nc.vector.tensor_scalar(out=tab[:, 1, 0, :], in0=tab[:, 0, 1, :], scalar1=-1.0, scalar2=None, op0=MULT)
 
-        def store(n, g, j0=0, j1=2):
-            b, i, w = units[n]
-            nc.sync.dma_start(
-                out=(k_out, v_out)[g][b].rearrange("(p i) h d -> p i (h d)", i=I)[:, i + j0 : i + j1, :],
-                in_=rows[b][:, g, i + j0 : i + j1].rearrange("p w h d -> p w (h d)"),
-            )
 
-        warm_up(4)
+        warm_up(3)
         widen(0, nc.vector.tensor_copy, 0, 1)
         turn(0, 0, 1)
         widen(0, nc.scalar.copy, 1, 2)
         turn(0, 1, 2)
-        warm_up(1)
-        widen(1, nc.scalar.copy, 0, 1)
-        widen(1, nc.scalar.copy, 1, 2)
-        turn(1)
-        warm_up(1)
-        widen(2, nc.scalar.copy)
-        widen(3, nc.scalar.copy, 0, 1)
-        negate_sin()
+        warm_up(2)
+        order_latent_words()
         scale_x(0, 0, 1)
         order_latent_scales()
         quant_x(0, 0, 1)
-        order_latent_words()
-        latent(0, 0)
         scale_x(0, 1, 2)
-        turn(2)
-        scale_x(1, 0, 1)
+        widen(1, nc.scalar.copy)
+        latent(0, 0)
+        turn(1)
+        warm_up(1)
+        widen(2, nc.scalar.copy)
+        negate_sin()
         quant_x(0, 1, 2)
-        latent(0, 1)
         latent_out(0, 0)
-        widen(3, nc.scalar.copy, 1, 2)
-        repeat_cos()
-        quant_x(1, 0, 1)
-        latent(1, 0)
+        latent(0, 1)
         rope_key(0)
-        latent_out(0, 1)
-        scale_x(1, 1, 2)
+        repeat_cos()
+        order_up_scales(wk_s, 0, DH)
+        order_up_scales(wv_s, DH, UP)
+        scale_x(1, 0, 1)
         quant_c(0, 0)
-        order_up_scales()
-        expand(0, 0, 0)
-        expand(0, 1, 0)
-        latent_out(1, 0)
-        quant_x(1, 1, 2)
-        latent(1, 1)
+        expand_v(0, 0)
+        turn(2)
+        scale_x(1, 1, 2)
+        latent_out(0, 1)
+        widen(3, nc.scalar.copy)
+        quant_x(1, 0, 1)
         rotate(0)
         quant_c(0, 1)
-        expand(0, 0, 1)
-        rope_key(1)
-        new_rows(0)
+        quant_x(1, 1, 2)
+        latent(1, 0)
+        expand_k(0)
+        latent(1, 1)
         rotate_sum(0)
-        quant_c(1, 0)
         spread(0)
-        first_out(0, 0)
-        second_out(0, 0, nc.scalar.copy)
-        store(0, 1, 0, 1)
-        expand(0, 1, 1)
+        widen(4, nc.gpsimd.tensor_copy, 0, 1)
+        v_out_copy(0, 0, nc.scalar.copy)
+        latent_out(1, 0)
+        k_out_copy(0)
+        store_k(0)
+        rope_key(1)
+        expand_v(0, 2)
+        expand_v(0, 1)
         turn(3)
-        first_out(0, 1)
-        store(0, 0)
-        expand(1, 0, 0)
-        latent_out(1, 1)
-        second_out(0, 1, nc.scalar.copy)
-        store(0, 1, 1, 2)
         scale_x(2)
         rotate(1)
-        quant_x(2)
-        latent(2, 0)
-        quant_c(1, 1)
-        expand(1, 0, 1)
-        latent(2, 1)
-        rope_key(2)
-        new_rows(1)
-        rotate_sum(1)
-        widen(4, nc.vector.tensor_copy)
-        spread(1)
-        first_out(1, 0)
-        latent_out(2, 0)
-        first_out(1, 1)
-        store(1, 0)
-        scale_x(3)
-        expand(1, 1, 0)
-        turn(4)
-        expand(1, 1, 1)
-        rotate(2)
-        for n in range(2, last + 1):
+        latent_out(1, 1)
+        v_out_copy(0, 2, nc.scalar.copy)
+
+        for n in range(1, last + 1):
             for j in range(2):
                 if (n, j) not in cg:
                     latent_out(n, j)
-            second_out(n - 1, 0, nc.scalar.copy)
-            if n < last:
-                second_out(n - 1, 1, nc.scalar.copy)
-                leave(n - 1, 1)
+            v_out_copy(n - 1, 1, nc.scalar.copy)
+            leave(n - 1, store_v, (12, 14))
+            if n + 3 <= last:
+                widen(n + 3, nc.scalar.copy, 1, 2)
             quant_c(n, 0)
-            expand(n, 0, 0)
+            expand_v(n, 0)
             if n < last:
                 quant_x(n + 1)
                 latent(n + 1, 0)
             quant_c(n, 1)
-            expand(n, 0, 1)
+            expand_k(n)
             if n < last:
-                latent(n + 1, 1)
                 rope_key(n + 1)
-            new_rows(n)
+                latent(n + 1, 1)
             rotate_sum(n)
-            if n == last:
-                second_out(n - 1, 1, nc.vector.tensor_copy)
-                leave(n - 1, 1)
-            if n + 3 <= last:
-                widen(n + 3, nc.vector.tensor_copy)
             spread(n)
-            first_out(n, 0)
-            first_out(n, 1)
-            leave(n, 0)
+            if n + 4 <= last:
+                widen(n + 4, nc.gpsimd.tensor_copy, 0, 1)
+            v_out_copy(n, 0, nc.scalar.copy)
+            k_out_copy(n)
+            leave(n, store_k, (8, 10, 12, 14))
             if n + 2 <= last:
                 scale_x(n + 2)
-            expand(n, 1, 0)
+            expand_v(n, 2)
+            expand_v(n, 1)
             if n + 3 <= last:
                 turn(n + 3)
-            expand(n, 1, 1)
             if n < last:
                 rotate(n + 1)
-        second_out(last, 0, nc.vector.tensor_copy)
-        second_out(last, 1, nc.scalar.copy)
-        leave(last, 1)
+            v_out_copy(n, 2, nc.vector.tensor_copy)
+        v_out_copy(last, 1, nc.scalar.copy)
+        leave(last, store_v, (12, 14))

@@ -48,15 +48,16 @@ def tile_multiheadlatentattention_pa_t_w8_kernel(
         wd_s_raw = keep.tile([P, RK + RD], U8, name="wd_s_raw", align_bytes=64)
         wd = keep.tile([P, RK], U32, name="wd", align_bytes=64)
         wd_s = keep.tile([P, RK], U8, name="wd_s", align_bytes=64)
+        wu_raw = keep.tile([P, H * UP], U32, name="wu_raw", align_bytes=64)
         wk = keep.tile([P, KW], U32, name="wk", align_bytes=64)
         wv = keep.tile([P, VW], U32, name="wv", align_bytes=64)
         wu_s_raw = keep.tile([P, H * UP], U8, name="wu_s_raw", align_bytes=64)
         wk_s = keep.tile([P, KW], U8, name="wk_s", align_bytes=64)
         wv_s = keep.tile([P, VW], U8, name="wv_s", align_bytes=64)
         xb_a = keep.tile([P, 2 * E], U8, name="xb_a", align_bytes=64)
-        xb_b = keep.tile([P, (I - 2) * E], U8, name="xb_b", align_bytes=64)
-        xb_c = keep.tile([P, I * E], U8, name="xb_c", align_bytes=64)
-        xb_d = keep.tile([P, (B - 2) * I * E], U8, name="xb_d", align_bytes=64)
+        xb_b = keep.tile([P, 2 * E], U8, name="xb_b", align_bytes=64)
+        xb_r = keep.tile([P, (I - 4) * E], U8, name="xb_r", align_bytes=64)
+        xb_d = keep.tile([P, (B - 1) * I * E], U8, name="xb_d", align_bytes=64)
         xsc = keep.tile([P, 2, 2], F32, name="xsc")
         tab = keep.tile([P, 2, 2, I * J], BF16, name="tab")
         ident = keep.tile([P, P], F32, name="ident")
@@ -67,21 +68,19 @@ def tile_multiheadlatentattention_pa_t_w8_kernel(
         nc.vector.memset(wu_s_raw[:].bitcast(I32), 0)
         make_identity(nc, ident[:])
         xv = x_bytes.rearrange("b (p i) k -> p b (i k)", i=I)
-        wu_heads = wu_words[0].rearrange("p n t -> p (n t)").bitcast(I32).rearrange("p (h c) -> p h c", h=H)
         nc.sync.dma_start(out=xb_a[:], in_=xv[:, 0, 0 : 2 * E])
         nc.sync.dma_start(out=wd_raw[:].bitcast(I32), in_=wd_words[0].rearrange("p n t -> p (n t)").bitcast(I32))
         nc.sync.dma_start(out=xsc[:], in_=x_scale.rearrange("a b (p u e) -> p (a b u) e", u=2, e=2))
         for q in range(4):
             nc.sync.dma_start(out=wd_s_raw[q:P:32, :].bitcast(I32), in_=wd_scales[0, q:16:4, :].bitcast(I32))
-        nc.sync.dma_start(out=xb_b[:], in_=xv[:, 0, 2 * E :])
-        nc.sync.dma_start(out=tab[:, 0, 1, :], in_=sin.rearrange("(p i) j -> p (i j)", i=I))
-        nc.sync.dma_start(out=tab[:, 0, 0, :], in_=cos.rearrange("(p i) j -> p (i j)", i=I))
+        nc.sync.dma_start(out=xb_b[:], in_=xv[:, 0, 2 * E : 4 * E])
+        nc.sync.dma_start(out=xb_r[:], in_=xv[:, 0, 4 * E :])
+        nc.sync.dma_start(out=wu_raw[:].bitcast(I32), in_=wu_words[0].rearrange("p n t -> p (n t)").bitcast(I32))
         for q in range(4):
             nc.sync.dma_start(out=wu_s_raw[q:P:32, :].bitcast(I32), in_=wu_scales[0, q:16:4, :].bitcast(I32))
-        nc.sync.dma_start(out=wv[:].bitcast(I32).rearrange("p (h c) -> p h c", h=H), in_=wu_heads[:, :, DH:])
-        nc.sync.dma_start(out=wk[:].bitcast(I32).rearrange("p (h c) -> p h c", h=H), in_=wu_heads[:, :, 0:DH])
-        nc.sync.dma_start(out=xb_c[:], in_=xv[:, 1, :])
-        nc.sync.dma_start(out=xb_d[:].rearrange("p (b c) -> p b c", b=B - 2), in_=xv[:, 2:, :])
+        nc.sync.dma_start(out=tab[:, 0, 1, :], in_=sin.rearrange("(p i) j -> p (i j)", i=I))
+        nc.sync.dma_start(out=tab[:, 0, 0, :], in_=cos.rearrange("(p i) j -> p (i j)", i=I))
+        nc.sync.dma_start(out=xb_d[:].rearrange("p (b c) -> p b c", b=B - 1), in_=xv[:, 1:, :])
 
         warm = ps_c.tile([P, BANK], F32, name="pc")
         xw, xt, xg, xq, xs, pc, cg, cq, cs, pr, ab, pk, pv, k_rows, v_rows = [{} for j in range(15)]
@@ -91,27 +90,20 @@ def tile_multiheadlatentattention_pa_t_w8_kernel(
 
         def x_source(n):
             b, i = place(n)
-            if b > 1:
-                return xb_d[:, ((b - 2) * I + i) * E : ((b - 2) * I + i + 2) * E]
-            if b == 1:
-                return xb_c[:, i * E : (i + 2) * E]
-            return xb_a[:] if i == 0 else xb_b[:, (i - 2) * E : i * E]
+            if b > 0:
+                return xb_d[:, ((b - 1) * I + i) * E : ((b - 1) * I + i + 2) * E]
+            return (xb_a, xb_b)[n][:] if n < 2 else xb_r[:, (i - 4) * E : (i - 2) * E]
 
-        def widen(n, copy, j0=0, j1=2):
-            cols = slice(j0 * E, j1 * E)
-            if n not in xw:
-                xw[n] = work.tile([P, 2 * E], BF16, name="xw", bufs=5)
-            copy(out=xw[n][:, cols], in_=x_source(n)[:, cols].bitcast(FP8))
+        def widen(n, j, copy, tag="xw", bufs=8):
+            xw[n, j] = work.tile([P, E], BF16, name=tag, bufs=bufs, align_bytes=64)
+            copy(out=xw[n, j][:], in_=x_source(n)[:, j * E : (j + 1) * E].bitcast(FP8))
 
-        def turn(n, j0=0, j1=2):
-            words = xw[n][:].bitcast(F32)
-            bank = ps_x.tile([P, 2, 2 * P], F32, name="xt")
+        def turn(n, j0=0, j1=2, pool=ps_x, tag="xt"):
+            bank = pool.tile([P, 2, 2 * P], F32, name=tag)
             for j in range(j0, j1):
                 xt[n, j] = bank
                 for u in range(2):
-                    nc.tensor.transpose(
-                        bank[:, u, j * P : (j + 1) * P], words[:, j * 256 + u : (j + 1) * 256 : 2], ident[:]
-                    )
+                    nc.tensor.transpose(bank[:, u, j * P : (j + 1) * P], xw[n, j][:].bitcast(F32)[:, u::2], ident[:])
 
         def scale_x(n, j0=0, j1=2):
             rows = slice(j0 * P, j1 * P)
@@ -160,7 +152,8 @@ def tile_multiheadlatentattention_pa_t_w8_kernel(
                 product(pr[n][:, j * RD : (j + 1) * RD], xq[n][:, rows], xs[n][:, rows], wd_raw[:, RK:], wd_s_raw[:, RK:])
 
         def latent_out(n, j):
-            cg[n, j] = work.tile([P, P, 4], BF16, name="cg", align_bytes=64, bufs=4)
+            tag, bufs = ("ring%d" % (n % 3), 1) if j == 1 else ("cg", 3)
+            cg[n, j] = work.tile([P, P, 4], BF16, name=tag, align_bytes=64, bufs=bufs)
             nc.scalar.copy(out=cg[n, j][:], in_=pc[n, j][:].rearrange("p t r -> p r t"))
 
         def quant_c(n, j):
@@ -236,9 +229,9 @@ def tile_multiheadlatentattention_pa_t_w8_kernel(
                 in_=k_rows[b][:, tiles].rearrange("p w h d -> p w (h d)"),
             )
 
-        def store_v(n, pairs=1):
+        def store_v(n, pairs=1, s0=0, s1=3):
             b, i = place(n)
-            cols = slice((i + 2 - 2 * pairs) * VW, (i + 2) * VW)
+            cols = slice((i + 2 - 2 * pairs) * VW + s0 * BANK, i * VW + s1 * BANK)
             nc.sync.dma_start(out=v_out[b].rearrange("(p i) h d -> p (i h d)", i=I)[:, cols], in_=v_rows[b][:, cols])
 
         def leave(n, store, waits):
@@ -261,101 +254,141 @@ def tile_multiheadlatentattention_pa_t_w8_kernel(
                 in_=wd_s_raw[:, 0:RK].rearrange("p (m i t) -> p m t i", t=4, i=16),
             )
 
+        def order_up_words(part, lo, hi):
+            nc.scalar.copy(
+                out=part[:].rearrange("p (h c) -> p h c", h=H),
+                in_=wu_raw[:].rearrange("p (h c) -> p h c", h=H)[:, :, lo:hi],
+            )
+
         def order_up_scales(part, lo, hi):
             nc.vector.tensor_copy(
                 out=part[:].bitcast(I32).rearrange("p (h c) -> p h c", h=H),
                 in_=wu_s_raw[:].bitcast(I32).rearrange("p (h c) -> p h c", h=H)[:, :, lo // 4 : hi // 4],
             )
 
-        def repeat_cos():
-            nc.vector.tensor_copy(out=tab[:, 1, 1, :], in_=tab[:, 0, 0, :])
+        def repeat_cos(copy):
+            copy(out=tab[:, 1, 1, :], in_=tab[:, 0, 0, :])
 
         def negate_sin():
             nc.vector.tensor_scalar(out=tab[:, 1, 0, :], in0=tab[:, 0, 1, :], scalar1=-1.0, scalar2=None, op0=MULT)
 
-
+        V, S = nc.vector.tensor_copy, nc.scalar.copy
         warm_up(3)
-        widen(0, nc.vector.tensor_copy, 0, 1)
+        widen(0, 0, V)
+        widen(0, 1, S)
         turn(0, 0, 1)
-        widen(0, nc.scalar.copy, 1, 2)
-        turn(0, 1, 2)
-        warm_up(2)
         order_latent_words()
+        widen(1, 0, S)
+        turn(0, 1, 2)
         scale_x(0, 0, 1)
+        widen(1, 1, S)
+        warm_up(2)
         order_latent_scales()
+        widen(2, 0, S)
+        turn(1, 0, 1, ps_u, "pu")
         quant_x(0, 0, 1)
-        scale_x(0, 1, 2)
-        widen(1, nc.scalar.copy)
+        widen(2, 1, S)
         latent(0, 0)
-        turn(1)
-        warm_up(1)
-        widen(2, nc.scalar.copy)
-        negate_sin()
-        quant_x(0, 1, 2)
-        latent_out(0, 0)
-        latent(0, 1)
-        rope_key(0)
-        repeat_cos()
-        order_up_scales(wk_s, 0, DH)
-        order_up_scales(wv_s, DH, UP)
+        scale_x(0, 1, 2)
+        widen(3, 0, S)
+        turn(1, 1, 2, ps_u, "pu")
         scale_x(1, 0, 1)
+        latent_out(0, 0)
+        turn(2)
+        quant_x(0, 1, 2)
+        order_up_words(wv, DH, UP)
+        latent(0, 1)
+        quant_x(1, 0, 1)
+        latent_out(0, 1)
+        rope_key(0)
+        scale_x(1, 1, 2)
+        order_up_words(wk, 0, DH)
+        latent(1, 0)
+        order_up_scales(wv_s, DH, UP)
         quant_c(0, 0)
         expand_v(0, 0)
-        turn(2)
-        scale_x(1, 1, 2)
-        latent_out(0, 1)
-        widen(3, nc.scalar.copy)
-        quant_x(1, 0, 1)
+        order_up_scales(wk_s, 0, DH)
+        v_out_copy(0, 0, S)
+        store_v(0, 1, 0, 1)
+        negate_sin()
+        latent_out(1, 0)
+        repeat_cos(V)
+        widen(3, 1, S)
+        quant_x(1, 1, 2)
+        latent(1, 1)
         rotate(0)
         quant_c(0, 1)
-        quant_x(1, 1, 2)
-        latent(1, 0)
         expand_k(0)
-        latent(1, 1)
         rotate_sum(0)
-        spread(0)
-        widen(4, nc.gpsimd.tensor_copy, 0, 1)
-        v_out_copy(0, 0, nc.scalar.copy)
-        latent_out(1, 0)
         k_out_copy(0)
+        spread(0)
         store_k(0)
         rope_key(1)
-        expand_v(0, 2)
-        expand_v(0, 1)
-        turn(3)
         scale_x(2)
-        rotate(1)
         latent_out(1, 1)
-        v_out_copy(0, 2, nc.scalar.copy)
+        expand_v(0, 1)
+        rotate(1)
+        v_out_copy(0, 1, S)
+        expand_v(0, 2)
+        quant_c(1, 0)
+        v_out_copy(0, 2, S)
+        store_v(0, 1, 1, 3)
+        turn(3)
+        quant_x(2)
+        expand_v(1, 0)
+        quant_c(1, 1)
+        v_out_copy(1, 0, S)
+        latent(2, 0)
+        rotate_sum(1)
+        spread(1)
+        expand_k(1)
+        scale_x(3)
+        k_out_copy(1)
+        widen(4, 0, nc.gpsimd.tensor_copy)
+        store_k(1)
+        rope_key(2)
+        rotate(2)
+        widen(4, 1, S)
+        latent(2, 1)
+        expand_v(1, 2)
+        v_out_copy(1, 2, V)
+        expand_v(1, 1)
+        turn(4)
 
-        for n in range(1, last + 1):
+        for n in range(2, last + 1):
             for j in range(2):
-                if (n, j) not in cg:
-                    latent_out(n, j)
+                latent_out(n, j)
+            if n > 16:
+                k_out_copy(n - 1)
+                leave(n - 1, store_k, (8, 10, 12, 14))
             v_out_copy(n - 1, 1, nc.scalar.copy)
             leave(n - 1, store_v, (12, 14))
             if n + 3 <= last:
-                widen(n + 3, nc.scalar.copy, 1, 2)
+                widen(n + 3, 1, nc.scalar.copy)
             quant_c(n, 0)
             expand_v(n, 0)
             if n < last:
                 quant_x(n + 1)
                 latent(n + 1, 0)
             quant_c(n, 1)
-            expand_k(n)
+            if n < 16:
+                expand_k(n)
             if n < last:
                 rope_key(n + 1)
                 latent(n + 1, 1)
             rotate_sum(n)
+            if n + 3 <= last:
+                widen(n + 3, 0, nc.gpsimd.tensor_copy, "ring%d" % (n % 3), 1)
             spread(n)
-            if n + 4 <= last:
-                widen(n + 4, nc.gpsimd.tensor_copy, 0, 1)
             v_out_copy(n, 0, nc.scalar.copy)
-            k_out_copy(n)
-            leave(n, store_k, (8, 10, 12, 14))
+            if n < 16:
+                k_out_copy(n)
+                leave(n, store_k, (8, 10, 12, 14))
             if n + 2 <= last:
                 scale_x(n + 2)
             expand_v(n, 2)
+            if n >= 16:
+                expand_k(n)
             expand_v(n, 1)
             if n + 3 <= last:
                 turn(n + 3)

@@ -360,7 +360,7 @@ def tile_multiheadlatentattention_pa_t_w8_kernel(
                 latent_out(n, j)
             if n > 16:
                 k_out_copy(n - 1)
-                leave(n - 1, store_k, (8, 10, 12, 14))
+                leave(n - 1, store_k, ())
             v_out_copy(n - 1, 1, nc.scalar.copy)
             leave(n - 1, store_v, (12, 14))
             if n + 3 <= last:
@@ -383,7 +383,7 @@ def tile_multiheadlatentattention_pa_t_w8_kernel(
             v_out_copy(n, 0, nc.scalar.copy)
             if n < 16:
                 k_out_copy(n)
-                leave(n, store_k, (8, 10, 12, 14))
+                leave(n, store_k, ())
             if n + 2 <= last:
                 scale_x(n + 2)
             expand_v(n, 2)

@@ -23,6 +23,7 @@ UP = DH + DV
 KW = H * DH
 VW = H * DV
 BANK = 512
+UNIT = BANK // 2
 PAIRS = B * I // 2
 
 FLOPS = 2 * B * L * E * (RK + RD + H * UP)
@@ -48,7 +49,6 @@ def tile_multiheadlatentattention_pa_t_w8_kernel(
         wd_s_raw = keep.tile([P, RK + RD], U8, name="wd_s_raw", align_bytes=64)
         wd = keep.tile([P, RK], U32, name="wd", align_bytes=64)
         wd_s = keep.tile([P, RK], U8, name="wd_s", align_bytes=64)
-        wu_raw = keep.tile([P, H * UP], U32, name="wu_raw", align_bytes=64)
         wk = keep.tile([P, KW], U32, name="wk", align_bytes=64)
         wv = keep.tile([P, VW], U32, name="wv", align_bytes=64)
         wu_s_raw = keep.tile([P, H * UP], U8, name="wu_s_raw", align_bytes=64)
@@ -57,30 +57,36 @@ def tile_multiheadlatentattention_pa_t_w8_kernel(
         xb_a = keep.tile([P, 2 * E], U8, name="xb_a", align_bytes=64)
         xb_b = keep.tile([P, 2 * E], U8, name="xb_b", align_bytes=64)
         xb_r = keep.tile([P, (I - 4) * E], U8, name="xb_r", align_bytes=64)
-        xb_d = keep.tile([P, (B - 1) * I * E], U8, name="xb_d", align_bytes=64)
+        xb_c = keep.tile([P, 4 * E], U8, name="xb_c", align_bytes=64)
+        xb_s = keep.tile([P, (I - 4) * E], U8, name="xb_s", align_bytes=64)
+        xb_d = keep.tile([P, (B - 2) * I * E], U8, name="xb_d", align_bytes=64)
         xsc = keep.tile([P, 2, 2], F32, name="xsc")
         tab = keep.tile([P, 2, 2, I * J], BF16, name="tab")
         ident = keep.tile([P, P], F32, name="ident")
         zeros = keep.tile([P, BANK], BF16, name="zeros")
 
-        nc.gpsimd.memset(wd_s_raw[:].bitcast(I32), 0)
+        nc.vector.memset(wd_s_raw[:].bitcast(I32), 0)
         nc.vector.memset(zeros[:], 0.0)
         nc.vector.memset(wu_s_raw[:].bitcast(I32), 0)
         make_identity(nc, ident[:])
         xv = x_bytes.rearrange("b (p i) k -> p b (i k)", i=I)
+        wu_heads = wu_words[0].rearrange("p n t -> p (n t)").bitcast(I32).rearrange("p (h c) -> p h c", h=H)
         nc.sync.dma_start(out=xb_a[:], in_=xv[:, 0, 0 : 2 * E])
-        nc.sync.dma_start(out=wd_raw[:].bitcast(I32), in_=wd_words[0].rearrange("p n t -> p (n t)").bitcast(I32))
         nc.sync.dma_start(out=xsc[:], in_=x_scale.rearrange("a b (p u e) -> p (a b u) e", u=2, e=2))
+        nc.sync.dma_start(out=xb_b[:], in_=xv[:, 0, 2 * E : 4 * E])
         for q in range(4):
             nc.sync.dma_start(out=wd_s_raw[q:P:32, :].bitcast(I32), in_=wd_scales[0, q:16:4, :].bitcast(I32))
-        nc.sync.dma_start(out=xb_b[:], in_=xv[:, 0, 2 * E : 4 * E])
+        nc.sync.dma_start(out=wd_raw[:].bitcast(I32), in_=wd_words[0].rearrange("p n t -> p (n t)").bitcast(I32))
         nc.sync.dma_start(out=xb_r[:], in_=xv[:, 0, 4 * E :])
-        nc.sync.dma_start(out=wu_raw[:].bitcast(I32), in_=wu_words[0].rearrange("p n t -> p (n t)").bitcast(I32))
+        nc.sync.dma_start(out=wv[:].bitcast(I32).rearrange("p (h c) -> p h c", h=H), in_=wu_heads[:, :, DH:])
+        nc.sync.dma_start(out=tab[:, 0, 1, :], in_=sin.rearrange("(p i) j -> p (i j)", i=I))
         for q in range(4):
             nc.sync.dma_start(out=wu_s_raw[q:P:32, :].bitcast(I32), in_=wu_scales[0, q:16:4, :].bitcast(I32))
-        nc.sync.dma_start(out=tab[:, 0, 1, :], in_=sin.rearrange("(p i) j -> p (i j)", i=I))
         nc.sync.dma_start(out=tab[:, 0, 0, :], in_=cos.rearrange("(p i) j -> p (i j)", i=I))
-        nc.sync.dma_start(out=xb_d[:].rearrange("p (b c) -> p b c", b=B - 1), in_=xv[:, 1:, :])
+        nc.sync.dma_start(out=xb_c[:], in_=xv[:, 1, 0 : 4 * E])
+        nc.sync.dma_start(out=wk[:].bitcast(I32).rearrange("p (h c) -> p h c", h=H), in_=wu_heads[:, :, 0:DH])
+        nc.sync.dma_start(out=xb_s[:], in_=xv[:, 1, 4 * E :])
+        nc.sync.dma_start(out=xb_d[:].rearrange("p (b c) -> p b c", b=B - 2), in_=xv[:, 2:, :])
 
         warm = ps_c.tile([P, BANK], F32, name="pc")
         xw, xt, xg, xq, xs, pc, cg, cq, cs, pr, ab, pk, pv, k_rows, v_rows = [{} for j in range(15)]
@@ -90,8 +96,10 @@ def tile_multiheadlatentattention_pa_t_w8_kernel(
 
         def x_source(n):
             b, i = place(n)
-            if b > 0:
-                return xb_d[:, ((b - 1) * I + i) * E : ((b - 1) * I + i + 2) * E]
+            if b > 1:
+                return xb_d[:, ((b - 2) * I + i) * E : ((b - 2) * I + i + 2) * E]
+            if b == 1:
+                return xb_c[:, i * E : (i + 2) * E] if i < 4 else xb_s[:, (i - 4) * E : (i - 2) * E]
             return (xb_a, xb_b)[n][:] if n < 2 else xb_r[:, (i - 4) * E : (i - 2) * E]
 
         def widen(n, j, copy, tag="xw", bufs=8):
@@ -202,24 +210,23 @@ def tile_multiheadlatentattention_pa_t_w8_kernel(
             for j in range(2):
                 product(pk[n][:, j * KW : (j + 1) * KW], cq[n, j][:], cs[n, j][:], wk[:], wk_s[:])
 
-        def expand_v(n, s):
-            pv[n, s] = ps_u.tile([P, BANK], F32, name="pu")
+        def expand_v(n, c0, c1):
+            pv[n, c0] = ps_u.tile([P, BANK], F32, name="pu")
             for j in range(2):
-                lo, hi = max(s * BANK, j * VW), min((s + 1) * BANK, (j + 1) * VW)
+                lo, hi = max(c0 * UNIT, j * VW), min(c1 * UNIT, (j + 1) * VW)
                 if lo < hi:
                     cols = slice(lo - j * VW, hi - j * VW)
-                    product(
-                        pv[n, s][:, lo - s * BANK : hi - s * BANK], cq[n, j][:], cs[n, j][:], wv[:, cols], wv_s[:, cols]
-                    )
+                    out = pv[n, c0][:, lo - c0 * UNIT : hi - c0 * UNIT]
+                    product(out, cq[n, j][:], cs[n, j][:], wv[:, cols], wv_s[:, cols])
 
         def k_out_copy(n):
             nc.scalar.copy(out=k_pair(n)[:, :, :, 0:DH], in_=pk[n][:].rearrange("p (w h c) -> p w h c", w=2, h=H))
 
-        def v_out_copy(n, s, copy):
+        def v_out_copy(n, c0, c1, copy):
             b, i = place(n)
             if b not in v_rows:
                 v_rows[b] = outs.tile([P, I * VW], F32, name="v_rows")
-            copy(out=v_rows[b][:, i * VW + s * BANK : i * VW + (s + 1) * BANK], in_=pv[n, s][:])
+            copy(out=v_rows[b][:, i * VW + c0 * UNIT : i * VW + c1 * UNIT], in_=pv[n, c0][:, 0 : (c1 - c0) * UNIT])
 
         def store_k(n, pairs=1):
             b, i = place(n)
@@ -229,9 +236,9 @@ def tile_multiheadlatentattention_pa_t_w8_kernel(
                 in_=k_rows[b][:, tiles].rearrange("p w h d -> p w (h d)"),
             )
 
-        def store_v(n, pairs=1, s0=0, s1=3):
+        def store_v(n, pairs=1, c0=0, c1=6):
             b, i = place(n)
-            cols = slice((i + 2 - 2 * pairs) * VW + s0 * BANK, i * VW + s1 * BANK)
+            cols = slice((i + 2 - 2 * pairs) * VW + c0 * UNIT, i * VW + c1 * UNIT)
             nc.sync.dma_start(out=v_out[b].rearrange("(p i) h d -> p (i h d)", i=I)[:, cols], in_=v_rows[b][:, cols])
 
         def leave(n, store, waits):
@@ -243,7 +250,7 @@ def tile_multiheadlatentattention_pa_t_w8_kernel(
                 nc.tensor.matmul(out=warm[:], lhsT=zeros[:, 0:P], rhs=zeros[:], start=True, stop=True)
 
         def order_latent_words():
-            nc.vector.tensor_copy(
+            nc.gpsimd.tensor_copy(
                 out=wd[:].bitcast(I32).rearrange("p (t m i) -> p m t i", t=4, i=4),
                 in_=wd_raw[:, 0:RK].bitcast(I32).rearrange("p (m i t) -> p m t i", t=4, i=4),
             )
@@ -252,12 +259,6 @@ def tile_multiheadlatentattention_pa_t_w8_kernel(
             nc.vector.tensor_copy(
                 out=wd_s[:].rearrange("p (t m i) -> p m t i", t=4, i=16),
                 in_=wd_s_raw[:, 0:RK].rearrange("p (m i t) -> p m t i", t=4, i=16),
-            )
-
-        def order_up_words(part, lo, hi):
-            nc.scalar.copy(
-                out=part[:].rearrange("p (h c) -> p h c", h=H),
-                in_=wu_raw[:].rearrange("p (h c) -> p h c", h=H)[:, :, lo:hi],
             )
 
         def order_up_scales(part, lo, hi):
@@ -272,87 +273,87 @@ def tile_multiheadlatentattention_pa_t_w8_kernel(
         def negate_sin():
             nc.vector.tensor_scalar(out=tab[:, 1, 0, :], in0=tab[:, 0, 1, :], scalar1=-1.0, scalar2=None, op0=MULT)
 
-        V, S = nc.vector.tensor_copy, nc.scalar.copy
+        V, S, G = nc.vector.tensor_copy, nc.scalar.copy, nc.gpsimd.tensor_copy
         warm_up(3)
         widen(0, 0, V)
         widen(0, 1, S)
-        turn(0, 0, 1)
         order_latent_words()
+        turn(0, 0, 1)
+        order_latent_scales()
         widen(1, 0, S)
         turn(0, 1, 2)
         scale_x(0, 0, 1)
         widen(1, 1, S)
-        warm_up(2)
-        order_latent_scales()
+        warm_up(1)
+        scale_x(0, 1, 2)
         widen(2, 0, S)
-        turn(1, 0, 1, ps_u, "pu")
+        turn(1, 0, 2, ps_u, "pu")
         quant_x(0, 0, 1)
         widen(2, 1, S)
-        latent(0, 0)
-        scale_x(0, 1, 2)
-        widen(3, 0, S)
-        turn(1, 1, 2, ps_u, "pu")
+        warm_up(2)
         scale_x(1, 0, 1)
-        latent_out(0, 0)
-        turn(2)
+        widen(3, 0, S)
+        latent(0, 0)
         quant_x(0, 1, 2)
-        order_up_words(wv, DH, UP)
-        latent(0, 1)
-        quant_x(1, 0, 1)
-        latent_out(0, 1)
-        rope_key(0)
-        scale_x(1, 1, 2)
-        order_up_words(wk, 0, DH)
-        latent(1, 0)
-        order_up_scales(wv_s, DH, UP)
-        quant_c(0, 0)
-        expand_v(0, 0)
-        order_up_scales(wk_s, 0, DH)
-        v_out_copy(0, 0, S)
-        store_v(0, 1, 0, 1)
-        negate_sin()
-        latent_out(1, 0)
-        repeat_cos(V)
         widen(3, 1, S)
-        quant_x(1, 1, 2)
-        latent(1, 1)
+        latent(0, 1)
+        scale_x(1, 1, 2)
+        latent_out(0, 0)
+        rope_key(0)
+        negate_sin()
+        latent_out(0, 1)
+        turn(2)
+        order_up_scales(wv_s, DH, UP)
+        widen(4, 0, S)
+        quant_x(1)
+        widen(4, 1, S)
+        repeat_cos(V)
+        quant_c(0, 0)
+        expand_v(0, 0, 2)
+        order_up_scales(wk_s, 0, DH)
+        v_out_copy(0, 0, 2, S)
+        expand_v(0, 2, 3)
         rotate(0)
+        v_out_copy(0, 2, 3, S)
+        store_v(0, 1, 0, 3)
+        latent(1, 0)
         quant_c(0, 1)
-        expand_k(0)
+        latent_out(1, 0)
+        latent(1, 1)
         rotate_sum(0)
-        k_out_copy(0)
         spread(0)
+        expand_k(0)
+        scale_x(2)
+        k_out_copy(0)
         store_k(0)
         rope_key(1)
-        scale_x(2)
-        latent_out(1, 1)
-        expand_v(0, 1)
         rotate(1)
-        v_out_copy(0, 1, S)
-        expand_v(0, 2)
+        latent_out(1, 1)
+        expand_v(0, 3, 4)
         quant_c(1, 0)
-        v_out_copy(0, 2, S)
-        store_v(0, 1, 1, 3)
-        turn(3)
+        v_out_copy(0, 3, 4, S)
+        expand_v(0, 4, 6)
         quant_x(2)
-        expand_v(1, 0)
+        v_out_copy(0, 4, 6, S)
+        store_v(0, 1, 3, 6)
+        turn(3)
         quant_c(1, 1)
-        v_out_copy(1, 0, S)
-        latent(2, 0)
+        expand_v(1, 0, 2)
         rotate_sum(1)
+        v_out_copy(1, 0, 2, S)
         spread(1)
-        expand_k(1)
+        latent(2, 0)
         scale_x(3)
+        widen(5, 0, G)
+        expand_k(1)
         k_out_copy(1)
-        widen(4, 0, nc.gpsimd.tensor_copy)
         store_k(1)
         rope_key(2)
         rotate(2)
-        widen(4, 1, S)
         latent(2, 1)
-        expand_v(1, 2)
-        v_out_copy(1, 2, V)
-        expand_v(1, 1)
+        expand_v(1, 4, 6)
+        v_out_copy(1, 4, 6, V)
+        expand_v(1, 2, 4)
         turn(4)
 
         for n in range(2, last + 1):
@@ -361,12 +362,12 @@ def tile_multiheadlatentattention_pa_t_w8_kernel(
             if n > 16:
                 k_out_copy(n - 1)
                 leave(n - 1, store_k, ())
-            v_out_copy(n - 1, 1, nc.scalar.copy)
-            leave(n - 1, store_v, (12, 14))
+            v_out_copy(n - 1, 2, 4, S)
+            leave(n - 1, store_v, (last - 1,))
             if n + 3 <= last:
-                widen(n + 3, 1, nc.scalar.copy)
+                widen(n + 3, 1, S)
             quant_c(n, 0)
-            expand_v(n, 0)
+            expand_v(n, 0, 2)
             if n < last:
                 quant_x(n + 1)
                 latent(n + 1, 0)
@@ -377,23 +378,25 @@ def tile_multiheadlatentattention_pa_t_w8_kernel(
                 rope_key(n + 1)
                 latent(n + 1, 1)
             rotate_sum(n)
-            if n + 3 <= last:
-                widen(n + 3, 0, nc.gpsimd.tensor_copy, "ring%d" % (n % 3), 1)
+            if 16 <= n <= last - 4:
+                widen(n + 4, 0, G, "ring%d" % (n % 3), 1)
             spread(n)
-            v_out_copy(n, 0, nc.scalar.copy)
+            if n < 16 and n + 4 <= last:
+                widen(n + 4, 0, G)
+            v_out_copy(n, 0, 2, S)
             if n < 16:
                 k_out_copy(n)
                 leave(n, store_k, ())
             if n + 2 <= last:
                 scale_x(n + 2)
-            expand_v(n, 2)
+            expand_v(n, 4, 6)
             if n >= 16:
                 expand_k(n)
-            expand_v(n, 1)
+            expand_v(n, 2, 4)
             if n + 3 <= last:
                 turn(n + 3)
             if n < last:
                 rotate(n + 1)
-            v_out_copy(n, 2, nc.vector.tensor_copy)
-        v_out_copy(last, 1, nc.scalar.copy)
-        leave(last, store_v, (12, 14))
+            v_out_copy(n, 4, 6, V)
+        v_out_copy(last, 2, 4, S)
+        leave(last, store_v, (last - 1,))

@@ -73,16 +73,16 @@ def tile_multiheadlatentattention_pa_t_w8_kernel(
         wu_heads = wu_words[0].rearrange("p n t -> p (n t)").bitcast(I32).rearrange("p (h c) -> p h c", h=H)
         nc.sync.dma_start(out=xb_a[:], in_=xv[:, 0, 0 : 2 * E])
         nc.sync.dma_start(out=xsc[:], in_=x_scale.rearrange("a b (p u e) -> p (a b u) e", u=2, e=2))
-        nc.sync.dma_start(out=xb_b[:], in_=xv[:, 0, 2 * E : 4 * E])
+        nc.sync.dma_start(out=wd_raw[:].bitcast(I32), in_=wd_words[0].rearrange("p n t -> p (n t)").bitcast(I32))
         for q in range(4):
             nc.sync.dma_start(out=wd_s_raw[q:P:32, :].bitcast(I32), in_=wd_scales[0, q:16:4, :].bitcast(I32))
-        nc.sync.dma_start(out=wd_raw[:].bitcast(I32), in_=wd_words[0].rearrange("p n t -> p (n t)").bitcast(I32))
+        nc.sync.dma_start(out=xb_b[:], in_=xv[:, 0, 2 * E : 4 * E])
         nc.sync.dma_start(out=xb_r[:], in_=xv[:, 0, 4 * E :])
         nc.sync.dma_start(out=wv[:].bitcast(I32).rearrange("p (h c) -> p h c", h=H), in_=wu_heads[:, :, DH:])
         nc.sync.dma_start(out=tab[:, 0, 1, :], in_=sin.rearrange("(p i) j -> p (i j)", i=I))
+        nc.sync.dma_start(out=tab[:, 0, 0, :], in_=cos.rearrange("(p i) j -> p (i j)", i=I))
         for q in range(4):
             nc.sync.dma_start(out=wu_s_raw[q:P:32, :].bitcast(I32), in_=wu_scales[0, q:16:4, :].bitcast(I32))
-        nc.sync.dma_start(out=tab[:, 0, 0, :], in_=cos.rearrange("(p i) j -> p (i j)", i=I))
         nc.sync.dma_start(out=xb_c[:], in_=xv[:, 1, 0 : 4 * E])
         nc.sync.dma_start(out=wk[:].bitcast(I32).rearrange("p (h c) -> p h c", h=H), in_=wu_heads[:, :, 0:DH])
         nc.sync.dma_start(out=xb_s[:], in_=xv[:, 1, 4 * E :])
@@ -250,7 +250,7 @@ def tile_multiheadlatentattention_pa_t_w8_kernel(
                 nc.tensor.matmul(out=warm[:], lhsT=zeros[:, 0:P], rhs=zeros[:], start=True, stop=True)
 
         def order_latent_words():
-            nc.gpsimd.tensor_copy(
+            nc.vector.tensor_copy(
                 out=wd[:].bitcast(I32).rearrange("p (t m i) -> p m t i", t=4, i=4),
                 in_=wd_raw[:, 0:RK].bitcast(I32).rearrange("p (m i t) -> p m t i", t=4, i=4),
             )
@@ -277,76 +277,77 @@ def tile_multiheadlatentattention_pa_t_w8_kernel(
         warm_up(3)
         widen(0, 0, V)
         widen(0, 1, S)
-        order_latent_words()
         turn(0, 0, 1)
-        order_latent_scales()
+        order_latent_words()
         widen(1, 0, S)
         turn(0, 1, 2)
         scale_x(0, 0, 1)
         widen(1, 1, S)
-        warm_up(1)
-        scale_x(0, 1, 2)
+        warm_up(2)
+        order_latent_scales()
         widen(2, 0, S)
-        turn(1, 0, 2, ps_u, "pu")
+        turn(1, 0, 1, ps_u, "pu")
         quant_x(0, 0, 1)
         widen(2, 1, S)
-        warm_up(2)
-        scale_x(1, 0, 1)
+        turn(1, 1, 2, ps_u, "pu")
+        scale_x(0, 1, 2)
         widen(3, 0, S)
         latent(0, 0)
+        scale_x(1, 0, 1)
+        latent_out(0, 0)
+        warm_up(1)
         quant_x(0, 1, 2)
         widen(3, 1, S)
         latent(0, 1)
         scale_x(1, 1, 2)
-        latent_out(0, 0)
+        latent_out(0, 1)
         rope_key(0)
         negate_sin()
-        latent_out(0, 1)
-        turn(2)
-        order_up_scales(wv_s, DH, UP)
         widen(4, 0, S)
-        quant_x(1)
-        widen(4, 1, S)
+        turn(2)
         repeat_cos(V)
+        widen(4, 1, S)
         quant_c(0, 0)
+        order_up_scales(wv_s, DH, UP)
         expand_v(0, 0, 2)
-        order_up_scales(wk_s, 0, DH)
+        quant_x(1)
         v_out_copy(0, 0, 2, S)
         expand_v(0, 2, 3)
         rotate(0)
         v_out_copy(0, 2, 3, S)
         store_v(0, 1, 0, 3)
         latent(1, 0)
-        quant_c(0, 1)
+        order_up_scales(wk_s, 0, DH)
         latent_out(1, 0)
         latent(1, 1)
-        rotate_sum(0)
-        spread(0)
+        quant_c(0, 1)
         expand_k(0)
-        scale_x(2)
+        rotate_sum(0)
         k_out_copy(0)
+        spread(0)
         store_k(0)
         rope_key(1)
-        rotate(1)
+        scale_x(2)
         latent_out(1, 1)
         expand_v(0, 3, 4)
-        quant_c(1, 0)
+        rotate(1)
         v_out_copy(0, 3, 4, S)
         expand_v(0, 4, 6)
-        quant_x(2)
+        quant_c(1, 0)
         v_out_copy(0, 4, 6, S)
         store_v(0, 1, 3, 6)
         turn(3)
-        quant_c(1, 1)
+        quant_x(2)
         expand_v(1, 0, 2)
-        rotate_sum(1)
+        quant_c(1, 1)
         v_out_copy(1, 0, 2, S)
-        spread(1)
         latent(2, 0)
-        scale_x(3)
-        widen(5, 0, G)
+        rotate_sum(1)
+        spread(1)
         expand_k(1)
+        scale_x(3)
         k_out_copy(1)
+        widen(5, 0, G)
         store_k(1)
         rope_key(2)
         rotate(2)
@@ -363,7 +364,7 @@ def tile_multiheadlatentattention_pa_t_w8_kernel(
                 k_out_copy(n - 1)
                 leave(n - 1, store_k, ())
             v_out_copy(n - 1, 2, 4, S)
-            leave(n - 1, store_v, (last - 1,))
+            leave(n - 1, store_v, (12, 14))
             if n + 3 <= last:
                 widen(n + 3, 1, S)
             quant_c(n, 0)
@@ -399,4 +400,4 @@ def tile_multiheadlatentattention_pa_t_w8_kernel(
                 rotate(n + 1)
             v_out_copy(n, 4, 6, V)
         v_out_copy(last, 2, 4, S)
-        leave(last, store_v, (last - 1,))
+        leave(last, store_v, (12, 14))

@@ -24,6 +24,7 @@ KW = H * DH
 VW = H * DV
 BANK = 512
 UNIT = BANK // 2
+SHARE = 256
 PAIRS = B * I // 2
 
 FLOPS = 2 * B * L * E * (RK + RD + H * UP)
@@ -102,9 +103,17 @@ def tile_multiheadlatentattention_pa_t_w8_kernel(
                 return xb_c[:, i * E : (i + 2) * E] if i < 4 else xb_s[:, (i - 4) * E : (i - 2) * E]
             return (xb_a, xb_b)[n][:] if n < 2 else xb_r[:, (i - 4) * E : (i - 2) * E]
 
-        def widen(n, j, copy, tag="xw", bufs=8):
-            xw[n, j] = work.tile([P, E], BF16, name=tag, bufs=bufs, align_bytes=64)
-            copy(out=xw[n, j][:], in_=x_source(n)[:, j * E : (j + 1) * E].bitcast(FP8))
+        def widen(n, j, copy, c0=0, c1=E):
+            if (n, j) not in xw:
+                xw[n, j] = work.tile([P, E], BF16, name="xw", bufs=8, align_bytes=64)
+            copy(out=xw[n, j][:, c0:c1], in_=x_source(n)[:, j * E + c0 : j * E + c1].bitcast(FP8))
+
+        def widen_pair(n, copy, c0, c1):
+            if (n, 0) not in xw:
+                both = work.tile([P, 2 * E], BF16, name="xw2", bufs=4, align_bytes=64)
+                xw[n] = both
+                xw[n, 0], xw[n, 1] = both[:, 0:E], both[:, E:]
+            copy(out=xw[n][:, c0:c1], in_=x_source(n)[:, c0:c1].bitcast(FP8))
 
         def turn(n, j0=0, j1=2, pool=ps_x, tag="xt"):
             bank = pool.tile([P, 2, 2 * P], F32, name=tag)
@@ -160,8 +169,7 @@ def tile_multiheadlatentattention_pa_t_w8_kernel(
                 product(pr[n][:, j * RD : (j + 1) * RD], xq[n][:, rows], xs[n][:, rows], wd_raw[:, RK:], wd_s_raw[:, RK:])
 
         def latent_out(n, j):
-            tag, bufs = ("ring%d" % (n % 3), 1) if j == 1 else ("cg", 3)
-            cg[n, j] = work.tile([P, P, 4], BF16, name=tag, align_bytes=64, bufs=bufs)
+            cg[n, j] = work.tile([P, P, 4], BF16, name="cg", align_bytes=64, bufs=4)
             nc.scalar.copy(out=cg[n, j][:], in_=pc[n, j][:].rearrange("p t r -> p r t"))
 
         def quant_c(n, j):
@@ -273,7 +281,7 @@ def tile_multiheadlatentattention_pa_t_w8_kernel(
         def negate_sin():
             nc.vector.tensor_scalar(out=tab[:, 1, 0, :], in0=tab[:, 0, 1, :], scalar1=-1.0, scalar2=None, op0=MULT)
 
-        V, S, G = nc.vector.tensor_copy, nc.scalar.copy, nc.gpsimd.tensor_copy
+        V, S = nc.vector.tensor_copy, nc.scalar.copy
         warm_up(3)
         widen(0, 0, V)
         widen(0, 1, S)
@@ -347,7 +355,6 @@ def tile_multiheadlatentattention_pa_t_w8_kernel(
         expand_k(1)
         scale_x(3)
         k_out_copy(1)
-        widen(5, 0, G)
         store_k(1)
         rope_key(2)
         rotate(2)
@@ -360,39 +367,30 @@ def tile_multiheadlatentattention_pa_t_w8_kernel(
         for n in range(2, last + 1):
             for j in range(2):
                 latent_out(n, j)
-            if n > 16:
-                k_out_copy(n - 1)
-                leave(n - 1, store_k, ())
             v_out_copy(n - 1, 2, 4, S)
-            leave(n - 1, store_v, (12, 14))
+            leave(n - 1, store_v, ())
             if n + 3 <= last:
-                widen(n + 3, 1, S)
+                widen_pair(n + 3, S, SHARE, 2 * E)
             quant_c(n, 0)
             expand_v(n, 0, 2)
             if n < last:
                 quant_x(n + 1)
                 latent(n + 1, 0)
             quant_c(n, 1)
-            if n < 16:
-                expand_k(n)
+            expand_k(n)
             if n < last:
                 rope_key(n + 1)
                 latent(n + 1, 1)
+            if n + 3 <= last:
+                widen_pair(n + 3, V, 0, SHARE)
             rotate_sum(n)
-            if 16 <= n <= last - 4:
-                widen(n + 4, 0, G, "ring%d" % (n % 3), 1)
             spread(n)
-            if n < 16 and n + 4 <= last:
-                widen(n + 4, 0, G)
             v_out_copy(n, 0, 2, S)
-            if n < 16:
-                k_out_copy(n)
-                leave(n, store_k, ())
+            k_out_copy(n)
+            leave(n, store_k, ())
             if n + 2 <= last:
                 scale_x(n + 2)
             expand_v(n, 4, 6)
-            if n >= 16:
-                expand_k(n)
             expand_v(n, 2, 4)
             if n + 3 <= last:
                 turn(n + 3)
@@ -400,4 +398,4 @@ def tile_multiheadlatentattention_pa_t_w8_kernel(
                 rotate(n + 1)
             v_out_copy(n, 4, 6, V)
         v_out_copy(last, 2, 4, S)
-        leave(last, store_v, (12, 14))
+        leave(last, store_v, ())

@@ -368,7 +368,7 @@ def tile_multiheadlatentattention_pa_t_w8_kernel(
             for j in range(2):
                 latent_out(n, j)
             v_out_copy(n - 1, 2, 4, S)
-            leave(n - 1, store_v, ())
+            leave(n - 1, store_v, (last - 3, last - 1))
             if n + 3 <= last:
                 widen_pair(n + 3, S, SHARE, 2 * E)
             quant_c(n, 0)
@@ -398,4 +398,4 @@ def tile_multiheadlatentattention_pa_t_w8_kernel(
                 rotate(n + 1)
             v_out_copy(n, 4, 6, V)
         v_out_copy(last, 2, 4, S)
-        leave(last, store_v, ())
+        leave(last, store_v, (last - 3, last - 1))

@@ -281,7 +281,7 @@ def tile_multiheadlatentattention_pa_t_w8_kernel(
         def negate_sin():
             nc.vector.tensor_scalar(out=tab[:, 1, 0, :], in0=tab[:, 0, 1, :], scalar1=-1.0, scalar2=None, op0=MULT)
 
-        V, S = nc.vector.tensor_copy, nc.scalar.copy
+        V, S, G = nc.vector.tensor_copy, nc.scalar.copy, nc.gpsimd.tensor_copy
         warm_up(3)
         widen(0, 0, V)
         widen(0, 1, S)
@@ -352,6 +352,7 @@ def tile_multiheadlatentattention_pa_t_w8_kernel(
         latent(2, 0)
         rotate_sum(1)
         spread(1)
+        widen_pair(5, G, 0, SHARE)
         expand_k(1)
         scale_x(3)
         k_out_copy(1)
@@ -381,10 +382,10 @@ def tile_multiheadlatentattention_pa_t_w8_kernel(
             if n < last:
                 rope_key(n + 1)
                 latent(n + 1, 1)
-            if n + 3 <= last:
-                widen_pair(n + 3, V, 0, SHARE)
             rotate_sum(n)
             spread(n)
+            if n + 4 <= last:
+                widen_pair(n + 4, G, 0, SHARE)
             v_out_copy(n, 0, 2, S)
             k_out_copy(n)
             leave(n, store_k, ())

@@ -56,10 +56,10 @@ def tile_multiheadlatentattention_pa_t_w8_kernel(
         wk_s = keep.tile([P, KW], U8, name="wk_s", align_bytes=64)
         wv_s = keep.tile([P, VW], U8, name="wv_s", align_bytes=64)
         xb_a = keep.tile([P, 2 * E], U8, name="xb_a", align_bytes=64)
-        xb_b = keep.tile([P, 2 * E], U8, name="xb_b", align_bytes=64)
-        xb_r = keep.tile([P, (I - 4) * E], U8, name="xb_r", align_bytes=64)
-        xb_c = keep.tile([P, 4 * E], U8, name="xb_c", align_bytes=64)
-        xb_s = keep.tile([P, (I - 4) * E], U8, name="xb_s", align_bytes=64)
+        xb_b = keep.tile([P, 4 * E], U8, name="xb_b", align_bytes=64)
+        xb_r = keep.tile([P, 2 * E], U8, name="xb_r", align_bytes=64)
+        xb_c = keep.tile([P, 2 * E], U8, name="xb_c", align_bytes=64)
+        xb_s = keep.tile([P, (I - 2) * E], U8, name="xb_s", align_bytes=64)
         xb_d = keep.tile([P, (B - 2) * I * E], U8, name="xb_d", align_bytes=64)
         xsc = keep.tile([P, 2, 2], F32, name="xsc")
         tab = keep.tile([P, 2, 2, I * J], BF16, name="tab")
@@ -74,19 +74,19 @@ def tile_multiheadlatentattention_pa_t_w8_kernel(
         wu_heads = wu_words[0].rearrange("p n t -> p (n t)").bitcast(I32).rearrange("p (h c) -> p h c", h=H)
         nc.sync.dma_start(out=xb_a[:], in_=xv[:, 0, 0 : 2 * E])
         nc.sync.dma_start(out=xsc[:], in_=x_scale.rearrange("a b (p u e) -> p (a b u) e", u=2, e=2))
-        nc.sync.dma_start(out=wd_raw[:].bitcast(I32), in_=wd_words[0].rearrange("p n t -> p (n t)").bitcast(I32))
+        nc.sync.dma_start(out=xb_b[:], in_=xv[:, 0, 2 * E : 6 * E])
         for q in range(4):
             nc.sync.dma_start(out=wd_s_raw[q:P:32, :].bitcast(I32), in_=wd_scales[0, q:16:4, :].bitcast(I32))
-        nc.sync.dma_start(out=xb_b[:], in_=xv[:, 0, 2 * E : 4 * E])
-        nc.sync.dma_start(out=xb_r[:], in_=xv[:, 0, 4 * E :])
+        nc.sync.dma_start(out=wd_raw[:].bitcast(I32), in_=wd_words[0].rearrange("p n t -> p (n t)").bitcast(I32))
+        nc.sync.dma_start(out=xb_r[:], in_=xv[:, 0, 6 * E :])
+        nc.sync.dma_start(out=xb_c[:], in_=xv[:, 1, 0 : 2 * E])
         nc.sync.dma_start(out=wv[:].bitcast(I32).rearrange("p (h c) -> p h c", h=H), in_=wu_heads[:, :, DH:])
         nc.sync.dma_start(out=tab[:, 0, 1, :], in_=sin.rearrange("(p i) j -> p (i j)", i=I))
         nc.sync.dma_start(out=tab[:, 0, 0, :], in_=cos.rearrange("(p i) j -> p (i j)", i=I))
         for q in range(4):
             nc.sync.dma_start(out=wu_s_raw[q:P:32, :].bitcast(I32), in_=wu_scales[0, q:16:4, :].bitcast(I32))
-        nc.sync.dma_start(out=xb_c[:], in_=xv[:, 1, 0 : 4 * E])
         nc.sync.dma_start(out=wk[:].bitcast(I32).rearrange("p (h c) -> p h c", h=H), in_=wu_heads[:, :, 0:DH])
-        nc.sync.dma_start(out=xb_s[:], in_=xv[:, 1, 4 * E :])
+        nc.sync.dma_start(out=xb_s[:], in_=xv[:, 1, 2 * E :])
         nc.sync.dma_start(out=xb_d[:].rearrange("p (b c) -> p b c", b=B - 2), in_=xv[:, 2:, :])
 
         warm = ps_c.tile([P, BANK], F32, name="pc")
@@ -100,8 +100,8 @@ def tile_multiheadlatentattention_pa_t_w8_kernel(
             if b > 1:
                 return xb_d[:, ((b - 2) * I + i) * E : ((b - 2) * I + i + 2) * E]
             if b == 1:
-                return xb_c[:, i * E : (i + 2) * E] if i < 4 else xb_s[:, (i - 4) * E : (i - 2) * E]
-            return (xb_a, xb_b)[n][:] if n < 2 else xb_r[:, (i - 4) * E : (i - 2) * E]
+                return xb_c[:] if i == 0 else xb_s[:, (i - 2) * E : i * E]
+            return xb_b[:, (i - 2) * E : i * E] if 0 < n < 3 else (xb_a if n == 0 else xb_r)[:]
 
         def widen(n, j, copy, c0=0, c1=E):
             if (n, j) not in xw:
@@ -258,9 +258,9 @@ def tile_multiheadlatentattention_pa_t_w8_kernel(
                 nc.tensor.matmul(out=warm[:], lhsT=zeros[:, 0:P], rhs=zeros[:], start=True, stop=True)
 
         def order_latent_words():
-            nc.vector.tensor_copy(
-                out=wd[:].bitcast(I32).rearrange("p (t m i) -> p m t i", t=4, i=4),
-                in_=wd_raw[:, 0:RK].bitcast(I32).rearrange("p (m i t) -> p m t i", t=4, i=4),
+            nc.scalar.copy(
+                out=wd[:].rearrange("p (t m i) -> p m t i", t=4, i=4),
+                in_=wd_raw[:, 0:RK].rearrange("p (m i t) -> p m t i", t=4, i=4),
             )
 
         def order_latent_scales():
@@ -286,47 +286,48 @@ def tile_multiheadlatentattention_pa_t_w8_kernel(
         widen(0, 0, V)
         widen(0, 1, S)
         turn(0, 0, 1)
-        order_latent_words()
+        order_latent_scales()
         widen(1, 0, S)
         turn(0, 1, 2)
         scale_x(0, 0, 1)
         widen(1, 1, S)
         warm_up(2)
-        order_latent_scales()
+        scale_x(0, 1, 2)
         widen(2, 0, S)
         turn(1, 0, 1, ps_u, "pu")
         quant_x(0, 0, 1)
-        widen(2, 1, S)
+        order_latent_words()
         turn(1, 1, 2, ps_u, "pu")
-        scale_x(0, 1, 2)
-        widen(3, 0, S)
-        latent(0, 0)
         scale_x(1, 0, 1)
-        latent_out(0, 0)
+        widen(2, 1, S)
         warm_up(1)
         quant_x(0, 1, 2)
-        widen(3, 1, S)
-        latent(0, 1)
+        widen(3, 0, S)
+        latent(0, 0)
         scale_x(1, 1, 2)
-        latent_out(0, 1)
-        rope_key(0)
+        widen(3, 1, S)
+        turn(2)
+        quant_x(1, 0, 1)
+        latent_out(0, 0)
+        latent(0, 1)
         negate_sin()
         widen(4, 0, S)
-        turn(2)
+        rope_key(0)
         repeat_cos(V)
-        widen(4, 1, S)
+        latent_out(0, 1)
+        latent(1, 0)
         quant_c(0, 0)
+        latent_out(1, 0)
         order_up_scales(wv_s, DH, UP)
         expand_v(0, 0, 2)
-        quant_x(1)
+        rotate(0)
         v_out_copy(0, 0, 2, S)
         expand_v(0, 2, 3)
-        rotate(0)
+        order_up_scales(wk_s, 0, DH)
         v_out_copy(0, 2, 3, S)
         store_v(0, 1, 0, 3)
-        latent(1, 0)
-        order_up_scales(wk_s, 0, DH)
-        latent_out(1, 0)
+        quant_x(1, 1, 2)
+        widen(4, 1, S)
         latent(1, 1)
         quant_c(0, 1)
         expand_k(0)

@@ -26,6 +26,7 @@ BANK = 512
 UNIT = BANK // 2
 SHARE = 256
 PAIRS = B * I // 2
+ROW = 256
 
 FLOPS = 2 * B * L * E * (RK + RD + H * UP)
 
@@ -46,23 +47,23 @@ def tile_multiheadlatentattention_pa_t_w8_kernel(
         ps_u = ctx.enter_context(tc.psum_pool(name="ps_u", bufs=3))
         ctx.enter_context(tc.manual_schedule())
 
-        wd_raw = keep.tile([P, RK + RD], U32, name="wd_raw", align_bytes=64)
-        wd_s_raw = keep.tile([P, RK + RD], U8, name="wd_s_raw", align_bytes=64)
+        wd_raw = keep.tile([P, RK + RD], U32, name="wd_raw", align_bytes=ROW)
+        wd_s_raw = keep.tile([P, RK + RD], U8, name="wd_s_raw", align_bytes=ROW)
         wd = keep.tile([P, RK], U32, name="wd", align_bytes=64)
         wd_s = keep.tile([P, RK], U8, name="wd_s", align_bytes=64)
-        wk = keep.tile([P, KW], U32, name="wk", align_bytes=64)
-        wv = keep.tile([P, VW], U32, name="wv", align_bytes=64)
-        wu_s_raw = keep.tile([P, H * UP], U8, name="wu_s_raw", align_bytes=64)
+        wk = keep.tile([P, KW], U32, name="wk", align_bytes=ROW)
+        wv = keep.tile([P, VW], U32, name="wv", align_bytes=ROW)
+        wu_s_raw = keep.tile([P, H * UP], U8, name="wu_s_raw", align_bytes=ROW)
         wk_s = keep.tile([P, KW], U8, name="wk_s", align_bytes=64)
         wv_s = keep.tile([P, VW], U8, name="wv_s", align_bytes=64)
-        xb_a = keep.tile([P, 2 * E], U8, name="xb_a", align_bytes=64)
-        xb_b = keep.tile([P, 4 * E], U8, name="xb_b", align_bytes=64)
-        xb_r = keep.tile([P, 2 * E], U8, name="xb_r", align_bytes=64)
-        xb_c = keep.tile([P, 2 * E], U8, name="xb_c", align_bytes=64)
-        xb_s = keep.tile([P, (I - 2) * E], U8, name="xb_s", align_bytes=64)
-        xb_d = keep.tile([P, (B - 2) * I * E], U8, name="xb_d", align_bytes=64)
-        xsc = keep.tile([P, 2, 2], F32, name="xsc")
-        tab = keep.tile([P, 2, 2, I * J], BF16, name="tab")
+        xb_a = keep.tile([P, 2 * E], U8, name="xb_a", align_bytes=ROW)
+        xb_b = keep.tile([P, 4 * E], U8, name="xb_b", align_bytes=ROW)
+        xb_r = keep.tile([P, 2 * E], U8, name="xb_r", align_bytes=ROW)
+        xb_c = keep.tile([P, 2 * E], U8, name="xb_c", align_bytes=ROW)
+        xb_s = keep.tile([P, (I - 2) * E], U8, name="xb_s", align_bytes=ROW)
+        xb_d = keep.tile([P, (B - 2) * I * E], U8, name="xb_d", align_bytes=ROW)
+        xsc = keep.tile([P, 2, 2], F32, name="xsc", align_bytes=ROW)
+        tab = keep.tile([P, 2, 2, I * J], BF16, name="tab", align_bytes=ROW)
         ident = keep.tile([P, P], F32, name="ident")
         zeros = keep.tile([P, BANK], BF16, name="zeros")
 
@@ -192,7 +193,7 @@ def tile_multiheadlatentattention_pa_t_w8_kernel(
         def k_pair(n):
             b, i = place(n)
             if b not in k_rows:
-                k_rows[b] = outs.tile([P, I, H, DV], F32, name="k_rows")
+                k_rows[b] = outs.tile([P, I, H, DV], F32, name="k_rows", align_bytes=ROW)
             return k_rows[b][:, i : i + 2]
 
         def rotate_sum(n):
@@ -233,7 +234,7 @@ def tile_multiheadlatentattention_pa_t_w8_kernel(
         def v_out_copy(n, c0, c1, copy):
             b, i = place(n)
             if b not in v_rows:
-                v_rows[b] = outs.tile([P, I * VW], F32, name="v_rows")
+                v_rows[b] = outs.tile([P, I * VW], F32, name="v_rows", align_bytes=ROW)
             copy(out=v_rows[b][:, i * VW + c0 * UNIT : i * VW + c1 * UNIT], in_=pv[n, c0][:, 0 : (c1 - c0) * UNIT])
 
         def store_k(n, pairs=1):

@@ -20,13 +20,13 @@ I = L // P
 J = RD // 2
 DV = DH + RD
 UP = DH + DV
-KW = H * DH
-VW = H * DV
+HALF = UP // 2
 BANK = 512
-UNIT = BANK // 2
 SHARE = 256
 PAIRS = B * I // 2
 ROW = 256
+
+X_LOADS = ((0, 2), (2, 4), (6, 2), (8, 2), (10, 6), (16, 16))
 
 FLOPS = 2 * B * L * E * (RK + RD + H * UP)
 
@@ -51,17 +51,12 @@ def tile_multiheadlatentattention_pa_t_w8_kernel(
         wd_s_raw = keep.tile([P, RK + RD], U8, name="wd_s_raw", align_bytes=ROW)
         wd = keep.tile([P, RK], U32, name="wd", align_bytes=64)
         wd_s = keep.tile([P, RK], U8, name="wd_s", align_bytes=64)
-        wk = keep.tile([P, KW], U32, name="wk", align_bytes=ROW)
-        wv = keep.tile([P, VW], U32, name="wv", align_bytes=ROW)
+        wu = keep.tile([P, 2, H * HALF], U32, name="wu", align_bytes=ROW)
         wu_s_raw = keep.tile([P, H * UP], U8, name="wu_s_raw", align_bytes=ROW)
-        wk_s = keep.tile([P, KW], U8, name="wk_s", align_bytes=64)
-        wv_s = keep.tile([P, VW], U8, name="wv_s", align_bytes=64)
-        xb_a = keep.tile([P, 2 * E], U8, name="xb_a", align_bytes=ROW)
-        xb_b = keep.tile([P, 4 * E], U8, name="xb_b", align_bytes=ROW)
-        xb_r = keep.tile([P, 2 * E], U8, name="xb_r", align_bytes=ROW)
-        xb_c = keep.tile([P, 2 * E], U8, name="xb_c", align_bytes=ROW)
-        xb_s = keep.tile([P, (I - 2) * E], U8, name="xb_s", align_bytes=ROW)
-        xb_d = keep.tile([P, (B - 2) * I * E], U8, name="xb_d", align_bytes=ROW)
+        wu_s = keep.tile([P, 2, H * HALF], U8, name="wu_s", align_bytes=64)
+        xb = {}
+        for first, count in X_LOADS:
+            xb[first] = keep.tile([P, count * E], U8, name="xb_%d" % first, align_bytes=ROW)
         xsc = keep.tile([P, 2, 2], F32, name="xsc", align_bytes=ROW)
         tab = keep.tile([P, 2, 2, I * J], BF16, name="tab", align_bytes=ROW)
         ident = keep.tile([P, P], F32, name="ident")
@@ -72,37 +67,56 @@ def tile_multiheadlatentattention_pa_t_w8_kernel(
         nc.vector.memset(wu_s_raw[:].bitcast(I32), 0)
         make_identity(nc, ident[:])
         xv = x_bytes.rearrange("b (p i) k -> p b (i k)", i=I)
-        wu_heads = wu_words[0].rearrange("p n t -> p (n t)").bitcast(I32).rearrange("p (h c) -> p h c", h=H)
-        nc.sync.dma_start(out=xb_a[:], in_=xv[:, 0, 0 : 2 * E])
-        nc.sync.dma_start(out=xsc[:], in_=x_scale.rearrange("a b (p u e) -> p (a b u) e", u=2, e=2))
-        nc.sync.dma_start(out=xb_b[:], in_=xv[:, 0, 2 * E : 6 * E])
-        for q in range(4):
-            nc.sync.dma_start(out=wd_s_raw[q:P:32, :].bitcast(I32), in_=wd_scales[0, q:16:4, :].bitcast(I32))
-        nc.sync.dma_start(out=wd_raw[:].bitcast(I32), in_=wd_words[0].rearrange("p n t -> p (n t)").bitcast(I32))
-        nc.sync.dma_start(out=xb_r[:], in_=xv[:, 0, 6 * E :])
-        nc.sync.dma_start(out=xb_c[:], in_=xv[:, 1, 0 : 2 * E])
-        nc.sync.dma_start(out=wv[:].bitcast(I32).rearrange("p (h c) -> p h c", h=H), in_=wu_heads[:, :, DH:])
-        nc.sync.dma_start(out=tab[:, 0, 1, :], in_=sin.rearrange("(p i) j -> p (i j)", i=I))
-        nc.sync.dma_start(out=tab[:, 0, 0, :], in_=cos.rearrange("(p i) j -> p (i j)", i=I))
-        for q in range(4):
-            nc.sync.dma_start(out=wu_s_raw[q:P:32, :].bitcast(I32), in_=wu_scales[0, q:16:4, :].bitcast(I32))
-        nc.sync.dma_start(out=wk[:].bitcast(I32).rearrange("p (h c) -> p h c", h=H), in_=wu_heads[:, :, 0:DH])
-        nc.sync.dma_start(out=xb_s[:], in_=xv[:, 1, 2 * E :])
-        nc.sync.dma_start(out=xb_d[:].rearrange("p (b c) -> p b c", b=B - 2), in_=xv[:, 2:, :])
+
+        def load_x(load):
+            first, count = X_LOADS[load]
+            b, i = divmod(first, I)
+            if count > I:
+                nc.sync.dma_start(out=xb[first][:].rearrange("p (b c) -> p b c", c=I * E), in_=xv[:, b : b + count // I, :])
+            else:
+                nc.sync.dma_start(out=xb[first][:], in_=xv[:, b, i * E : (i + count) * E])
+
+        def load_x_scale():
+            nc.sync.dma_start(out=xsc[:], in_=x_scale.rearrange("a b (p u e) -> p (a b u) e", u=2, e=2))
+
+        def load_scale_rows(plane, rows):
+            for q in range(4):
+                nc.sync.dma_start(out=plane[q:P:32, :].bitcast(I32), in_=rows[0, q:16:4, :].bitcast(I32))
+
+        def load_words(tile, words):
+            nc.sync.dma_start(out=tile[:].bitcast(I32), in_=words[0].rearrange("p n t -> p (n t)").bitcast(I32))
+
+        def load_half(q):
+            heads = wu_words[0].rearrange("p n t -> p (n t)").bitcast(I32).rearrange("p (h q c) -> p q h c", h=H, q=2)
+            nc.sync.dma_start(out=wu[:, q, :].bitcast(I32).rearrange("p (h c) -> p h c", h=H), in_=heads[:, q])
+
+        def load_table(plane, table):
+            nc.sync.dma_start(out=tab[:, 0, plane, :], in_=table.rearrange("(p i) j -> p (i j)", i=I))
+
+        load_x(0)
+        load_x_scale()
+        load_x(1)
+        load_scale_rows(wd_s_raw, wd_scales)
+        load_words(wd_raw, wd_words)
+        load_x(2)
+        load_x(3)
+        load_half(0)
+        load_table(1, sin)
+        load_table(0, cos)
+        load_scale_rows(wu_s_raw, wu_scales)
+        load_half(1)
+        load_x(4)
+        load_x(5)
 
         warm = ps_c.tile([P, BANK], F32, name="pc")
-        xw, xt, xg, xq, xs, pc, cg, cq, cs, pr, ab, pk, pv, k_rows, v_rows = [{} for j in range(15)]
+        xw, xt, xg, xq, xs, pc, cg, cq, cs, pr, ab, pu, rows = [{} for j in range(13)]
 
         def place(n):
             return divmod(2 * n, I)
 
         def x_source(n):
-            b, i = place(n)
-            if b > 1:
-                return xb_d[:, ((b - 2) * I + i) * E : ((b - 2) * I + i + 2) * E]
-            if b == 1:
-                return xb_c[:] if i == 0 else xb_s[:, (i - 2) * E : i * E]
-            return xb_b[:, (i - 2) * E : i * E] if 0 < n < 3 else (xb_a if n == 0 else xb_r)[:]
+            first = max(f for f in xb if f <= 2 * n)
+            return xb[first][:, (2 * n - first) * E : (2 * n - first + 2) * E]
 
         def widen(n, j, copy, c0=0, c1=E):
             if (n, j) not in xw:
@@ -190,14 +204,17 @@ def tile_multiheadlatentattention_pa_t_w8_kernel(
                 op=MULT,
             )
 
-        def k_pair(n):
+        def rows_of(n):
             b, i = place(n)
-            if b not in k_rows:
-                k_rows[b] = outs.tile([P, I, H, DV], F32, name="k_rows", align_bytes=ROW)
-            return k_rows[b][:, i : i + 2]
+            if b not in rows:
+                rows[b] = outs.tile([P, 2, I, H, DV], F32, name="rows", align_bytes=ROW)
+            return rows[b][:, :, i : i + 2]
 
-        def rotate_sum(n):
-            nc.vector.tensor_tensor(
+        def k_pair(n):
+            return rows_of(n)[:, 0]
+
+        def rotate_sum(n, engine):
+            engine.tensor_tensor(
                 out=k_pair(n)[:, :, 0, DH:],
                 in0=ab[n][:, 0, :].rearrange("p (w c) -> p w c", w=2),
                 in1=ab[n][:, 1, :].rearrange("p (w c) -> p w c", w=2),
@@ -214,41 +231,30 @@ def tile_multiheadlatentattention_pa_t_w8_kernel(
                 op1=ADD,
             )
 
-        def expand_k(n):
-            pk[n] = ps_u.tile([P, BANK], F32, name="pu")
-            for j in range(2):
-                product(pk[n][:, j * KW : (j + 1) * KW], cq[n, j][:], cs[n, j][:], wk[:], wk_s[:])
+        def expand_half(n, j, q):
+            pu[n, j, q] = ps_u.tile([P, H, HALF], F32, name="pu")
+            product(pu[n, j, q][:].rearrange("p h c -> p (h c)"), cq[n, j][:], cs[n, j][:], wu[:, q, :], wu_s[:, q, :])
 
-        def expand_v(n, c0, c1):
-            pv[n, c0] = ps_u.tile([P, BANK], F32, name="pu")
-            for j in range(2):
-                lo, hi = max(c0 * UNIT, j * VW), min(c1 * UNIT, (j + 1) * VW)
-                if lo < hi:
-                    cols = slice(lo - j * VW, hi - j * VW)
-                    out = pv[n, c0][:, lo - c0 * UNIT : hi - c0 * UNIT]
-                    product(out, cq[n, j][:], cs[n, j][:], wv[:, cols], wv_s[:, cols])
+        def half_out(n, j, q, copy):
+            if q == 0:
+                out = rows_of(n)[:, :, j, :, 0:DH].rearrange("p o h c -> p h o c")
+                copy(out=out, in_=pu[n, j, q][:].rearrange("p h (o c) -> p h o c", o=2))
+            else:
+                copy(out=rows_of(n)[:, 1, j, :, DH:], in_=pu[n, j, q][:])
 
-        def k_out_copy(n):
-            nc.scalar.copy(out=k_pair(n)[:, :, :, 0:DH], in_=pk[n][:].rearrange("p (w h c) -> p w h c", w=2, h=H))
-
-        def v_out_copy(n, c0, c1, copy):
+        def store(which, out, n, pairs, j0, j1):
             b, i = place(n)
-            if b not in v_rows:
-                v_rows[b] = outs.tile([P, I * VW], F32, name="v_rows", align_bytes=ROW)
-            copy(out=v_rows[b][:, i * VW + c0 * UNIT : i * VW + c1 * UNIT], in_=pv[n, c0][:, 0 : (c1 - c0) * UNIT])
-
-        def store_k(n, pairs=1):
-            b, i = place(n)
-            tiles = slice(i + 2 - 2 * pairs, i + 2)
+            tiles = slice(i + 2 - 2 * pairs + j0, i + j1)
             nc.sync.dma_start(
-                out=k_out[b].rearrange("(p i) h d -> p i (h d)", i=I)[:, tiles, :],
-                in_=k_rows[b][:, tiles].rearrange("p w h d -> p w (h d)"),
+                out=out[b].rearrange("(p i) h d -> p i (h d)", i=I)[:, tiles, :],
+                in_=rows[b][:, which, tiles].rearrange("p w h d -> p w (h d)"),
             )
 
-        def store_v(n, pairs=1, c0=0, c1=6):
-            b, i = place(n)
-            cols = slice((i + 2 - 2 * pairs) * VW + c0 * UNIT, i * VW + c1 * UNIT)
-            nc.sync.dma_start(out=v_out[b].rearrange("(p i) h d -> p (i h d)", i=I)[:, cols], in_=v_rows[b][:, cols])
+        def store_kk(n, pairs=1, j0=0, j1=2):
+            store(0, k_out, n, pairs, j0, j1)
+
+        def store_vv(n, pairs=1, j0=0, j1=2):
+            store(1, v_out, n, pairs, j0, j1)
 
         def leave(n, store, waits):
             if n not in waits:
@@ -270,10 +276,10 @@ def tile_multiheadlatentattention_pa_t_w8_kernel(
                 in_=wd_s_raw[:, 0:RK].rearrange("p (m i t) -> p m t i", t=4, i=16),
             )
 
-        def order_up_scales(part, lo, hi):
+        def order_up_scales(part):
             nc.vector.tensor_copy(
-                out=part[:].bitcast(I32).rearrange("p (h c) -> p h c", h=H),
-                in_=wu_s_raw[:].bitcast(I32).rearrange("p (h c) -> p h c", h=H)[:, :, lo // 4 : hi // 4],
+                out=part[:].bitcast(I32).rearrange("p q (h c) -> p q h c", h=H),
+                in_=wu_s_raw[:].bitcast(I32).rearrange("p (h q c) -> p q h c", h=H, q=2),
             )
 
         def repeat_cos(copy):
@@ -284,121 +290,119 @@ def tile_multiheadlatentattention_pa_t_w8_kernel(
 
         V, S, G = nc.vector.tensor_copy, nc.scalar.copy, nc.gpsimd.tensor_copy
         warm_up(3)
-        widen(0, 0, V)
         widen(0, 1, S)
+        widen(0, 0, V)
         turn(0, 0, 1)
-        order_latent_scales()
         widen(1, 0, S)
+        order_latent_scales()
         turn(0, 1, 2)
-        scale_x(0, 0, 1)
         widen(1, 1, S)
+        scale_x(0, 0, 1)
         warm_up(2)
-        scale_x(0, 1, 2)
         widen(2, 0, S)
+        scale_x(0, 1, 2)
         turn(1, 0, 1, ps_u, "pu")
-        quant_x(0, 0, 1)
         order_latent_words()
+        quant_x(0, 0, 1)
         turn(1, 1, 2, ps_u, "pu")
-        scale_x(1, 0, 1)
         widen(2, 1, S)
+        scale_x(1, 0, 1)
         warm_up(1)
-        quant_x(0, 1, 2)
         widen(3, 0, S)
+        quant_x(0, 1, 2)
         latent(0, 0)
-        scale_x(1, 1, 2)
         widen(3, 1, S)
+        scale_x(1, 1, 2)
         turn(2)
-        quant_x(1, 0, 1)
         latent_out(0, 0)
+        quant_x(1, 0, 1)
         latent(0, 1)
-        negate_sin()
         widen(4, 0, S)
+        negate_sin()
         rope_key(0)
-        repeat_cos(V)
         latent_out(0, 1)
+        repeat_cos(V)
         latent(1, 0)
-        quant_c(0, 0)
         latent_out(1, 0)
-        order_up_scales(wv_s, DH, UP)
-        expand_v(0, 0, 2)
+        quant_c(0, 0)
+        order_up_scales(wu_s)
+        expand_half(0, 0, 0)
+        half_out(0, 0, 0, S)
         rotate(0)
-        v_out_copy(0, 0, 2, S)
-        expand_v(0, 2, 3)
-        order_up_scales(wk_s, 0, DH)
-        v_out_copy(0, 2, 3, S)
-        store_v(0, 1, 0, 3)
+        expand_half(0, 0, 1)
+        half_out(0, 0, 1, S)
         quant_x(1, 1, 2)
-        widen(4, 1, S)
+        store_vv(0, 1, 0, 1)
         latent(1, 1)
         quant_c(0, 1)
-        expand_k(0)
-        rotate_sum(0)
-        k_out_copy(0)
+        expand_half(0, 1, 0)
+        half_out(0, 1, 0, S)
+        rotate_sum(0, nc.vector)
         spread(0)
-        store_k(0)
         rope_key(1)
-        scale_x(2)
         latent_out(1, 1)
-        expand_v(0, 3, 4)
+        scale_x(2)
+        store_kk(0)
+        expand_half(0, 1, 1)
+        widen(4, 1, S)
         rotate(1)
-        v_out_copy(0, 3, 4, S)
-        expand_v(0, 4, 6)
-        quant_c(1, 0)
-        v_out_copy(0, 4, 6, S)
-        store_v(0, 1, 3, 6)
         turn(3)
+        half_out(0, 1, 1, S)
+        quant_c(1, 0)
+        store_vv(0, 1, 1, 2)
+        expand_half(1, 0, 0)
+        half_out(1, 0, 0, S)
         quant_x(2)
-        expand_v(1, 0, 2)
-        quant_c(1, 1)
-        v_out_copy(1, 0, 2, S)
         latent(2, 0)
-        rotate_sum(1)
+        quant_c(1, 1)
+        expand_half(1, 1, 0)
+        half_out(1, 1, 0, S)
+        rotate_sum(1, nc.vector)
         spread(1)
-        widen_pair(5, G, 0, SHARE)
-        expand_k(1)
-        scale_x(3)
-        k_out_copy(1)
-        store_k(1)
         rope_key(2)
-        rotate(2)
+        scale_x(3)
+        store_kk(1)
+        widen_pair(5, G, 0, SHARE)
         latent(2, 1)
-        expand_v(1, 4, 6)
-        v_out_copy(1, 4, 6, V)
-        expand_v(1, 2, 4)
+        rotate(2)
+        expand_half(1, 0, 1)
+        half_out(1, 0, 1, V)
+        expand_half(1, 1, 1)
         turn(4)
 
         for n in range(2, last + 1):
-            for j in range(2):
-                latent_out(n, j)
-            v_out_copy(n - 1, 2, 4, S)
-            leave(n - 1, store_v, (last - 3, last - 1))
-            if n + 3 <= last:
-                widen_pair(n + 3, S, SHARE, 2 * E)
+            latent_out(n, 0)
             quant_c(n, 0)
-            expand_v(n, 0, 2)
-            if n < last:
+            expand_half(n, 0, 0)
+            latent_out(n, 1)
+            if n + 1 <= last:
                 quant_x(n + 1)
                 latent(n + 1, 0)
+            half_out(n - 1, 1, 1, S)
             quant_c(n, 1)
-            expand_k(n)
-            if n < last:
+            expand_half(n, 1, 0)
+            leave(n - 1, store_vv, (last - 3, last - 1))
+            if n + 3 <= last:
+                widen_pair(n + 3, S, SHARE, 2 * E)
+            rotate_sum(n, nc.vector)
+            if n + 1 <= last:
                 rope_key(n + 1)
-                latent(n + 1, 1)
-            rotate_sum(n)
             spread(n)
-            if n + 4 <= last:
-                widen_pair(n + 4, G, 0, SHARE)
-            v_out_copy(n, 0, 2, S)
-            k_out_copy(n)
-            leave(n, store_k, ())
+            half_out(n, 0, 0, S)
             if n + 2 <= last:
                 scale_x(n + 2)
-            expand_v(n, 4, 6)
-            expand_v(n, 2, 4)
+            if n + 1 <= last:
+                latent(n + 1, 1)
+            if n + 4 <= last:
+                widen_pair(n + 4, G, 0, SHARE)
+            half_out(n, 1, 0, S)
+            if n + 1 <= last:
+                rotate(n + 1)
+            expand_half(n, 0, 1)
+            leave(n, store_kk, ())
+            half_out(n, 0, 1, V)
+            expand_half(n, 1, 1)
             if n + 3 <= last:
                 turn(n + 3)
-            if n < last:
-                rotate(n + 1)
-            v_out_copy(n, 4, 6, V)
-        v_out_copy(last, 2, 4, S)
-        leave(last, store_v, (last - 3, last - 1))
+        half_out(last, 1, 1, S)
+        leave(last, store_vv, (last - 3, last - 1))

from contextlib import ExitStack

import concourse.mybir as mybir
from concourse.masks import make_identity

F32 = mybir.dt.float32
BF16 = mybir.dt.bfloat16
I32 = mybir.dt.int32
U32 = mybir.dt.uint32
U8 = mybir.dt.uint8
FP8 = mybir.dt.float8_e4m3fn
FP8X4 = mybir.dt.float8_e4m3fn_x4
MULT = mybir.AluOpType.mult
ADD = mybir.AluOpType.add
COPY = mybir.ActivationFunctionType.Copy

P = 128
B, L, E, H, DH, RK, RD = 4, 1024, 512, 4, 64, 512, 128
I = L // P
J = RD // 2
DV = DH + RD
UP = DH + DV
HALF = UP // 2
BANK = 512
SHARE = 256
PAIRS = B * I // 2
ROW = 256

X_LOADS = ((0, 2), (2, 4), (6, 2), (8, 2), (10, 6), (16, 16))

FLOPS = 2 * B * L * E * (RK + RD + H * UP)


def tile_multiheadlatentattention_pa_t_w8_kernel(
    tc, x_bytes, x_scale, cos, sin, wd_words, wd_scales, wu_words, wu_scales, k_out, v_out
):
    nc = tc.nc
    last = PAIRS - 1

    with ExitStack() as ctx:
        keep = ctx.enter_context(tc.tile_pool(name="keep", bufs=1))
        work = ctx.enter_context(tc.tile_pool(name="work", bufs=3))
        outs = ctx.enter_context(tc.tile_pool(name="outs", bufs=3))
        ps_x = ctx.enter_context(tc.psum_pool(name="ps_x", bufs=2))
        ps_c = ctx.enter_context(tc.psum_pool(name="ps_c", bufs=2))
        ps_r = ctx.enter_context(tc.psum_pool(name="ps_r", bufs=1))
        ps_u = ctx.enter_context(tc.psum_pool(name="ps_u", bufs=3))
        ctx.enter_context(tc.manual_schedule())

        wd_raw = keep.tile([P, RK + RD], U32, name="wd_raw", align_bytes=ROW)
        wd_s_raw = keep.tile([P, RK + RD], U8, name="wd_s_raw", align_bytes=ROW)
        wd = keep.tile([P, RK], U32, name="wd", align_bytes=64)
        wd_s = keep.tile([P, RK], U8, name="wd_s", align_bytes=64)
        wu = keep.tile([P, 2, H * HALF], U32, name="wu", align_bytes=ROW)
        wu_s_raw = keep.tile([P, H * UP], U8, name="wu_s_raw", align_bytes=ROW)
        wu_s = keep.tile([P, 2, H * HALF], U8, name="wu_s", align_bytes=64)
        xb = {}
        for first, count in X_LOADS:
            xb[first] = keep.tile([P, count * E], U8, name="xb_%d" % first, align_bytes=ROW)
        xsc = keep.tile([P, 2, 2], F32, name="xsc", align_bytes=ROW)
        tab = keep.tile([P, 2, 2, I * J], BF16, name="tab", align_bytes=ROW)
        ident = keep.tile([P, P], F32, name="ident")
        zeros = keep.tile([P, BANK], BF16, name="zeros")

        nc.vector.memset(wd_s_raw[:].bitcast(I32), 0)
        nc.vector.memset(zeros[:], 0.0)
        nc.vector.memset(wu_s_raw[:].bitcast(I32), 0)
        make_identity(nc, ident[:])
        xv = x_bytes.rearrange("b (p i) k -> p b (i k)", i=I)

        def load_x(load):
            first, count = X_LOADS[load]
            b, i = divmod(first, I)
            if count > I:
                nc.sync.dma_start(out=xb[first][:].rearrange("p (b c) -> p b c", c=I * E), in_=xv[:, b : b + count // I, :])
            else:
                nc.sync.dma_start(out=xb[first][:], in_=xv[:, b, i * E : (i + count) * E])

        def load_x_scale():
            nc.sync.dma_start(out=xsc[:], in_=x_scale.rearrange("a b (p u e) -> p (a b u) e", u=2, e=2))

        def load_scale_rows(plane, rows):
            for q in range(4):
                nc.sync.dma_start(out=plane[q:P:32, :].bitcast(I32), in_=rows[0, q:16:4, :].bitcast(I32))

        def load_words(tile, words):
            nc.sync.dma_start(out=tile[:].bitcast(I32), in_=words[0].rearrange("p n t -> p (n t)").bitcast(I32))

        def load_half(q):
            heads = wu_words[0].rearrange("p n t -> p (n t)").bitcast(I32).rearrange("p (h q c) -> p q h c", h=H, q=2)
            nc.sync.dma_start(out=wu[:, q, :].bitcast(I32).rearrange("p (h c) -> p h c", h=H), in_=heads[:, q])

        def load_table(plane, table):
            nc.sync.dma_start(out=tab[:, 0, plane, :], in_=table.rearrange("(p i) j -> p (i j)", i=I))

        load_x(0)
        load_x_scale()
        load_x(1)
        load_scale_rows(wd_s_raw, wd_scales)
        load_words(wd_raw, wd_words)
        load_x(2)
        load_x(3)
        load_half(0)
        load_table(1, sin)
        load_table(0, cos)
        load_scale_rows(wu_s_raw, wu_scales)
        load_half(1)
        load_x(4)
        load_x(5)

        warm = ps_c.tile([P, BANK], F32, name="pc")
        xw, xt, xg, xq, xs, pc, cg, cq, cs, pr, ab, pu, rows = [{} for j in range(13)]

        def place(n):
            return divmod(2 * n, I)

        def x_source(n):
            first = max(f for f in xb if f <= 2 * n)
            return xb[first][:, (2 * n - first) * E : (2 * n - first + 2) * E]

        def widen(n, j, copy, c0=0, c1=E):
            if (n, j) not in xw:
                xw[n, j] = work.tile([P, E], BF16, name="xw", bufs=8, align_bytes=64)
            copy(out=xw[n, j][:, c0:c1], in_=x_source(n)[:, j * E + c0 : j * E + c1].bitcast(FP8))

        def widen_pair(n, copy, c0, c1):
            if (n, 0) not in xw:
                both = work.tile([P, 2 * E], BF16, name="xw2", bufs=4, align_bytes=64)
                xw[n] = both
                xw[n, 0], xw[n, 1] = both[:, 0:E], both[:, E:]
            copy(out=xw[n][:, c0:c1], in_=x_source(n)[:, c0:c1].bitcast(FP8))

        def turn(n, j0=0, j1=2, pool=ps_x, tag="xt"):
            bank = pool.tile([P, 2, 2 * P], F32, name=tag)
            for j in range(j0, j1):
                xt[n, j] = bank
                for u in range(2):
                    nc.tensor.transpose(bank[:, u, j * P : (j + 1) * P], xw[n, j][:].bitcast(F32)[:, u::2], ident[:])

        def scale_x(n, j0=0, j1=2):
            rows = slice(j0 * P, j1 * P)
            if j0 == 0:
                xg[n] = work.tile([P, 2 * P, 4], BF16, name="xg", align_bytes=64)
            nc.vector.tensor_tensor(
                out=xg[n][:, rows, :].rearrange("p r (u e) -> p r u e", e=2),
                in0=xt[n, j0][:].bitcast(BF16).rearrange("p u (r e) -> p r u e", e=2)[:, rows],
                in1=xsc[:].unsqueeze(1).to_broadcast([P, rows.stop - rows.start, 2, 2]),
                op=MULT,
            )

        def quant_x(n, j0=0, j1=2):
            rows = slice(j0 * P, j1 * P)
            if j0 == 0:
                xq[n] = work.tile([P, 2 * P], U32, name="xq", align_bytes=64)
                xs[n] = work.tile([P, 2 * P], U8, name="xs", align_bytes=64)
            nc.vector.quantize_mx(
                out=xq[n][:, rows].bitcast(FP8X4),
                scales=xs[n][:, rows],
                in_=xg[n][:, rows, :].rearrange("p r t -> p (r t)"),
            )

        def product(out, lhs, lhs_s, rhs, rhs_s):
            nc.tensor.matmul_mx(
                out=out,
                lhsT=lhs.bitcast(FP8X4),
                lhsT_scale=lhs_s,
                rhs=rhs.bitcast(FP8X4),
                rhs_scale=rhs_s,
                start=True,
                stop=True,
            )

        def latent(n, j):
            rows = slice(j * P, (j + 1) * P)
            pc[n, j] = ps_c.tile([P, 4, P], F32, name="pc")
            for t in range(4):
                cols = slice(t * P, (t + 1) * P)
                product(pc[n, j][:, t, :], wd[:, cols], wd_s[:, cols], xq[n][:, rows], xs[n][:, rows])

        def rope_key(n):
            pr[n] = ps_r.tile([P, 2 * RD], F32, name="pr")
            for j in range(2):
                rows = slice(j * P, (j + 1) * P)
                product(pr[n][:, j * RD : (j + 1) * RD], xq[n][:, rows], xs[n][:, rows], wd_raw[:, RK:], wd_s_raw[:, RK:])

        def latent_out(n, j):
            cg[n, j] = work.tile([P, P, 4], BF16, name="cg", align_bytes=64, bufs=4)
            nc.scalar.copy(out=cg[n, j][:], in_=pc[n, j][:].rearrange("p t r -> p r t"))

        def quant_c(n, j):
            cq[n, j] = work.tile([P, P], U32, name="cq", align_bytes=64, bufs=4)
            cs[n, j] = work.tile([P, P], U8, name="cs", align_bytes=64, bufs=4)
            nc.vector.quantize_mx(
                out=cq[n, j][:].bitcast(FP8X4), scales=cs[n, j][:], in_=cg[n, j][:].rearrange("p r t -> p (r t)")
            )

        def rotate(n):
            i = place(n)[1]
            ab[n] = work.tile([P, 2, 2 * RD], F32, name="ab")
            nc.vector.tensor_tensor(
                out=ab[n][:].rearrange("p a (q e) -> p a q e", e=2),
                in0=pr[n][:].rearrange("p (q a) -> p a q", a=2).unsqueeze(3).to_broadcast([P, 2, 2 * J, 2]),
                in1=tab[:, :, :, i * J : (i + 2) * J].rearrange("p a e q -> p a q e"),
                op=MULT,
            )

        def rows_of(n):
            b, i = place(n)
            if b not in rows:
                rows[b] = outs.tile([P, 2, I, H, DV], F32, name="rows", align_bytes=ROW)
            return rows[b][:, :, i : i + 2]

        def k_pair(n):
            return rows_of(n)[:, 0]

        def rotate_sum(n, engine):
            engine.tensor_tensor(
                out=k_pair(n)[:, :, 0, DH:],
                in0=ab[n][:, 0, :].rearrange("p (w c) -> p w c", w=2),
                in1=ab[n][:, 1, :].rearrange("p (w c) -> p w c", w=2),
                op=ADD,
            )

        def spread(n):
            nc.gpsimd.tensor_scalar(
                out=k_pair(n)[:, :, 1:, DH:],
                in0=k_pair(n)[:, :, 0:1, DH:].to_broadcast([P, 2, H - 1, RD]),
                scalar1=1.0,
                scalar2=0.0,
                op0=MULT,
                op1=ADD,
            )

        def expand_half(n, j, q):
            pu[n, j, q] = ps_u.tile([P, H, HALF], F32, name="pu")
            product(pu[n, j, q][:].rearrange("p h c -> p (h c)"), cq[n, j][:], cs[n, j][:], wu[:, q, :], wu_s[:, q, :])

        def half_out(n, j, q, copy):
            if q == 0:
                out = rows_of(n)[:, :, j, :, 0:DH].rearrange("p o h c -> p h o c")
                copy(out=out, in_=pu[n, j, q][:].rearrange("p h (o c) -> p h o c", o=2))
            else:
                copy(out=rows_of(n)[:, 1, j, :, DH:], in_=pu[n, j, q][:])

        def store(which, out, n, pairs, j0, j1):
            b, i = place(n)
            tiles = slice(i + 2 - 2 * pairs + j0, i + j1)
            nc.sync.dma_start(
                out=out[b].rearrange("(p i) h d -> p i (h d)", i=I)[:, tiles, :],
                in_=rows[b][:, which, tiles].rearrange("p w h d -> p w (h d)"),
            )

        def store_kk(n, pairs=1, j0=0, j1=2):
            store(0, k_out, n, pairs, j0, j1)

        def store_vv(n, pairs=1, j0=0, j1=2):
            store(1, v_out, n, pairs, j0, j1)

        def leave(n, store, waits):
            if n not in waits:
                store(n, 2 if n - 1 in waits else 1)

        def warm_up(count):
            for j in range(count):
                nc.tensor.matmul(out=warm[:], lhsT=zeros[:, 0:P], rhs=zeros[:], start=True, stop=True)

        def order_latent_words():
            nc.scalar.copy(
                out=wd[:].rearrange("p (t m i) -> p m t i", t=4, i=4),
                in_=wd_raw[:, 0:RK].rearrange("p (m i t) -> p m t i", t=4, i=4),
            )

        def order_latent_scales():
            nc.vector.tensor_copy(
                out=wd_s[:].rearrange("p (t m i) -> p m t i", t=4, i=16),
                in_=wd_s_raw[:, 0:RK].rearrange("p (m i t) -> p m t i", t=4, i=16),
            )

        def order_up_scales(part):
            nc.vector.tensor_copy(
                out=part[:].bitcast(I32).rearrange("p q (h c) -> p q h c", h=H),
                in_=wu_s_raw[:].bitcast(I32).rearrange("p (h q c) -> p q h c", h=H, q=2),
            )

        def repeat_cos(copy):
            copy(out=tab[:, 1, 1, :], in_=tab[:, 0, 0, :])

        def negate_sin():
            nc.vector.tensor_scalar(out=tab[:, 1, 0, :], in0=tab[:, 0, 1, :], scalar1=-1.0, scalar2=None, op0=MULT)

        V, S, G = nc.vector.tensor_copy, nc.scalar.copy, nc.gpsimd.tensor_copy
        warm_up(3)
        widen(0, 1, S)
        widen(0, 0, V)
        turn(0, 0, 1)
        widen(1, 0, S)
        order_latent_scales()
        turn(0, 1, 2)
        widen(1, 1, S)
        scale_x(0, 0, 1)
        warm_up(2)
        widen(2, 0, S)
        scale_x(0, 1, 2)
        turn(1, 0, 1, ps_u, "pu")
        order_latent_words()
        quant_x(0, 0, 1)
        turn(1, 1, 2, ps_u, "pu")
        widen(2, 1, S)
        scale_x(1, 0, 1)
        warm_up(1)
        widen(3, 0, S)
        quant_x(0, 1, 2)
        latent(0, 0)
        widen(3, 1, S)
        scale_x(1, 1, 2)
        turn(2)
        latent_out(0, 0)
        quant_x(1, 0, 1)
        latent(0, 1)
        widen(4, 0, S)
        negate_sin()
        rope_key(0)
        latent_out(0, 1)
        repeat_cos(V)
        latent(1, 0)
        latent_out(1, 0)
        quant_c(0, 0)
        order_up_scales(wu_s)
        expand_half(0, 0, 0)
        half_out(0, 0, 0, S)
        rotate(0)
        expand_half(0, 0, 1)
        half_out(0, 0, 1, S)
        quant_x(1, 1, 2)
        store_vv(0, 1, 0, 1)
        latent(1, 1)
        quant_c(0, 1)
        expand_half(0, 1, 0)
        half_out(0, 1, 0, S)
        rotate_sum(0, nc.vector)
        spread(0)
        rope_key(1)
        latent_out(1, 1)
        scale_x(2)
        store_kk(0)
        expand_half(0, 1, 1)
        widen(4, 1, S)
        rotate(1)
        turn(3)
        half_out(0, 1, 1, S)
        quant_c(1, 0)
        store_vv(0, 1, 1, 2)
        expand_half(1, 0, 0)
        half_out(1, 0, 0, S)
        quant_x(2)
        latent(2, 0)
        quant_c(1, 1)
        expand_half(1, 1, 0)
        half_out(1, 1, 0, S)
        rotate_sum(1, nc.vector)
        spread(1)
        rope_key(2)
        scale_x(3)
        store_kk(1)
        widen_pair(5, G, 0, SHARE)
        latent(2, 1)
        rotate(2)
        expand_half(1, 0, 1)
        half_out(1, 0, 1, V)
        expand_half(1, 1, 1)
        turn(4)

        for n in range(2, last + 1):
            latent_out(n, 0)
            quant_c(n, 0)
            expand_half(n, 0, 0)
            latent_out(n, 1)
            if n + 1 <= last:
                quant_x(n + 1)
                latent(n + 1, 0)
            half_out(n - 1, 1, 1, S)
            quant_c(n, 1)
            expand_half(n, 1, 0)
            leave(n - 1, store_vv, (last - 3, last - 1))
            if n + 3 <= last:
                widen_pair(n + 3, S, SHARE, 2 * E)
            rotate_sum(n, nc.vector)
            if n + 1 <= last:
                rope_key(n + 1)
            spread(n)
            half_out(n, 0, 0, S)
            if n + 2 <= last:
                scale_x(n + 2)
            if n + 1 <= last:
                latent(n + 1, 1)
            if n + 4 <= last:
                widen_pair(n + 4, G, 0, SHARE)
            half_out(n, 1, 0, S)
            if n + 1 <= last:
                rotate(n + 1)
            expand_half(n, 0, 1)
            leave(n, store_kk, ())
            half_out(n, 0, 1, V)
            expand_half(n, 1, 1)
            if n + 3 <= last:
                turn(n + 3)
        half_out(last, 1, 1, S)
        leave(last, store_vv, (last - 3, last - 1))
